import numpy as np
import ml_dtypes


def mxq(x, axis, fmt="e4m3"):
    dtype, down = {"e4m3": (ml_dtypes.float8_e4m3fn, 7), "e5m2": (ml_dtypes.float8_e5m2, 14)}[fmt]
    v = np.moveaxis(np.asarray(x, np.float32).astype(ml_dtypes.bfloat16).astype(np.float64), axis, -1)
    blocks = v.reshape(v.shape[:-1] + (-1, 32))
    amax = np.abs(blocks).max(-1, keepdims=True)
    byte = np.maximum(np.where(amax > 0, np.frexp(amax)[1] - 1 + 127, 0) - down, 1)
    scale = np.exp2(byte - 127.0)
    codes = (blocks / scale).astype(np.float32).astype(dtype).astype(np.float64)
    return np.moveaxis((codes * scale).reshape(v.shape), -1, axis)


WIDE = False


def mx_kscale(k):
    if not WIDE:
        return np.ones(k)
    levels = np.array([30, -30])
    if k % 512:
        return np.exp2(np.random.permutation(np.resize(levels, k // 32))).repeat(32)
    a = np.empty((k // 512, 16))
    for p in range(k // 512):
        a[p, :8] = np.random.permutation(np.resize(levels, 8))
        for g in range(8):
            far = levels[np.abs(levels - a[p, g]) >= 10]
            a[p, g + 8] = far[np.random.randint(len(far))]
    return np.exp2(a.ravel()).repeat(32)


BF16 = ml_dtypes.bfloat16


def bf(x):
    return np.asarray(x, np.float32).astype(BF16)


def f64(x):
    return np.asarray(x).astype(np.float64)


B, S, E, H, KD, HD, C = 1, 1024, 1024, 8, 128, 256, 512
W = H * KD


def angles():
    lin = np.linspace(0.0, 1.0, KD // 2)
    angle = np.repeat(1.0 / (10000.0 ** lin), 2)
    idx = np.arange(S, dtype=np.float64)
    return np.sin(idx[:, None] * angle[None, :]), np.cos(idx[:, None] * angle[None, :])


def rotate_every_two(t):
    t1 = t[..., ::2]
    t2 = t[..., 1::2]
    return np.stack((-t2, t1), axis=-1).reshape(t.shape)


def setup_inputs():
    s = mx_kscale(E)
    return {"x": bf(np.random.standard_normal((B, S, E)) * s),
            "wq": bf(np.random.standard_normal((E, W)) * 1.4 / np.sqrt(E) / s[:, None]),
            "wk": bf(np.random.standard_normal((E, W)) * 1.4 / np.sqrt(E) / s[:, None])}


def reference(x, wq, wk):
    sin, cos = angles()
    xq = mxq(f64(x), 2, "e5m2")
    q = xq @ mxq(f64(wq), 0, "e5m2")
    k = (xq @ mxq(f64(wk), 0, "e5m2")) * KD ** -0.5
    q = q.reshape(B, S, H, KD).transpose(0, 2, 1, 3)
    k = k.reshape(B, S, H, KD).transpose(0, 2, 1, 3)
    q_rot = q * cos + rotate_every_two(q) * sin
    k_rot = k * cos + rotate_every_two(k) * sin
    return q_rot, k_rot

@@ -1,0 +1,240 @@
+from contextlib import ExitStack
+
+import concourse.mybir as mybir
+from concourse.masks import make_identity
+
+F32 = mybir.dt.float32
+BF16 = mybir.dt.bfloat16
+U32 = mybir.dt.uint32
+U8 = mybir.dt.uint8
+I32 = mybir.dt.int32
+E5X4 = mybir.dt.float8_e5m2_x4
+ALU = mybir.AluOpType
+ACT = mybir.ActivationFunctionType
+
+S, E, H, KD = 1024, 1024, 8, 128
+P = 128
+NT = S // P
+NC = 512
+PI = 3.141592653589793
+FLOPS = 2 * S * E * 2 * H * KD
+
+X_GROUPS = ((0, 1), (1, 2), (2, 4), (4, 8))
+
+
+def tile_retnet_pa_kernel(tc, x, wq, wk, out_0, out_1):
+    nc = tc.nc
+    xv = x.rearrange("b (p a) k -> p (b a) k", a=NT)
+    wv = [w.rearrange("(g p j) n -> g p j n", g=2, j=4) for w in (wq, wk)]
+    ov = [o.rearrange("b h (p a) f -> p (b h) a f", a=NT) for o in (out_0, out_1)]
+
+    with ExitStack() as ctx:
+        const = ctx.enter_context(tc.tile_pool(name="const", bufs=1))
+        keep = ctx.enter_context(tc.tile_pool(name="keep", bufs=1))
+        stage = ctx.enter_context(tc.tile_pool(name="stage", bufs=4))
+        prod = ctx.enter_context(tc.tile_pool(name="prod", bufs=4))
+        psx = ctx.enter_context(tc.psum_pool(name="psx", bufs=2))
+        psa = ctx.enter_context(tc.psum_pool(name="psa", bufs=6))
+
+        xraw = {}
+        wraw = {}
+
+        def load_x(i):
+            lo, hi = X_GROUPS[i]
+            t = keep.tile([P, hi - lo, E], BF16, name="xraw%d" % i)
+            nc.sync.dma_start(out=t[:], in_=xv[:, lo:hi, :])
+            xraw[i] = t
+
+        def load_w(c, g):
+            t = keep.tile([P, 4, NC], BF16, name="wraw%d_%d" % (c, g))
+            n0 = NC * (c % 2)
+            nc.sync.dma_start(out=t[:], in_=wv[c // 2][g][:, :, n0 : n0 + NC])
+            wraw[(c, g)] = t
+
+        load_x(0)
+        load_w(0, 0)
+        load_w(0, 1)
+        load_x(1)
+        load_x(2)
+        load_x(3)
+        for c in (1, 2, 3):
+            load_w(c, 0)
+            load_w(c, 1)
+
+        ones = const.tile([P, 1], F32, name="ones")
+        nc.vector.memset(ones[:], 1.0)
+        junk = const.tile([P, 1], F32, name="junk")
+        nc.scalar.activation(out=junk[:], in_=ones[:], func=ACT.Sin)
+        ident = const.tile([P, P], F32, name="ident")
+        make_identity(nc, ident[:])
+        idx = const.tile([P, NT, 64], F32, name="idx")
+        nc.gpsimd.iota(
+            idx[:], pattern=[[1, NT], [0, 64]], base=0, channel_multiplier=NT,
+            allow_small_or_imprecise_dtypes=True,
+        )
+        halfpi = const.tile([P, 1], F32, name="halfpi")
+        nc.vector.tensor_scalar_mul(out=halfpi[:], in0=ones[:], scalar1=PI / 2.0)
+        ratio = 10000.0 ** (-1.0 / 63.0)
+        nu = const.tile([P, 64], F32, name="nu")
+        for j in range(8):
+            nc.vector.tensor_scalar_mul(
+                out=nu[:, j : j + 1], in0=ones[:], scalar1=ratio**j / (2.0 * PI)
+            )
+        for m in range(1, 8):
+            nc.vector.tensor_scalar_mul(
+                out=nu[:, 8 * m : 8 * m + 8], in0=nu[:, 0:8], scalar1=ratio ** (8 * m)
+            )
+        ph = const.tile([P, NT, 64], F32, name="ph")
+        nc.vector.tensor_tensor(
+            out=ph[:], in0=idx[:], in1=nu[:].unsqueeze(1).to_broadcast([P, NT, 64]), op=ALU.mult
+        )
+        ki = const.tile([P, NT, 64], I32, name="ki")
+        nc.vector.tensor_copy(out=ki[:], in_=ph[:])
+        kf = const.tile([P, NT, 64], F32, name="kf")
+        nc.vector.tensor_copy(out=kf[:], in_=ki[:])
+        fr = const.tile([P, NT, 64], F32, name="fr")
+        nc.vector.tensor_tensor(out=fr[:], in0=ph[:], in1=kf[:], op=ALU.subtract)
+        gneg = const.tile([P, NT, 64], F32, name="gneg")
+        nc.vector.scalar_tensor_tensor(
+            out=gneg[:].rearrange("p a c -> p (a c)"),
+            in0=fr[:].rearrange("p a c -> p (a c)"),
+            scalar=0.5,
+            in1=fr[:].rearrange("p a c -> p (a c)"),
+            op0=ALU.is_gt,
+            op1=ALU.subtract,
+        )
+        sin_q = const.tile([P, NT, 2, 64], F32, name="sin_q")
+        cos_q = const.tile([P, NT, 64], F32, name="cos_q")
+        gabs = const.tile([P, NT, 64], F32, name="gabs")
+        nc.scalar.activation(out=sin_q[:, :, 0, :], in_=gneg[:], func=ACT.Sin, scale=2.0 * PI)
+        nc.scalar.activation(out=sin_q[:, :, 1, :], in_=gneg[:], func=ACT.Sin, scale=-2.0 * PI)
+        nc.scalar.activation(out=gabs[:], in_=gneg[:], func=ACT.Abs)
+        nc.scalar.activation(
+            out=cos_q[:], in_=gabs[:], func=ACT.Sin, scale=-2.0 * PI, bias=halfpi[:, 0:1]
+        )
+        kappa = KD**-0.5
+        sin_k = const.tile([P, NT, 2, 64], F32, name="sin_k")
+        cos_k = const.tile([P, NT, 64], F32, name="cos_k")
+        nc.gpsimd.tensor_scalar(
+            out=cos_k[:].rearrange("p a c -> p (a c)"), in0=cos_q[:].rearrange("p a c -> p (a c)"),
+            scalar1=kappa, scalar2=0.0, op0=ALU.mult, op1=ALU.add,
+        )
+        nc.gpsimd.tensor_scalar(
+            out=sin_k[:].rearrange("p a e c -> p (a e c)"),
+            in0=sin_q[:].rearrange("p a e c -> p (a e c)"),
+            scalar1=kappa, scalar2=0.0, op0=ALU.mult, op1=ALU.add,
+        )
+        cos_t = (cos_q, cos_k)
+        sin_t = (sin_q, sin_k)
+
+        xc = {}
+        xs = {}
+
+        def x_prep(i):
+            lo, hi = X_GROUPS[i]
+            n = hi - lo
+            xg = keep.tile([P, n * 1024], BF16, name="xg%d" % i, align_bytes=64)
+            for t in range(n):
+                words = xraw[i][:, t, :].bitcast(F32)
+                xt = psx.tile([P, 2, 2, P], F32, name="xt")
+                for g in range(2):
+                    for u in range(2):
+                        nc.tensor.transpose(
+                            xt[:, g, u, :], words[:, 256 * g + u : 256 * (g + 1) : 2], ident[:]
+                        )
+                nc.scalar.copy(
+                    out=xg[:, 1024 * t : 1024 * (t + 1)]
+                    .bitcast(F32)
+                    .rearrange("p (g r u) -> p g r u", g=2, u=2),
+                    in_=xt[:].rearrange("p g u r -> p g r u"),
+                )
+            codes = keep.tile([P, n * 256], U32, name="xc%d" % i, align_bytes=64)
+            scales = keep.tile([P, n * 256], U8, name="xs%d" % i, align_bytes=64)
+            nc.vector.quantize_mx(out=codes[:].bitcast(E5X4), scales=scales[:], in_=xg[:])
+            for t in range(n):
+                xc[lo + t] = codes[:, 256 * t : 256 * (t + 1)]
+                xs[lo + t] = scales[:, 256 * t : 256 * (t + 1)]
+
+        wgr = {}
+        wc = {}
+        ws = {}
+
+        def w_interleave(c, g, eng):
+            t = stage.tile([P, 4 * NC], BF16, name="wgr", align_bytes=64)
+            dst = t[:].rearrange("p (n j) -> p n j", j=4)
+            src = wraw[(c, g)][:].rearrange("p j n -> p n j")
+            if eng == "v":
+                nc.vector.tensor_copy(out=dst, in_=src)
+            else:
+                nc.scalar.copy(out=dst, in_=src)
+            wgr[(c, g)] = t
+
+        def w_quantise(c, g):
+            codes = keep.tile([P, NC], U32, name="wc%d_%d" % (c, g), align_bytes=64)
+            scales = keep.tile([P, NC], U8, name="ws%d_%d" % (c, g), align_bytes=64)
+            nc.vector.quantize_mx(
+                out=codes[:].bitcast(E5X4), scales=scales[:], in_=wgr[(c, g)][:]
+            )
+            wc[(c, g)] = codes
+            ws[(c, g)] = scales
+
+        x_prep(0)
+        w_interleave(0, 0, "v")
+        w_interleave(0, 1, "s")
+        w_quantise(0, 0)
+        w_quantise(0, 1)
+        x_prep(1)
+        x_prep(2)
+        x_prep(3)
+
+        for c in range(4):
+            mat = c // 2
+            h0 = 4 * (c % 2)
+            m1 = None
+            m2 = None
+            for a in range(NT):
+                if a == 0 and c < 3:
+                    w_interleave(c + 1, 0, "s")
+                    w_interleave(c + 1, 1, "s")
+                if a == 5 and c < 3:
+                    w_quantise(c + 1, 0)
+                    w_quantise(c + 1, 1)
+                acc = psa.tile([P, NC], F32, name="acc")
+                for g in range(2):
+                    nc.tensor.matmul_mx(
+                        out=acc[:],
+                        lhsT=xc[a][:, P * g : P * (g + 1)].bitcast(E5X4),
+                        lhsT_scale=xs[a][:, P * g : P * (g + 1)],
+                        rhs=wc[(c, g)][:].bitcast(E5X4),
+                        rhs_scale=ws[(c, g)][:],
+                        start=(g == 0),
+                        stop=(g == 1),
+                    )
+                aq = a % 2
+                if aq == 0:
+                    m1 = prod.tile([P, 4, 2, KD], F32, name="m1")
+                    m2 = prod.tile([P, 4, 2, KD], F32, name="m2")
+                accv = acc[:].rearrange("p (h c e) -> p h c e", h=4, e=2)
+                nc.vector.tensor_tensor(
+                    out=m1[:, :, aq, :].rearrange("p h (c e) -> p h c e", e=2),
+                    in0=accv,
+                    in1=cos_t[mat][:, a, :].unsqueeze(1).unsqueeze(3).to_broadcast([P, 4, 64, 2]),
+                    op=ALU.mult,
+                )
+                nc.vector.tensor_tensor(
+                    out=m2[:, :, aq, :].rearrange("p h (c e) -> p h c e", e=2),
+                    in0=accv[:, :, :, ::-1],
+                    in1=sin_t[mat][:, a, :, :]
+                    .rearrange("p e c -> p c e")
+                    .unsqueeze(1)
+                    .to_broadcast([P, 4, 64, 2]),
+                    op=ALU.mult,
+                )
+                if aq == 1:
+                    nc.gpsimd.tensor_tensor(
+                        out=m1[:].rearrange("p h a f -> p (h a f)"),
+                        in0=m1[:].rearrange("p h a f -> p (h a f)"),
+                        in1=m2[:].rearrange("p h a f -> p (h a f)"),
+                        op=ALU.add,
+                    )
+                    nc.sync.dma_start(out=ov[mat][:, h0 : h0 + 4, a - 1 : a + 1, :], in_=m1[:])

@@ -19,7 +19,7 @@ NC = 512
 PI = 3.141592653589793
 FLOPS = 2 * S * E * 2 * H * KD
 
-X_GROUPS = ((0, 1), (1, 2), (2, 4), (4, 8))
+CHUNKS = ((0, 0, "A"), (1, 0, "B"), (0, 1, "A"), (1, 1, "B"))
 
 
 def tile_retnet_pa_kernel(tc, x, wq, wk, out_0, out_1):
@@ -27,29 +27,31 @@ def tile_retnet_pa_kernel(tc, x, wq, wk, out_0, out_1):
     xv = x.rearrange("b (p a) k -> p (b a) k", a=NT)
     wv = [w.rearrange("(g p j) n -> g p j n", g=2, j=4) for w in (wq, wk)]
     ov = [o.rearrange("b h (p a) f -> p (b h) a f", a=NT) for o in (out_0, out_1)]
+    kappa = KD**-0.5
 
     with ExitStack() as ctx:
         const = ctx.enter_context(tc.tile_pool(name="const", bufs=1))
         keep = ctx.enter_context(tc.tile_pool(name="keep", bufs=1))
-        stage = ctx.enter_context(tc.tile_pool(name="stage", bufs=4))
-        prod = ctx.enter_context(tc.tile_pool(name="prod", bufs=4))
-        psx = ctx.enter_context(tc.psum_pool(name="psx", bufs=2))
-        psa = ctx.enter_context(tc.psum_pool(name="psa", bufs=6))
+        stage = ctx.enter_context(tc.tile_pool(name="stage", bufs=3))
+        prod_a = ctx.enter_context(tc.tile_pool(name="prod_a", bufs=3))
+        prod_b = ctx.enter_context(tc.tile_pool(name="prod_b", bufs=4))
+        resp = ctx.enter_context(tc.tile_pool(name="resp", bufs=3))
+        psa = ctx.enter_context(tc.psum_pool(name="psa", bufs=5))
+        pso = ctx.enter_context(tc.psum_pool(name="pso", bufs=3))
 
         xraw = {}
         wraw = {}
 
-        def load_x(i):
-            lo, hi = X_GROUPS[i]
-            t = keep.tile([P, hi - lo, E], BF16, name="xraw%d" % i)
-            nc.sync.dma_start(out=t[:], in_=xv[:, lo:hi, :])
-            xraw[i] = t
+        def load_x(pr):
+            t = keep.tile([P, 2, E], BF16, name="xraw%d" % pr)
+            nc.sync.dma_start(out=t[:], in_=xv[:, 2 * pr : 2 * pr + 2, :])
+            xraw[pr] = t
 
-        def load_w(c, g):
-            t = keep.tile([P, 4, NC], BF16, name="wraw%d_%d" % (c, g))
-            n0 = NC * (c % 2)
-            nc.sync.dma_start(out=t[:], in_=wv[c // 2][g][:, :, n0 : n0 + NC])
-            wraw[(c, g)] = t
+        def load_w(ch, g):
+            mat, hg, kind = CHUNKS[ch]
+            t = keep.tile([P, 4, NC], BF16, name="wraw%d_%d" % (ch, g))
+            nc.sync.dma_start(out=t[:], in_=wv[mat][g][:, :, NC * hg : NC * (hg + 1)])
+            wraw[(ch, g)] = t
 
         load_x(0)
         load_w(0, 0)
@@ -57,9 +59,9 @@ def tile_retnet_pa_kernel(tc, x, wq, wk, out_0, out_1):
         load_x(1)
         load_x(2)
         load_x(3)
-        for c in (1, 2, 3):
-            load_w(c, 0)
-            load_w(c, 1)
+        for ch in (1, 2, 3):
+            load_w(ch, 0)
+            load_w(ch, 1)
 
         ones = const.tile([P, 1], F32, name="ones")
         nc.vector.memset(ones[:], 1.0)
@@ -88,153 +90,239 @@ def tile_retnet_pa_kernel(tc, x, wq, wk, out_0, out_1):
         nc.vector.tensor_tensor(
             out=ph[:], in0=idx[:], in1=nu[:].unsqueeze(1).to_broadcast([P, NT, 64]), op=ALU.mult
         )
-        ki = const.tile([P, NT, 64], I32, name="ki")
-        nc.vector.tensor_copy(out=ki[:], in_=ph[:])
-        kf = const.tile([P, NT, 64], F32, name="kf")
-        nc.vector.tensor_copy(out=kf[:], in_=ki[:])
-        fr = const.tile([P, NT, 64], F32, name="fr")
-        nc.vector.tensor_tensor(out=fr[:], in0=ph[:], in1=kf[:], op=ALU.subtract)
+        ki = const.tile([P, NT * 64], I32, name="ki")
+        nc.vector.tensor_copy(out=ki[:], in_=ph[:].rearrange("p a c -> p (a c)"))
+        fr = const.tile([P, NT * 64], F32, name="fr")
+        nc.vector.scalar_tensor_tensor(
+            out=fr[:], in0=ki[:], scalar=-1.0, in1=ph[:].rearrange("p a c -> p (a c)"),
+            op0=ALU.mult, op1=ALU.add,
+        )
         gneg = const.tile([P, NT, 64], F32, name="gneg")
         nc.vector.scalar_tensor_tensor(
-            out=gneg[:].rearrange("p a c -> p (a c)"),
-            in0=fr[:].rearrange("p a c -> p (a c)"),
-            scalar=0.5,
-            in1=fr[:].rearrange("p a c -> p (a c)"),
-            op0=ALU.is_gt,
-            op1=ALU.subtract,
+            out=gneg[:].rearrange("p a c -> p (a c)"), in0=fr[:], scalar=0.5, in1=fr[:],
+            op0=ALU.is_gt, op1=ALU.subtract,
         )
-        sin_q = const.tile([P, NT, 2, 64], F32, name="sin_q")
-        cos_q = const.tile([P, NT, 64], F32, name="cos_q")
-        gabs = const.tile([P, NT, 64], F32, name="gabs")
-        nc.scalar.activation(out=sin_q[:, :, 0, :], in_=gneg[:], func=ACT.Sin, scale=2.0 * PI)
-        nc.scalar.activation(out=sin_q[:, :, 1, :], in_=gneg[:], func=ACT.Sin, scale=-2.0 * PI)
-        nc.scalar.activation(out=gabs[:], in_=gneg[:], func=ACT.Abs)
-        nc.scalar.activation(
-            out=cos_q[:], in_=gabs[:], func=ACT.Sin, scale=-2.0 * PI, bias=halfpi[:, 0:1]
-        )
-        kappa = KD**-0.5
-        sin_k = const.tile([P, NT, 2, 64], F32, name="sin_k")
-        cos_k = const.tile([P, NT, 64], F32, name="cos_k")
-        nc.gpsimd.tensor_scalar(
-            out=cos_k[:].rearrange("p a c -> p (a c)"), in0=cos_q[:].rearrange("p a c -> p (a c)"),
-            scalar1=kappa, scalar2=0.0, op0=ALU.mult, op1=ALU.add,
-        )
-        nc.gpsimd.tensor_scalar(
-            out=sin_k[:].rearrange("p a e c -> p (a e c)"),
-            in0=sin_q[:].rearrange("p a e c -> p (a e c)"),
-            scalar1=kappa, scalar2=0.0, op0=ALU.mult, op1=ALU.add,
-        )
-        cos_t = (cos_q, cos_k)
-        sin_t = (sin_q, sin_k)
 
-        xc = {}
-        xs = {}
+        xg = [keep.tile([P, 4096], BF16, name="xg%d" % hf, align_bytes=64) for hf in range(2)]
+        xc = [keep.tile([P, 1024], U32, name="xc%d" % hf, align_bytes=64) for hf in range(2)]
+        xs = [keep.tile([P, 1024], U8, name="xs%d" % hf, align_bytes=64) for hf in range(2)]
 
-        def x_prep(i):
-            lo, hi = X_GROUPS[i]
-            n = hi - lo
-            xg = keep.tile([P, n * 1024], BF16, name="xg%d" % i, align_bytes=64)
-            for t in range(n):
-                words = xraw[i][:, t, :].bitcast(F32)
-                xt = psx.tile([P, 2, 2, P], F32, name="xt")
+        def x_prep(pr):
+            hf = pr // 2
+            a40 = 2 * (pr % 2)
+            words_out = xg[hf][:].bitcast(F32).rearrange("p (g a r u) -> p g a r u", g=2, a=4, u=2)
+            for t in range(2):
+                words = xraw[pr][:, t, :].bitcast(F32)
+                xt = pso.tile([P, 2, 2, P], F32, name="xt", tag="o")
                 for g in range(2):
                     for u in range(2):
                         nc.tensor.transpose(
                             xt[:, g, u, :], words[:, 256 * g + u : 256 * (g + 1) : 2], ident[:]
                         )
                 nc.scalar.copy(
-                    out=xg[:, 1024 * t : 1024 * (t + 1)]
-                    .bitcast(F32)
-                    .rearrange("p (g r u) -> p g r u", g=2, u=2),
-                    in_=xt[:].rearrange("p g u r -> p g r u"),
+                    out=words_out[:, :, a40 + t, :, :], in_=xt[:].rearrange("p g u r -> p g r u")
                 )
-            codes = keep.tile([P, n * 256], U32, name="xc%d" % i, align_bytes=64)
-            scales = keep.tile([P, n * 256], U8, name="xs%d" % i, align_bytes=64)
-            nc.vector.quantize_mx(out=codes[:].bitcast(E5X4), scales=scales[:], in_=xg[:])
-            for t in range(n):
-                xc[lo + t] = codes[:, 256 * t : 256 * (t + 1)]
-                xs[lo + t] = scales[:, 256 * t : 256 * (t + 1)]
+            for g in range(2):
+                c0 = 512 * g + 128 * a40
+                nc.vector.quantize_mx(
+                    out=xc[hf][:, c0 : c0 + 256].bitcast(E5X4),
+                    scales=xs[hf][:, c0 : c0 + 256],
+                    in_=xg[hf][:, 4 * c0 : 4 * c0 + 1024],
+                )
 
         wgr = {}
         wc = {}
         ws = {}
 
-        def w_interleave(c, g, eng):
-            t = stage.tile([P, 4 * NC], BF16, name="wgr", align_bytes=64)
-            dst = t[:].rearrange("p (n j) -> p n j", j=4)
-            src = wraw[(c, g)][:].rearrange("p j n -> p n j")
-            if eng == "v":
-                nc.vector.tensor_copy(out=dst, in_=src)
-            else:
-                nc.scalar.copy(out=dst, in_=src)
-            wgr[(c, g)] = t
+        def w_interleave(ch, eng):
+            kind = CHUNKS[ch][2]
+            t = stage.tile([P, 2, 4 * NC], BF16, name="wgr", align_bytes=64)
+            cp = nc.vector.tensor_copy if eng == "v" else nc.scalar.copy
+            for g in range(2):
+                if kind == "A":
+                    cp(
+                        out=t[:, g, :].rearrange("p (n j) -> p n j", j=4),
+                        in_=wraw[(ch, g)][:].rearrange("p j n -> p n j"),
+                    )
+                else:
+                    dst = t[:, g, :].rearrange("p (h e c j) -> p e h c j", h=4, e=2, j=4)
+                    src = wraw[(ch, g)][:].rearrange("p j (h c e) -> p e h c j", h=4, e=2)
+                    for e in range(2):
+                        cp(out=dst[:, e], in_=src[:, e])
+            wgr[ch] = t
 
-        def w_quantise(c, g):
-            codes = keep.tile([P, NC], U32, name="wc%d_%d" % (c, g), align_bytes=64)
-            scales = keep.tile([P, NC], U8, name="ws%d_%d" % (c, g), align_bytes=64)
-            nc.vector.quantize_mx(
-                out=codes[:].bitcast(E5X4), scales=scales[:], in_=wgr[(c, g)][:]
-            )
-            wc[(c, g)] = codes
-            ws[(c, g)] = scales
+        def w_quantise(ch, split):
+            codes = keep.tile([P, 2, NC], U32, name="wc%d" % ch, align_bytes=64)
+            scales = keep.tile([P, 2, NC], U8, name="ws%d" % ch, align_bytes=64)
+            if split:
+                for g in range(2):
+                    nc.vector.quantize_mx(
+                        out=codes[:, g, :].bitcast(E5X4), scales=scales[:, g, :],
+                        in_=wgr[ch][:, g, :],
+                    )
+            else:
+                nc.vector.quantize_mx(
+                    out=codes[:].rearrange("p g n -> p (g n)").bitcast(E5X4),
+                    scales=scales[:].rearrange("p g n -> p (g n)"),
+                    in_=wgr[ch][:].rearrange("p g n -> p (g n)"),
+                )
+            wc[ch] = codes
+            ws[ch] = scales
 
         x_prep(0)
-        w_interleave(0, 0, "v")
-        w_interleave(0, 1, "s")
-        w_quantise(0, 0)
-        w_quantise(0, 1)
+
+        sin_a = const.tile([P, NT, 2, 64], F32, name="sin_a")
+        cos_a = const.tile([P, NT, 2, 64], F32, name="cos_a")
+        gabs = const.tile([P, NT, 64], F32, name="gabs")
+        nc.scalar.activation(out=gabs[:], in_=gneg[:], func=ACT.Abs)
+        for e in range(2):
+            nc.scalar.activation(
+                out=cos_a[:, :, e, :], in_=gabs[:], func=ACT.Sin, scale=-2.0 * PI,
+                bias=halfpi[:, 0:1],
+            )
+        nc.scalar.activation(out=sin_a[:, :, 0, :], in_=gneg[:], func=ACT.Sin, scale=2.0 * PI)
+        nc.scalar.activation(out=sin_a[:, :, 1, :], in_=gneg[:], func=ACT.Sin, scale=-2.0 * PI)
+
+        w_interleave(0, "v")
+        w_quantise(0, True)
         x_prep(1)
         x_prep(2)
         x_prep(3)
 
-        for c in range(4):
-            mat = c // 2
-            h0 = 4 * (c % 2)
-            m1 = None
-            m2 = None
-            for a in range(NT):
-                if a == 0 and c < 3:
-                    w_interleave(c + 1, 0, "s")
-                    w_interleave(c + 1, 1, "s")
-                if a == 5 and c < 3:
-                    w_quantise(c + 1, 0)
-                    w_quantise(c + 1, 1)
-                acc = psa.tile([P, NC], F32, name="acc")
-                for g in range(2):
-                    nc.tensor.matmul_mx(
-                        out=acc[:],
-                        lhsT=xc[a][:, P * g : P * (g + 1)].bitcast(E5X4),
-                        lhsT_scale=xs[a][:, P * g : P * (g + 1)],
-                        rhs=wc[(c, g)][:].bitcast(E5X4),
-                        rhs_scale=ws[(c, g)][:],
-                        start=(g == 0),
-                        stop=(g == 1),
+        ident_ce = ident[:].rearrange("p (e c) -> p c e", e=2)
+        pi1 = const.tile([P, 64, 2], F32, name="pi1")
+        pi2 = const.tile([P, 64, 2], F32, name="pi2")
+        nc.gpsimd.tensor_copy(out=pi1[:], in_=ident_ce)
+        nc.gpsimd.tensor_copy(out=pi2[:], in_=ident_ce[:, :, ::-1])
+        cos_f = const.tile([P, S], F32, name="cos_f")
+        sin_f = const.tile([P, S], F32, name="sin_f")
+        for tab_a, tab_f, sgn in ((cos_a, cos_f, 1.0), (sin_a, sin_f, -1.0)):
+            for hf in range(2):
+                pt = pso.tile([P, 4, P], F32, name="pt", tag="o")
+                for a4 in range(4):
+                    nc.tensor.transpose(
+                        pt[:, a4, :],
+                        tab_a[:, 4 * hf + a4, :, :].rearrange("p e c -> p (e c)"),
+                        ident[:],
                     )
-                aq = a % 2
-                if aq == 0:
-                    m1 = prod.tile([P, 4, 2, KD], F32, name="m1")
-                    m2 = prod.tile([P, 4, 2, KD], F32, name="m2")
-                accv = acc[:].rearrange("p (h c e) -> p h c e", h=4, e=2)
-                nc.vector.tensor_tensor(
-                    out=m1[:, :, aq, :].rearrange("p h (c e) -> p h c e", e=2),
-                    in0=accv,
-                    in1=cos_t[mat][:, a, :].unsqueeze(1).unsqueeze(3).to_broadcast([P, 4, 64, 2]),
-                    op=ALU.mult,
+                nc.scalar.activation(
+                    out=tab_f[:, 512 * hf : 512 * (hf + 1)],
+                    in_=pt[:].rearrange("p a r -> p (a r)"),
+                    func=ACT.Copy,
+                    scale=sgn,
                 )
-                nc.vector.tensor_tensor(
-                    out=m2[:, :, aq, :].rearrange("p h (c e) -> p h c e", e=2),
-                    in0=accv[:, :, :, ::-1],
-                    in1=sin_t[mat][:, a, :, :]
-                    .rearrange("p e c -> p c e")
-                    .unsqueeze(1)
-                    .to_broadcast([P, 4, 64, 2]),
-                    op=ALU.mult,
+
+        for ch in (1, 2, 3):
+            w_interleave(ch, "s")
+
+        pair = {}
+
+        def unit_a(ch, a):
+            mat, hg, kind = CHUNKS[ch]
+            hf, a4 = a // 4, a % 4
+            acc = psa.tile([P, NC], F32, name="acc")
+            for g in range(2):
+                c0 = 512 * g + 128 * a4
+                nc.tensor.matmul_mx(
+                    out=acc[:],
+                    lhsT=xc[hf][:, c0 : c0 + P].bitcast(E5X4),
+                    lhsT_scale=xs[hf][:, c0 : c0 + P],
+                    rhs=wc[ch][:, g, :].bitcast(E5X4),
+                    rhs_scale=ws[ch][:, g, :],
+                    start=(g == 0),
+                    stop=(g == 1),
                 )
-                if aq == 1:
-                    nc.gpsimd.tensor_tensor(
-                        out=m1[:].rearrange("p h a f -> p (h a f)"),
-                        in0=m1[:].rearrange("p h a f -> p (h a f)"),
-                        in1=m2[:].rearrange("p h a f -> p (h a f)"),
-                        op=ALU.add,
-                    )
-                    nc.sync.dma_start(out=ov[mat][:, h0 : h0 + 4, a - 1 : a + 1, :], in_=m1[:])
+            aq = a % 2
+            if aq == 0:
+                pair["m1"] = prod_a.tile([P, 4, 2, KD], F32, name="m1")
+                pair["m2"] = prod_a.tile([P, 4, 2, KD], F32, name="m2")
+            m1 = pair["m1"]
+            m2 = pair["m2"]
+            accv = acc[:].rearrange("p (h c e) -> p h c e", h=4, e=2)
+            nc.vector.tensor_tensor(
+                out=m1[:, :, aq, :].rearrange("p h (c e) -> p h c e", e=2),
+                in0=accv,
+                in1=cos_a[:, a, 0, :].unsqueeze(1).unsqueeze(3).to_broadcast([P, 4, 64, 2]),
+                op=ALU.mult,
+            )
+            nc.vector.tensor_tensor(
+                out=m2[:, :, aq, :].rearrange("p h (c e) -> p h c e", e=2),
+                in0=accv[:, :, :, ::-1],
+                in1=sin_a[:, a, :, :].rearrange("p e c -> p c e").unsqueeze(1)
+                .to_broadcast([P, 4, 64, 2]),
+                op=ALU.mult,
+            )
+            if aq == 1:
+                nc.gpsimd.tensor_tensor(
+                    out=m1[:].rearrange("p h a f -> p (h a f)"),
+                    in0=m1[:].rearrange("p h a f -> p (h a f)"),
+                    in1=m2[:].rearrange("p h a f -> p (h a f)"),
+                    op=ALU.add,
+                )
+                nc.sync.dma_start(
+                    out=ov[mat][:, 4 * hg : 4 * hg + 4, a - 1 : a + 1, :], in_=m1[:]
+                )
+
+        def unit_b(ch, hf, h4):
+            mat, hg, kind = CHUNKS[ch]
+            acc = psa.tile([P, NC], F32, name="acc")
+            for g in range(2):
+                nc.tensor.matmul_mx(
+                    out=acc[:],
+                    lhsT=wc[ch][:, g, P * h4 : P * (h4 + 1)].bitcast(E5X4),
+                    lhsT_scale=ws[ch][:, g, P * h4 : P * (h4 + 1)],
+                    rhs=xc[hf][:, 512 * g : 512 * (g + 1)].bitcast(E5X4),
+                    rhs_scale=xs[hf][:, 512 * g : 512 * (g + 1)],
+                    start=(g == 0),
+                    stop=(g == 1),
+                )
+            m1 = prod_b.tile([P, NC], F32, name="m1b")
+            m2 = prod_b.tile([P, NC], F32, name="m2b")
+            nc.vector.tensor_tensor(
+                out=m1[:], in0=acc[:], in1=cos_f[:, 512 * hf : 512 * (hf + 1)], op=ALU.mult
+            )
+            nc.vector.tensor_tensor(
+                out=m2[:], in0=acc[:], in1=sin_f[:, 512 * hf : 512 * (hf + 1)], op=ALU.mult
+            )
+            o = pso.tile([P, 4, P], F32, name="o", tag="o")
+            for a4 in range(4):
+                nc.tensor.matmul(
+                    out=o[:, a4, :], lhsT=m1[:, P * a4 : P * (a4 + 1)],
+                    rhs=pi1[:].rearrange("p c e -> p (c e)"),
+                    start=True, stop=False, is_transpose=True,
+                )
+                nc.tensor.matmul(
+                    out=o[:, a4, :], lhsT=m2[:, P * a4 : P * (a4 + 1)],
+                    rhs=pi2[:].rearrange("p c e -> p (c e)"),
+                    start=False, stop=True, is_transpose=True,
+                )
+            res = resp.tile([P, 4, P], F32, name="res")
+            nc.scalar.activation(
+                out=res[:].rearrange("p a f -> p (a f)"), in_=o[:].rearrange("p a f -> p (a f)"),
+                func=ACT.Copy, scale=(kappa if mat == 1 else 1.0),
+            )
+            nc.sync.dma_start(out=ov[mat][:, 4 * hg + h4, 4 * hf : 4 * hf + 4, :], in_=res[:])
+
+        for a in range(6):
+            unit_a(0, a)
+        w_quantise(1, False)
+        unit_a(0, 6)
+        unit_a(0, 7)
+        for h4 in range(4):
+            unit_b(1, 0, h4)
+        w_quantise(2, False)
+        unit_a(2, 0)
+        unit_a(2, 1)
+        for h4 in range(4):
+            unit_b(1, 1, h4)
+        unit_a(2, 2)
+        unit_a(2, 3)
+        w_quantise(3, False)
+        for h4 in range(4):
+            unit_b(3, 0, h4)
+        unit_a(2, 4)
+        unit_a(2, 5)
+        unit_a(2, 6)
+        unit_a(2, 7)
+        for h4 in range(4):
+            unit_b(3, 1, h4)

@@ -19,73 +19,81 @@ NC = 512
 PI = 3.141592653589793
 FLOPS = 2 * S * E * 2 * H * KD
 
-CHUNKS = ((0, 0, "A"), (1, 0, "B"), (0, 1, "A"), (1, 1, "B"))
+X_GROUPS = ((0, 1), (1, 2), (2, 4), (4, 8))
 
 
 def tile_retnet_pa_kernel(tc, x, wq, wk, out_0, out_1):
     nc = tc.nc
     xv = x.rearrange("b (p a) k -> p (b a) k", a=NT)
-    wv = [w.rearrange("(g p j) n -> g p j n", g=2, j=4) for w in (wq, wk)]
-    ov = [o.rearrange("b h (p a) f -> p (b h) a f", a=NT) for o in (out_0, out_1)]
+    wqv = wq.rearrange("(g p j) n -> g p j n", g=2, j=4)
+    wkv = wk.rearrange("(g p j) n -> g p j n", g=2, j=4)
+    oq = out_0.rearrange("b h (p a) f -> p (b h) a f", a=NT)
+    ok = out_1.rearrange("b h (p a) f -> p (b h) a f", a=NT)
     kappa = KD**-0.5
 
     with ExitStack() as ctx:
         const = ctx.enter_context(tc.tile_pool(name="const", bufs=1))
         keep = ctx.enter_context(tc.tile_pool(name="keep", bufs=1))
         stage = ctx.enter_context(tc.tile_pool(name="stage", bufs=3))
-        prod_a = ctx.enter_context(tc.tile_pool(name="prod_a", bufs=3))
-        prod_b = ctx.enter_context(tc.tile_pool(name="prod_b", bufs=4))
-        resp = ctx.enter_context(tc.tile_pool(name="resp", bufs=3))
-        psa = ctx.enter_context(tc.psum_pool(name="psa", bufs=5))
-        pso = ctx.enter_context(tc.psum_pool(name="pso", bufs=3))
+        prod = ctx.enter_context(tc.tile_pool(name="prod", bufs=3))
+        resp = ctx.enter_context(tc.tile_pool(name="resp", bufs=2))
+        psx = ctx.enter_context(tc.psum_pool(name="psx", bufs=2))
+        psa = ctx.enter_context(tc.psum_pool(name="psa", bufs=6))
 
         xraw = {}
         wraw = {}
 
-        def load_x(pr):
-            t = keep.tile([P, 2, E], BF16, name="xraw%d" % pr)
-            nc.sync.dma_start(out=t[:], in_=xv[:, 2 * pr : 2 * pr + 2, :])
-            xraw[pr] = t
+        def load_x(i):
+            lo, hi = X_GROUPS[i]
+            t = keep.tile([P, hi - lo, E], BF16, name="xraw%d" % i)
+            nc.sync.dma_start(out=t[:], in_=xv[:, lo:hi, :])
+            xraw[i] = t
 
-        def load_w(ch, g):
-            mat, hg, kind = CHUNKS[ch]
-            t = keep.tile([P, 4, NC], BF16, name="wraw%d_%d" % (ch, g))
-            nc.sync.dma_start(out=t[:], in_=wv[mat][g][:, :, NC * hg : NC * (hg + 1)])
-            wraw[(ch, g)] = t
+        def load_wq(c, g):
+            t = keep.tile([P, 4, NC], BF16, name="wqraw%d_%d" % (c, g))
+            nc.sync.dma_start(out=t[:], in_=wqv[g][:, :, NC * c : NC * (c + 1)])
+            wraw[("q", c, g)] = t
+
+        def load_wk(g):
+            t = keep.tile([P, 4, 2 * NC], BF16, name="wkraw%d" % g)
+            nc.sync.dma_start(out=t[:], in_=wkv[g])
+            wraw[("k", g)] = t
 
         load_x(0)
-        load_w(0, 0)
-        load_w(0, 1)
+        load_wq(0, 0)
+        load_wq(0, 1)
         load_x(1)
         load_x(2)
         load_x(3)
-        for ch in (1, 2, 3):
-            load_w(ch, 0)
-            load_w(ch, 1)
+        load_wk(0)
+        load_wk(1)
+        load_wq(1, 0)
+        load_wq(1, 1)
 
         ones = const.tile([P, 1], F32, name="ones")
         nc.vector.memset(ones[:], 1.0)
         junk = const.tile([P, 1], F32, name="junk")
         nc.scalar.activation(out=junk[:], in_=ones[:], func=ACT.Sin)
-        ident = const.tile([P, P], F32, name="ident")
-        make_identity(nc, ident[:])
         idx = const.tile([P, NT, 64], F32, name="idx")
         nc.gpsimd.iota(
             idx[:], pattern=[[1, NT], [0, 64]], base=0, channel_multiplier=NT,
             allow_small_or_imprecise_dtypes=True,
         )
-        halfpi = const.tile([P, 1], F32, name="halfpi")
-        nc.vector.tensor_scalar_mul(out=halfpi[:], in0=ones[:], scalar1=PI / 2.0)
+        ident = const.tile([P, P], F32, name="ident")
+        make_identity(nc, ident[:])
         ratio = 10000.0 ** (-1.0 / 63.0)
         nu = const.tile([P, 64], F32, name="nu")
-        for j in range(8):
+        for j in range(4):
             nc.vector.tensor_scalar_mul(
                 out=nu[:, j : j + 1], in0=ones[:], scalar1=ratio**j / (2.0 * PI)
             )
-        for m in range(1, 8):
-            nc.vector.tensor_scalar_mul(
-                out=nu[:, 8 * m : 8 * m + 8], in0=nu[:, 0:8], scalar1=ratio ** (8 * m)
-            )
+        for w in (4, 16):
+            for m in range(1, 4):
+                nc.vector.tensor_scalar_mul(
+                    out=nu[:, w * m : w * (m + 1)], in0=nu[:, 0:w], scalar1=ratio ** (w * m)
+                )
+        halfpi = const.tile([P, 1], F32, name="halfpi")
+        nc.vector.tensor_scalar_mul(out=halfpi[:], in0=ones[:], scalar1=PI / 2.0)
         ph = const.tile([P, NT, 64], F32, name="ph")
         nc.vector.tensor_tensor(
             out=ph[:], in0=idx[:], in1=nu[:].unsqueeze(1).to_broadcast([P, NT, 64]), op=ALU.mult
@@ -103,226 +111,207 @@ def tile_retnet_pa_kernel(tc, x, wq, wk, out_0, out_1):
             op0=ALU.is_gt, op1=ALU.subtract,
         )
 
-        xg = [keep.tile([P, 4096], BF16, name="xg%d" % hf, align_bytes=64) for hf in range(2)]
-        xc = [keep.tile([P, 1024], U32, name="xc%d" % hf, align_bytes=64) for hf in range(2)]
-        xs = [keep.tile([P, 1024], U8, name="xs%d" % hf, align_bytes=64) for hf in range(2)]
+        xc = {}
+        xs = {}
 
-        def x_prep(pr):
-            hf = pr // 2
-            a40 = 2 * (pr % 2)
-            words_out = xg[hf][:].bitcast(F32).rearrange("p (g a r u) -> p g a r u", g=2, a=4, u=2)
-            for t in range(2):
-                words = xraw[pr][:, t, :].bitcast(F32)
-                xt = pso.tile([P, 2, 2, P], F32, name="xt", tag="o")
+        def x_prep(i):
+            lo, hi = X_GROUPS[i]
+            n = hi - lo
+            xg = keep.tile([P, n * 1024], BF16, name="xg%d" % i, align_bytes=64)
+            for t in range(n):
+                words = xraw[i][:, t, :].bitcast(F32)
+                xt = psx.tile([P, 2, 2, P], F32, name="xt")
                 for g in range(2):
                     for u in range(2):
                         nc.tensor.transpose(
                             xt[:, g, u, :], words[:, 256 * g + u : 256 * (g + 1) : 2], ident[:]
                         )
                 nc.scalar.copy(
-                    out=words_out[:, :, a40 + t, :, :], in_=xt[:].rearrange("p g u r -> p g r u")
+                    out=xg[:, 1024 * t : 1024 * (t + 1)]
+                    .bitcast(F32)
+                    .rearrange("p (g r u) -> p g r u", g=2, u=2),
+                    in_=xt[:].rearrange("p g u r -> p g r u"),
                 )
-            for g in range(2):
-                c0 = 512 * g + 128 * a40
-                nc.vector.quantize_mx(
-                    out=xc[hf][:, c0 : c0 + 256].bitcast(E5X4),
-                    scales=xs[hf][:, c0 : c0 + 256],
-                    in_=xg[hf][:, 4 * c0 : 4 * c0 + 1024],
-                )
+            codes = keep.tile([P, n * 256], U32, name="xc%d" % i, align_bytes=64)
+            scales = keep.tile([P, n * 256], U8, name="xs%d" % i, align_bytes=64)
+            nc.vector.quantize_mx(out=codes[:].bitcast(E5X4), scales=scales[:], in_=xg[:])
+            for t in range(n):
+                xc[lo + t] = codes[:, 256 * t : 256 * (t + 1)]
+                xs[lo + t] = scales[:, 256 * t : 256 * (t + 1)]
 
         wgr = {}
         wc = {}
         ws = {}
 
-        def w_interleave(ch, eng):
-            kind = CHUNKS[ch][2]
-            t = stage.tile([P, 2, 4 * NC], BF16, name="wgr", align_bytes=64)
-            cp = nc.vector.tensor_copy if eng == "v" else nc.scalar.copy
-            for g in range(2):
-                if kind == "A":
-                    cp(
-                        out=t[:, g, :].rearrange("p (n j) -> p n j", j=4),
-                        in_=wraw[(ch, g)][:].rearrange("p j n -> p n j"),
-                    )
-                else:
-                    dst = t[:, g, :].rearrange("p (h e c j) -> p e h c j", h=4, e=2, j=4)
-                    src = wraw[(ch, g)][:].rearrange("p j (h c e) -> p e h c j", h=4, e=2)
-                    for e in range(2):
-                        cp(out=dst[:, e], in_=src[:, e])
-            wgr[ch] = t
+        def new_stage(key):
+            wgr[key] = stage.tile([P, 2, 4 * NC], BF16, name="wgr", align_bytes=64)
 
-        def w_quantise(ch, split):
-            codes = keep.tile([P, 2, NC], U32, name="wc%d" % ch, align_bytes=64)
-            scales = keep.tile([P, 2, NC], U8, name="ws%d" % ch, align_bytes=64)
+        def interleave(cp, key, piece, src, n0, n1):
+            cp(
+                out=wgr[key][:, piece, 4 * n0 : 4 * n1].rearrange("p (n j) -> p n j", j=4),
+                in_=src[:, :, n0:n1].rearrange("p j n -> p n j"),
+            )
+
+        def k_src(g, e):
+            return wraw[("k", g)][:].rearrange("p j (n e) -> p e j n", e=2)[:, e]
+
+        def w_quantise(key, split):
+            codes = keep.tile([P, 2, NC], U32, name="wc_%s" % key, align_bytes=64)
+            scales = keep.tile([P, 2, NC], U8, name="ws_%s" % key, align_bytes=64)
             if split:
-                for g in range(2):
+                for i in range(2):
                     nc.vector.quantize_mx(
-                        out=codes[:, g, :].bitcast(E5X4), scales=scales[:, g, :],
-                        in_=wgr[ch][:, g, :],
+                        out=codes[:, i, :].bitcast(E5X4), scales=scales[:, i, :],
+                        in_=wgr[key][:, i, :],
                     )
             else:
                 nc.vector.quantize_mx(
                     out=codes[:].rearrange("p g n -> p (g n)").bitcast(E5X4),
                     scales=scales[:].rearrange("p g n -> p (g n)"),
-                    in_=wgr[ch][:].rearrange("p g n -> p (g n)"),
+                    in_=wgr[key][:].rearrange("p g n -> p (g n)"),
                 )
-            wc[ch] = codes
-            ws[ch] = scales
+            wc[key] = codes
+            ws[key] = scales
 
         x_prep(0)
+        new_stage("q0")
+        interleave(nc.scalar.copy, "q0", 0, wraw[("q", 0, 0)][:], 0, NC)
+        interleave(nc.vector.tensor_copy, "q0", 1, wraw[("q", 0, 1)][:], 0, NC)
 
-        sin_a = const.tile([P, NT, 2, 64], F32, name="sin_a")
-        cos_a = const.tile([P, NT, 2, 64], F32, name="cos_a")
+        sin_q = const.tile([P, NT, 2, 64], F32, name="sin_q")
+        cos_q = const.tile([P, NT, 64], F32, name="cos_q")
         gabs = const.tile([P, NT, 64], F32, name="gabs")
         nc.scalar.activation(out=gabs[:], in_=gneg[:], func=ACT.Abs)
-        for e in range(2):
-            nc.scalar.activation(
-                out=cos_a[:, :, e, :], in_=gabs[:], func=ACT.Sin, scale=-2.0 * PI,
-                bias=halfpi[:, 0:1],
-            )
-        nc.scalar.activation(out=sin_a[:, :, 0, :], in_=gneg[:], func=ACT.Sin, scale=2.0 * PI)
-        nc.scalar.activation(out=sin_a[:, :, 1, :], in_=gneg[:], func=ACT.Sin, scale=-2.0 * PI)
+        nc.scalar.activation(
+            out=cos_q[:], in_=gabs[:], func=ACT.Sin, scale=-2.0 * PI, bias=halfpi[:, 0:1]
+        )
+        nc.scalar.activation(out=sin_q[:, :, 0, :], in_=gneg[:], func=ACT.Sin, scale=2.0 * PI)
+        nc.scalar.activation(out=sin_q[:, :, 1, :], in_=gneg[:], func=ACT.Sin, scale=-2.0 * PI)
 
-        w_interleave(0, "v")
-        w_quantise(0, True)
+        w_quantise("q0", True)
         x_prep(1)
         x_prep(2)
         x_prep(3)
 
-        ident_ce = ident[:].rearrange("p (e c) -> p c e", e=2)
-        pi1 = const.tile([P, 64, 2], F32, name="pi1")
-        pi2 = const.tile([P, 64, 2], F32, name="pi2")
-        nc.gpsimd.tensor_copy(out=pi1[:], in_=ident_ce)
-        nc.gpsimd.tensor_copy(out=pi2[:], in_=ident_ce[:, :, ::-1])
-        cos_f = const.tile([P, S], F32, name="cos_f")
-        sin_f = const.tile([P, S], F32, name="sin_f")
-        for tab_a, tab_f, sgn in ((cos_a, cos_f, 1.0), (sin_a, sin_f, -1.0)):
-            for hf in range(2):
-                pt = pso.tile([P, 4, P], F32, name="pt", tag="o")
-                for a4 in range(4):
-                    nc.tensor.transpose(
-                        pt[:, a4, :],
-                        tab_a[:, 4 * hf + a4, :, :].rearrange("p e c -> p (e c)"),
-                        ident[:],
-                    )
-                nc.scalar.activation(
-                    out=tab_f[:, 512 * hf : 512 * (hf + 1)],
-                    in_=pt[:].rearrange("p a r -> p (a r)"),
-                    func=ACT.Copy,
-                    scale=sgn,
-                )
+        for g in range(2):
+            new_stage("k%d" % g)
+            for e in range(2):
+                interleave(nc.scalar.copy, "k%d" % g, e, k_src(g, e), 0, NC)
+        new_stage("q1")
+        for g in range(2):
+            interleave(nc.scalar.copy, "q1", g, wraw[("q", 1, g)][:], 0, NC)
 
-        for ch in (1, 2, 3):
-            w_interleave(ch, "s")
+        t2 = const.tile([P, NT, 64], F32, name="t2")
+        t3 = const.tile([P, NT, 64], F32, name="t3")
+
+        def k_tables():
+            nc.gpsimd.tensor_tensor(out=t2[:], in0=sin_q[:, :, 1, :], in1=cos_q[:], op=ALU.subtract)
+            nc.gpsimd.tensor_tensor(out=t3[:], in0=sin_q[:, :, 0, :], in1=cos_q[:], op=ALU.subtract)
+
+        def mx(acc, a, passes):
+            last = len(passes) - 1
+            for i, (g, codes, scales) in enumerate(passes):
+                nc.tensor.matmul_mx(
+                    out=acc[:],
+                    lhsT=xc[a][:, P * g : P * (g + 1)].bitcast(E5X4),
+                    lhsT_scale=xs[a][:, P * g : P * (g + 1)],
+                    rhs=codes.bitcast(E5X4),
+                    rhs_scale=scales,
+                    start=(i == 0),
+                    stop=(i == last),
+                )
 
         pair = {}
 
-        def unit_a(ch, a):
-            mat, hg, kind = CHUNKS[ch]
-            hf, a4 = a // 4, a % 4
+        def unit_q(c, a, vector_adds):
+            key = "q%d" % c
             acc = psa.tile([P, NC], F32, name="acc")
-            for g in range(2):
-                c0 = 512 * g + 128 * a4
-                nc.tensor.matmul_mx(
-                    out=acc[:],
-                    lhsT=xc[hf][:, c0 : c0 + P].bitcast(E5X4),
-                    lhsT_scale=xs[hf][:, c0 : c0 + P],
-                    rhs=wc[ch][:, g, :].bitcast(E5X4),
-                    rhs_scale=ws[ch][:, g, :],
-                    start=(g == 0),
-                    stop=(g == 1),
-                )
+            mx(acc, a, [(g, wc[key][:, g, :], ws[key][:, g, :]) for g in range(2)])
             aq = a % 2
             if aq == 0:
-                pair["m1"] = prod_a.tile([P, 4, 2, KD], F32, name="m1")
-                pair["m2"] = prod_a.tile([P, 4, 2, KD], F32, name="m2")
+                pair["m1"] = prod.tile([P, 4, 2, KD], F32, name="m1")
+                pair["m2"] = prod.tile([P, 4, 2, KD], F32, name="m2")
             m1 = pair["m1"]
             m2 = pair["m2"]
             accv = acc[:].rearrange("p (h c e) -> p h c e", h=4, e=2)
             nc.vector.tensor_tensor(
                 out=m1[:, :, aq, :].rearrange("p h (c e) -> p h c e", e=2),
                 in0=accv,
-                in1=cos_a[:, a, 0, :].unsqueeze(1).unsqueeze(3).to_broadcast([P, 4, 64, 2]),
+                in1=cos_q[:, a, :].unsqueeze(1).unsqueeze(3).to_broadcast([P, 4, 64, 2]),
                 op=ALU.mult,
             )
             nc.vector.tensor_tensor(
                 out=m2[:, :, aq, :].rearrange("p h (c e) -> p h c e", e=2),
                 in0=accv[:, :, :, ::-1],
-                in1=sin_a[:, a, :, :].rearrange("p e c -> p c e").unsqueeze(1)
+                in1=sin_q[:, a, :, :].rearrange("p e c -> p c e").unsqueeze(1)
                 .to_broadcast([P, 4, 64, 2]),
                 op=ALU.mult,
             )
             if aq == 1:
-                nc.gpsimd.tensor_tensor(
-                    out=m1[:].rearrange("p h a f -> p (h a f)"),
-                    in0=m1[:].rearrange("p h a f -> p (h a f)"),
-                    in1=m2[:].rearrange("p h a f -> p (h a f)"),
-                    op=ALU.add,
-                )
-                nc.sync.dma_start(
-                    out=ov[mat][:, 4 * hg : 4 * hg + 4, a - 1 : a + 1, :], in_=m1[:]
-                )
+                parts = ((0, 2), (2, 4)) if vector_adds else ((0, 4),)
+                eng = nc.vector if vector_adds else nc.gpsimd
+                for h0, h1 in parts:
+                    eng.tensor_tensor(
+                        out=m1[:, h0:h1].rearrange("p h a f -> p (h a f)"),
+                        in0=m1[:, h0:h1].rearrange("p h a f -> p (h a f)"),
+                        in1=m2[:, h0:h1].rearrange("p h a f -> p (h a f)"),
+                        op=ALU.add,
+                    )
+                    nc.sync.dma_start(
+                        out=oq[:, 4 * c + h0 : 4 * c + h1, a - 1 : a + 1, :], in_=m1[:, h0:h1]
+                    )
 
-        def unit_b(ch, hf, h4):
-            mat, hg, kind = CHUNKS[ch]
-            acc = psa.tile([P, NC], F32, name="acc")
-            for g in range(2):
-                nc.tensor.matmul_mx(
-                    out=acc[:],
-                    lhsT=wc[ch][:, g, P * h4 : P * (h4 + 1)].bitcast(E5X4),
-                    lhsT_scale=ws[ch][:, g, P * h4 : P * (h4 + 1)],
-                    rhs=xc[hf][:, 512 * g : 512 * (g + 1)].bitcast(E5X4),
-                    rhs_scale=xs[hf][:, 512 * g : 512 * (g + 1)],
-                    start=(g == 0),
-                    stop=(g == 1),
+        def unit_k(a, vector_adds):
+            bank = {}
+            for name, es in (("a", (0,)), ("b", (1,)), ("s", (0, 1))):
+                bank[name] = psa.tile([P, NC], F32, name="acc")
+                mx(
+                    bank[name], a,
+                    [(g, wc["k%d" % g][:, e, :], ws["k%d" % g][:, e, :]) for g in range(2) for e in es],
                 )
-            m1 = prod_b.tile([P, NC], F32, name="m1b")
-            m2 = prod_b.tile([P, NC], F32, name="m2b")
-            nc.vector.tensor_tensor(
-                out=m1[:], in0=acc[:], in1=cos_f[:, 512 * hf : 512 * (hf + 1)], op=ALU.mult
-            )
-            nc.vector.tensor_tensor(
-                out=m2[:], in0=acc[:], in1=sin_f[:, 512 * hf : 512 * (hf + 1)], op=ALU.mult
-            )
-            o = pso.tile([P, 4, P], F32, name="o", tag="o")
-            for a4 in range(4):
-                nc.tensor.matmul(
-                    out=o[:, a4, :], lhsT=m1[:, P * a4 : P * (a4 + 1)],
-                    rhs=pi1[:].rearrange("p c e -> p (c e)"),
-                    start=True, stop=False, is_transpose=True,
+            k1 = prod.tile([P, H, 64], F32, name="k1")
+            k23 = prod.tile([P, 2, H, 64], F32, name="k23")
+            for dst, name, tab in ((k23[:, 1], "a", t2), (k23[:, 0], "b", t3), (k1[:], "s", cos_q)):
+                nc.vector.scalar_tensor_tensor(
+                    out=dst,
+                    in0=bank[name][:].rearrange("p (h c) -> p h c", h=H),
+                    scalar=kappa,
+                    in1=tab[:, a, :].unsqueeze(1).to_broadcast([P, H, 64]),
+                    op0=ALU.mult,
+                    op1=ALU.mult,
                 )
-                nc.tensor.matmul(
-                    out=o[:, a4, :], lhsT=m2[:, P * a4 : P * (a4 + 1)],
-                    rhs=pi2[:].rearrange("p c e -> p (c e)"),
-                    start=False, stop=True, is_transpose=True,
-                )
-            res = resp.tile([P, 4, P], F32, name="res")
-            nc.scalar.activation(
-                out=res[:].rearrange("p a f -> p (a f)"), in_=o[:].rearrange("p a f -> p (a f)"),
-                func=ACT.Copy, scale=(kappa if mat == 1 else 1.0),
+            aq = a % 2
+            if aq == 0:
+                pair["res"] = resp.tile([P, H, 2, KD], F32, name="res")
+            res = pair["res"]
+            eng = nc.vector if vector_adds else nc.gpsimd
+            eng.tensor_tensor(
+                out=res[:, :, aq, :].rearrange("p h (c e) -> p h c e", e=2),
+                in0=k1[:].unsqueeze(3).to_broadcast([P, H, 64, 2]),
+                in1=k23[:].rearrange("p e h c -> p h c e"),
+                op=ALU.add,
             )
-            nc.sync.dma_start(out=ov[mat][:, 4 * hg + h4, 4 * hf : 4 * hf + 4, :], in_=res[:])
+            if aq == 1:
+                nc.sync.dma_start(out=ok[:, :, a - 1 : a + 1, :], in_=res[:])
 
-        for a in range(6):
-            unit_a(0, a)
-        w_quantise(1, False)
-        unit_a(0, 6)
-        unit_a(0, 7)
-        for h4 in range(4):
-            unit_b(1, 0, h4)
-        w_quantise(2, False)
-        unit_a(2, 0)
-        unit_a(2, 1)
-        for h4 in range(4):
-            unit_b(1, 1, h4)
-        unit_a(2, 2)
-        unit_a(2, 3)
-        w_quantise(3, False)
-        for h4 in range(4):
-            unit_b(3, 0, h4)
-        unit_a(2, 4)
-        unit_a(2, 5)
-        unit_a(2, 6)
-        unit_a(2, 7)
-        for h4 in range(4):
-            unit_b(3, 1, h4)
+        for a in range(NT):
+            unit_q(0, a, False)
+            if a == 1:
+                k_tables()
+            if a == 5:
+                w_quantise("k0", False)
+            if a == 6:
+                w_quantise("k1", False)
+        for a in range(4):
+            unit_k(a, False)
+        w_quantise("q1", False)
+        unit_q(1, 0, False)
+        unit_q(1, 1, False)
+        unit_k(4, False)
+        unit_k(5, False)
+        unit_k(6, True)
+        unit_k(7, True)
+        for a in range(2, 6):
+            unit_q(1, a, False)
+        unit_q(1, 6, True)
+        unit_q(1, 7, True)

@@ -35,10 +35,10 @@ def tile_retnet_pa_kernel(tc, x, wq, wk, out_0, out_1):
         const = ctx.enter_context(tc.tile_pool(name="const", bufs=1))
         keep = ctx.enter_context(tc.tile_pool(name="keep", bufs=1))
         stage = ctx.enter_context(tc.tile_pool(name="stage", bufs=3))
-        prod = ctx.enter_context(tc.tile_pool(name="prod", bufs=3))
-        resp = ctx.enter_context(tc.tile_pool(name="resp", bufs=2))
+        prod = ctx.enter_context(tc.tile_pool(name="prod", bufs=4))
         psx = ctx.enter_context(tc.psum_pool(name="psx", bufs=2))
         psa = ctx.enter_context(tc.psum_pool(name="psa", bufs=6))
+        ctx.enter_context(tc.manual_schedule(engines={mybir.EngineType.Activation}))
 
         xraw = {}
         wraw = {}
@@ -49,26 +49,21 @@ def tile_retnet_pa_kernel(tc, x, wq, wk, out_0, out_1):
             nc.sync.dma_start(out=t[:], in_=xv[:, lo:hi, :])
             xraw[i] = t
 
-        def load_wq(c, g):
-            t = keep.tile([P, 4, NC], BF16, name="wqraw%d_%d" % (c, g))
-            nc.sync.dma_start(out=t[:], in_=wqv[g][:, :, NC * c : NC * (c + 1)])
-            wraw[("q", c, g)] = t
-
-        def load_wk(g):
-            t = keep.tile([P, 4, 2 * NC], BF16, name="wkraw%d" % g)
-            nc.sync.dma_start(out=t[:], in_=wkv[g])
-            wraw[("k", g)] = t
+        def load_w(c, g):
+            t = keep.tile([P, 4, NC], BF16, name="wraw%d_%d" % (c, g))
+            wv = wqv if c < 2 else wkv
+            nc.sync.dma_start(out=t[:], in_=wv[g][:, :, NC * (c % 2) : NC * (c % 2 + 1)])
+            wraw[(c, g)] = t
 
         load_x(0)
-        load_wq(0, 0)
-        load_wq(0, 1)
+        load_w(0, 0)
+        load_w(0, 1)
         load_x(1)
         load_x(2)
         load_x(3)
-        load_wk(0)
-        load_wk(1)
-        load_wq(1, 0)
-        load_wq(1, 1)
+        for c in (1, 2, 3):
+            load_w(c, 0)
+            load_w(c, 1)
 
         ones = const.tile([P, 1], F32, name="ones")
         nc.vector.memset(ones[:], 1.0)
@@ -152,12 +147,9 @@ def tile_retnet_pa_kernel(tc, x, wq, wk, out_0, out_1):
                 in_=src[:, :, n0:n1].rearrange("p j n -> p n j"),
             )
 
-        def k_src(g, e):
-            return wraw[("k", g)][:].rearrange("p j (n e) -> p e j n", e=2)[:, e]
-
         def w_quantise(key, split):
-            codes = keep.tile([P, 2, NC], U32, name="wc_%s" % key, align_bytes=64)
-            scales = keep.tile([P, 2, NC], U8, name="ws_%s" % key, align_bytes=64)
+            codes = keep.tile([P, 2, NC], U32, name="wc%d" % key, align_bytes=64)
+            scales = keep.tile([P, 2, NC], U8, name="ws%d" % key, align_bytes=64)
             if split:
                 for i in range(2):
                     nc.vector.quantize_mx(
@@ -174,9 +166,9 @@ def tile_retnet_pa_kernel(tc, x, wq, wk, out_0, out_1):
             ws[key] = scales
 
         x_prep(0)
-        new_stage("q0")
-        interleave(nc.scalar.copy, "q0", 0, wraw[("q", 0, 0)][:], 0, NC)
-        interleave(nc.vector.tensor_copy, "q0", 1, wraw[("q", 0, 1)][:], 0, NC)
+        new_stage(0)
+        interleave(nc.scalar.copy, 0, 0, wraw[(0, 0)][:], 0, NC)
+        interleave(nc.vector.tensor_copy, 0, 1, wraw[(0, 1)][:], 0, NC)
 
         sin_q = const.tile([P, NT, 2, 64], F32, name="sin_q")
         cos_q = const.tile([P, NT, 64], F32, name="cos_q")
@@ -188,45 +180,42 @@ def tile_retnet_pa_kernel(tc, x, wq, wk, out_0, out_1):
         nc.scalar.activation(out=sin_q[:, :, 0, :], in_=gneg[:], func=ACT.Sin, scale=2.0 * PI)
         nc.scalar.activation(out=sin_q[:, :, 1, :], in_=gneg[:], func=ACT.Sin, scale=-2.0 * PI)
 
-        w_quantise("q0", True)
+        w_quantise(0, True)
         x_prep(1)
-        x_prep(2)
-        x_prep(3)
 
-        for g in range(2):
-            new_stage("k%d" % g)
-            for e in range(2):
-                interleave(nc.scalar.copy, "k%d" % g, e, k_src(g, e), 0, NC)
-        new_stage("q1")
-        for g in range(2):
-            interleave(nc.scalar.copy, "q1", g, wraw[("q", 1, g)][:], 0, NC)
+        def w_prep(c):
+            new_stage(c)
+            for g in range(2):
+                interleave(nc.scalar.copy, c, g, wraw[(c, g)][:], 0, NC)
 
-        t2 = const.tile([P, NT, 64], F32, name="t2")
-        t3 = const.tile([P, NT, 64], F32, name="t3")
+        sin_k = const.tile([P, NT, 2, 64], F32, name="sin_k")
+        cos_k = const.tile([P, NT, 64], F32, name="cos_k")
+        nc.gpsimd.tensor_scalar(
+            out=cos_k[:].rearrange("p a c -> p (a c)"), in0=cos_q[:].rearrange("p a c -> p (a c)"),
+            scalar1=kappa, scalar2=0.0, op0=ALU.mult, op1=ALU.add,
+        )
+        nc.gpsimd.tensor_scalar(
+            out=sin_k[:].rearrange("p a e c -> p (a e c)"),
+            in0=sin_q[:].rearrange("p a e c -> p (a e c)"),
+            scalar1=kappa, scalar2=0.0, op0=ALU.mult, op1=ALU.add,
+        )
 
-        def k_tables():
-            nc.gpsimd.tensor_tensor(out=t2[:], in0=sin_q[:, :, 1, :], in1=cos_q[:], op=ALU.subtract)
-            nc.gpsimd.tensor_tensor(out=t3[:], in0=sin_q[:, :, 0, :], in1=cos_q[:], op=ALU.subtract)
+        pair = {}
 
-        def mx(acc, a, passes):
-            last = len(passes) - 1
-            for i, (g, codes, scales) in enumerate(passes):
+        def bank(c, a, vector_adds):
+            cos_t, sin_t, ov = (cos_q, sin_q, oq) if c < 2 else (cos_k, sin_k, ok)
+            hb = 4 * (c % 2)
+            acc = psa.tile([P, NC], F32, name="acc")
+            for g in range(2):
                 nc.tensor.matmul_mx(
                     out=acc[:],
                     lhsT=xc[a][:, P * g : P * (g + 1)].bitcast(E5X4),
                     lhsT_scale=xs[a][:, P * g : P * (g + 1)],
-                    rhs=codes.bitcast(E5X4),
-                    rhs_scale=scales,
-                    start=(i == 0),
-                    stop=(i == last),
+                    rhs=wc[c][:, g, :].bitcast(E5X4),
+                    rhs_scale=ws[c][:, g, :],
+                    start=(g == 0),
+                    stop=(g == 1),
                 )
-
-        pair = {}
-
-        def unit_q(c, a, vector_adds):
-            key = "q%d" % c
-            acc = psa.tile([P, NC], F32, name="acc")
-            mx(acc, a, [(g, wc[key][:, g, :], ws[key][:, g, :]) for g in range(2)])
             aq = a % 2
             if aq == 0:
                 pair["m1"] = prod.tile([P, 4, 2, KD], F32, name="m1")
@@ -237,13 +226,13 @@ def tile_retnet_pa_kernel(tc, x, wq, wk, out_0, out_1):
             nc.vector.tensor_tensor(
                 out=m1[:, :, aq, :].rearrange("p h (c e) -> p h c e", e=2),
                 in0=accv,
-                in1=cos_q[:, a, :].unsqueeze(1).unsqueeze(3).to_broadcast([P, 4, 64, 2]),
+                in1=cos_t[:, a, :].unsqueeze(1).unsqueeze(3).to_broadcast([P, 4, 64, 2]),
                 op=ALU.mult,
             )
             nc.vector.tensor_tensor(
                 out=m2[:, :, aq, :].rearrange("p h (c e) -> p h c e", e=2),
                 in0=accv[:, :, :, ::-1],
-                in1=sin_q[:, a, :, :].rearrange("p e c -> p c e").unsqueeze(1)
+                in1=sin_t[:, a, :, :].rearrange("p e c -> p c e").unsqueeze(1)
                 .to_broadcast([P, 4, 64, 2]),
                 op=ALU.mult,
             )
@@ -258,60 +247,19 @@ def tile_retnet_pa_kernel(tc, x, wq, wk, out_0, out_1):
                         op=ALU.add,
                     )
                     nc.sync.dma_start(
-                        out=oq[:, 4 * c + h0 : 4 * c + h1, a - 1 : a + 1, :], in_=m1[:, h0:h1]
+                        out=ov[:, hb + h0 : hb + h1, a - 1 : a + 1, :], in_=m1[:, h0:h1]
                     )
 
-        def unit_k(a, vector_adds):
-            bank = {}
-            for name, es in (("a", (0,)), ("b", (1,)), ("s", (0, 1))):
-                bank[name] = psa.tile([P, NC], F32, name="acc")
-                mx(
-                    bank[name], a,
-                    [(g, wc["k%d" % g][:, e, :], ws["k%d" % g][:, e, :]) for g in range(2) for e in es],
-                )
-            k1 = prod.tile([P, H, 64], F32, name="k1")
-            k23 = prod.tile([P, 2, H, 64], F32, name="k23")
-            for dst, name, tab in ((k23[:, 1], "a", t2), (k23[:, 0], "b", t3), (k1[:], "s", cos_q)):
-                nc.vector.scalar_tensor_tensor(
-                    out=dst,
-                    in0=bank[name][:].rearrange("p (h c) -> p h c", h=H),
-                    scalar=kappa,
-                    in1=tab[:, a, :].unsqueeze(1).to_broadcast([P, H, 64]),
-                    op0=ALU.mult,
-                    op1=ALU.mult,
-                )
-            aq = a % 2
-            if aq == 0:
-                pair["res"] = resp.tile([P, H, 2, KD], F32, name="res")
-            res = pair["res"]
-            eng = nc.vector if vector_adds else nc.gpsimd
-            eng.tensor_tensor(
-                out=res[:, :, aq, :].rearrange("p h (c e) -> p h c e", e=2),
-                in0=k1[:].unsqueeze(3).to_broadcast([P, H, 64, 2]),
-                in1=k23[:].rearrange("p e h c -> p h c e"),
-                op=ALU.add,
-            )
-            if aq == 1:
-                nc.sync.dma_start(out=ok[:, :, a - 1 : a + 1, :], in_=res[:])
-
-        for a in range(NT):
-            unit_q(0, a, False)
-            if a == 1:
-                k_tables()
-            if a == 5:
-                w_quantise("k0", False)
-            if a == 6:
-                w_quantise("k1", False)
-        for a in range(4):
-            unit_k(a, False)
-        w_quantise("q1", False)
-        unit_q(1, 0, False)
-        unit_q(1, 1, False)
-        unit_k(4, False)
-        unit_k(5, False)
-        unit_k(6, True)
-        unit_k(7, True)
-        for a in range(2, 6):
-            unit_q(1, a, False)
-        unit_q(1, 6, True)
-        unit_q(1, 7, True)
+        for c in range(4):
+            for a in range(NT):
+                bank(c, a, c == 3 and a >= 6)
+                if c == 0 and a == 0:
+                    x_prep(2)
+                if c == 0 and a == 1:
+                    x_prep(3)
+                if c == 0 and a == 2:
+                    w_prep(1)
+                if c < 2 and a == 6:
+                    w_prep(c + 2)
+                if a == 5 and c < 3:
+                    w_quantise(c + 1, False)

@@ -19,7 +19,7 @@ NC = 512
 PI = 3.141592653589793
 FLOPS = 2 * S * E * 2 * H * KD
 
-X_GROUPS = ((0, 1), (1, 2), (2, 4), (4, 8))
+X_GROUPS = ((0, 1), (1, 2), (2, 4), (4, 6), (6, 8))
 
 
 def tile_retnet_pa_kernel(tc, x, wq, wk, out_0, out_1):
@@ -36,8 +36,8 @@ def tile_retnet_pa_kernel(tc, x, wq, wk, out_0, out_1):
         keep = ctx.enter_context(tc.tile_pool(name="keep", bufs=1))
         stage = ctx.enter_context(tc.tile_pool(name="stage", bufs=3))
         prod = ctx.enter_context(tc.tile_pool(name="prod", bufs=4))
-        psx = ctx.enter_context(tc.psum_pool(name="psx", bufs=2))
-        psa = ctx.enter_context(tc.psum_pool(name="psa", bufs=6))
+        psx = ctx.enter_context(tc.psum_pool(name="psx", bufs=3))
+        psa = ctx.enter_context(tc.psum_pool(name="psa", bufs=5))
         ctx.enter_context(tc.manual_schedule(engines={mybir.EngineType.Activation}))
 
         xraw = {}
@@ -61,6 +61,7 @@ def tile_retnet_pa_kernel(tc, x, wq, wk, out_0, out_1):
         load_x(1)
         load_x(2)
         load_x(3)
+        load_x(4)
         for c in (1, 2, 3):
             load_w(c, 0)
             load_w(c, 1)
@@ -257,6 +258,7 @@ def tile_retnet_pa_kernel(tc, x, wq, wk, out_0, out_1):
                     x_prep(2)
                 if c == 0 and a == 1:
                     x_prep(3)
+                    x_prep(4)
                 if c == 0 and a == 2:
                     w_prep(1)
                 if c < 2 and a == 6:

@@ -107,6 +107,17 @@ def tile_retnet_pa_kernel(tc, x, wq, wk, out_0, out_1):
             op0=ALU.is_gt, op1=ALU.subtract,
         )
 
+        sgn = const.tile([P, 2], F32, name="sgn")
+        nc.vector.memset(sgn[:, 0:1], -1.0)
+        nc.vector.memset(sgn[:, 1:2], 1.0)
+        gpm = const.tile([P, NT, KD], F32, name="gpm")
+        nc.vector.tensor_tensor(
+            out=gpm[:].rearrange("p a (c e) -> p a c e", e=2),
+            in0=gneg[:].unsqueeze(3).to_broadcast([P, NT, 64, 2]),
+            in1=sgn[:].unsqueeze(1).unsqueeze(1).to_broadcast([P, NT, 64, 2]),
+            op=ALU.mult,
+        )
+
         xc = {}
         xs = {}
 
@@ -171,15 +182,15 @@ def tile_retnet_pa_kernel(tc, x, wq, wk, out_0, out_1):
         interleave(nc.scalar.copy, 0, 0, wraw[(0, 0)][:], 0, NC)
         interleave(nc.vector.tensor_copy, 0, 1, wraw[(0, 1)][:], 0, NC)
 
-        sin_q = const.tile([P, NT, 2, 64], F32, name="sin_q")
-        cos_q = const.tile([P, NT, 64], F32, name="cos_q")
+        tab_q = const.tile([P, NT, 2, KD], F32, name="tab_q")
         gabs = const.tile([P, NT, 64], F32, name="gabs")
         nc.scalar.activation(out=gabs[:], in_=gneg[:], func=ACT.Abs)
         nc.scalar.activation(
-            out=cos_q[:], in_=gabs[:], func=ACT.Sin, scale=-2.0 * PI, bias=halfpi[:, 0:1]
+            out=tab_q[:, :, 0, :].rearrange("p a (c e) -> p a c e", e=2),
+            in_=gabs[:].unsqueeze(3).to_broadcast([P, NT, 64, 2]),
+            func=ACT.Sin, scale=-2.0 * PI, bias=halfpi[:, 0:1],
         )
-        nc.scalar.activation(out=sin_q[:, :, 0, :], in_=gneg[:], func=ACT.Sin, scale=2.0 * PI)
-        nc.scalar.activation(out=sin_q[:, :, 1, :], in_=gneg[:], func=ACT.Sin, scale=-2.0 * PI)
+        nc.scalar.activation(out=tab_q[:, :, 1, :], in_=gpm[:], func=ACT.Sin, scale=2.0 * PI)
 
         w_quantise(0, True)
         x_prep(1)
@@ -189,22 +200,17 @@ def tile_retnet_pa_kernel(tc, x, wq, wk, out_0, out_1):
             for g in range(2):
                 interleave(nc.scalar.copy, c, g, wraw[(c, g)][:], 0, NC)
 
-        sin_k = const.tile([P, NT, 2, 64], F32, name="sin_k")
-        cos_k = const.tile([P, NT, 64], F32, name="cos_k")
+        tab_k = const.tile([P, NT, 2, KD], F32, name="tab_k")
         nc.gpsimd.tensor_scalar(
-            out=cos_k[:].rearrange("p a c -> p (a c)"), in0=cos_q[:].rearrange("p a c -> p (a c)"),
-            scalar1=kappa, scalar2=0.0, op0=ALU.mult, op1=ALU.add,
-        )
-        nc.gpsimd.tensor_scalar(
-            out=sin_k[:].rearrange("p a e c -> p (a e c)"),
-            in0=sin_q[:].rearrange("p a e c -> p (a e c)"),
+            out=tab_k[:].rearrange("p a r f -> p (a r f)"),
+            in0=tab_q[:].rearrange("p a r f -> p (a r f)"),
             scalar1=kappa, scalar2=0.0, op0=ALU.mult, op1=ALU.add,
         )
 
         pair = {}
 
         def bank(c, a, vector_adds):
-            cos_t, sin_t, ov = (cos_q, sin_q, oq) if c < 2 else (cos_k, sin_k, ok)
+            tab, ov = (tab_q, oq) if c < 2 else (tab_k, ok)
             hb = 4 * (c % 2)
             acc = psa.tile([P, NC], F32, name="acc")
             for g in range(2):
@@ -219,22 +225,13 @@ def tile_retnet_pa_kernel(tc, x, wq, wk, out_0, out_1):
                 )
             aq = a % 2
             if aq == 0:
-                pair["m1"] = prod.tile([P, 4, 2, KD], F32, name="m1")
-                pair["m2"] = prod.tile([P, 4, 2, KD], F32, name="m2")
-            m1 = pair["m1"]
-            m2 = pair["m2"]
-            accv = acc[:].rearrange("p (h c e) -> p h c e", h=4, e=2)
+                pair["m"] = prod.tile([P, 2, 4, 2, KD], F32, name="m")
+            m = pair["m"]
             nc.vector.tensor_tensor(
-                out=m1[:, :, aq, :].rearrange("p h (c e) -> p h c e", e=2),
-                in0=accv,
-                in1=cos_t[:, a, :].unsqueeze(1).unsqueeze(3).to_broadcast([P, 4, 64, 2]),
-                op=ALU.mult,
-            )
-            nc.vector.tensor_tensor(
-                out=m2[:, :, aq, :].rearrange("p h (c e) -> p h c e", e=2),
-                in0=accv[:, :, :, ::-1],
-                in1=sin_t[:, a, :, :].rearrange("p e c -> p c e").unsqueeze(1)
-                .to_broadcast([P, 4, 64, 2]),
+                out=m[:, :, :, aq, :],
+                in0=acc[:].rearrange("p (h f) -> p h f", h=4).unsqueeze(1)
+                .to_broadcast([P, 2, 4, KD]),
+                in1=tab[:, a, :, :].unsqueeze(2).to_broadcast([P, 2, 4, KD]),
                 op=ALU.mult,
             )
             if aq == 1:
@@ -242,13 +239,13 @@ def tile_retnet_pa_kernel(tc, x, wq, wk, out_0, out_1):
                 eng = nc.vector if vector_adds else nc.gpsimd
                 for h0, h1 in parts:
                     eng.tensor_tensor(
-                        out=m1[:, h0:h1].rearrange("p h a f -> p (h a f)"),
-                        in0=m1[:, h0:h1].rearrange("p h a f -> p (h a f)"),
-                        in1=m2[:, h0:h1].rearrange("p h a f -> p (h a f)"),
+                        out=m[:, 0, h0:h1].rearrange("p h a (c e) -> p (h a c) e", e=2),
+                        in0=m[:, 0, h0:h1].rearrange("p h a (c e) -> p (h a c) e", e=2),
+                        in1=m[:, 1, h0:h1].rearrange("p h a (c e) -> p (h a c) e", e=2)[:, :, ::-1],
                         op=ALU.add,
                     )
                     nc.sync.dma_start(
-                        out=ov[:, hb + h0 : hb + h1, a - 1 : a + 1, :], in_=m1[:, h0:h1]
+                        out=ov[:, hb + h0 : hb + h1, a - 1 : a + 1, :], in_=m[:, 0, h0:h1]
                     )
 
         for c in range(4):

@@ -16,10 +16,12 @@ S, E, H, KD = 1024, 1024, 8, 128
 P = 128
 NT = S // P
 NC = 512
+NF = KD // 2
 PI = 3.141592653589793
 FLOPS = 2 * S * E * 2 * H * KD
 
 X_GROUPS = ((0, 1), (1, 2), (2, 4), (4, 6), (6, 8))
+TAB_PARTS = ((0, 2), (2, 8))
 
 
 def tile_retnet_pa_kernel(tc, x, wq, wk, out_0, out_1):
@@ -38,7 +40,7 @@ def tile_retnet_pa_kernel(tc, x, wq, wk, out_0, out_1):
         prod = ctx.enter_context(tc.tile_pool(name="prod", bufs=4))
         psx = ctx.enter_context(tc.psum_pool(name="psx", bufs=3))
         psa = ctx.enter_context(tc.psum_pool(name="psa", bufs=5))
-        ctx.enter_context(tc.manual_schedule(engines={mybir.EngineType.Activation}))
+        ctx.enter_context(tc.manual_schedule())
 
         xraw = {}
         wraw = {}
@@ -70,15 +72,15 @@ def tile_retnet_pa_kernel(tc, x, wq, wk, out_0, out_1):
         nc.vector.memset(ones[:], 1.0)
         junk = const.tile([P, 1], F32, name="junk")
         nc.scalar.activation(out=junk[:], in_=ones[:], func=ACT.Sin)
-        idx = const.tile([P, NT, 64], F32, name="idx")
+        idx = const.tile([P, NT, NF], F32, name="idx")
         nc.gpsimd.iota(
-            idx[:], pattern=[[1, NT], [0, 64]], base=0, channel_multiplier=NT,
+            idx[:], pattern=[[1, NT], [0, NF]], base=0, channel_multiplier=NT,
             allow_small_or_imprecise_dtypes=True,
         )
         ident = const.tile([P, P], F32, name="ident")
         make_identity(nc, ident[:])
         ratio = 10000.0 ** (-1.0 / 63.0)
-        nu = const.tile([P, 64], F32, name="nu")
+        nu = const.tile([P, NF], F32, name="nu")
         for j in range(4):
             nc.vector.tensor_scalar_mul(
                 out=nu[:, j : j + 1], in0=ones[:], scalar1=ratio**j / (2.0 * PI)
@@ -90,58 +92,94 @@ def tile_retnet_pa_kernel(tc, x, wq, wk, out_0, out_1):
                 )
         halfpi = const.tile([P, 1], F32, name="halfpi")
         nc.vector.tensor_scalar_mul(out=halfpi[:], in0=ones[:], scalar1=PI / 2.0)
-        ph = const.tile([P, NT, 64], F32, name="ph")
-        nc.vector.tensor_tensor(
-            out=ph[:], in0=idx[:], in1=nu[:].unsqueeze(1).to_broadcast([P, NT, 64]), op=ALU.mult
-        )
-        ki = const.tile([P, NT * 64], I32, name="ki")
-        nc.vector.tensor_copy(out=ki[:], in_=ph[:].rearrange("p a c -> p (a c)"))
-        fr = const.tile([P, NT * 64], F32, name="fr")
-        nc.vector.scalar_tensor_tensor(
-            out=fr[:], in0=ki[:], scalar=-1.0, in1=ph[:].rearrange("p a c -> p (a c)"),
-            op0=ALU.mult, op1=ALU.add,
-        )
-        gneg = const.tile([P, NT, 64], F32, name="gneg")
-        nc.vector.scalar_tensor_tensor(
-            out=gneg[:].rearrange("p a c -> p (a c)"), in0=fr[:], scalar=0.5, in1=fr[:],
-            op0=ALU.is_gt, op1=ALU.subtract,
-        )
 
         sgn = const.tile([P, 2], F32, name="sgn")
         nc.vector.memset(sgn[:, 0:1], -1.0)
         nc.vector.memset(sgn[:, 1:2], 1.0)
-        gpm = const.tile([P, NT, KD], F32, name="gpm")
-        nc.vector.tensor_tensor(
-            out=gpm[:].rearrange("p a (c e) -> p a c e", e=2),
-            in0=gneg[:].unsqueeze(3).to_broadcast([P, NT, 64, 2]),
-            in1=sgn[:].unsqueeze(1).unsqueeze(1).to_broadcast([P, NT, 64, 2]),
-            op=ALU.mult,
-        )
 
+        ph = const.tile([P, NT, NF], F32, name="ph")
+        ki = const.tile([P, NT, NF], I32, name="ki")
+        fr = const.tile([P, NT, NF], F32, name="fr")
+        gneg = const.tile([P, NT, NF], F32, name="gneg")
+        gabs = const.tile([P, NT, NF], F32, name="gabs")
+        gpm = const.tile([P, NT, KD], F32, name="gpm")
+        tab_q = const.tile([P, NT, 2, KD], F32, name="tab_q")
+        tab_k = const.tile([P, NT, 2, KD], F32, name="tab_k")
+
+        def phases(lo, hi):
+            n = hi - lo
+            nc.vector.tensor_tensor(
+                out=ph[:, lo:hi, :], in0=idx[:, lo:hi, :],
+                in1=nu[:].unsqueeze(1).to_broadcast([P, n, NF]), op=ALU.mult,
+            )
+
+            def flat(t):
+                return t[:, lo:hi, :].rearrange("p a c -> p (a c)")
+
+            nc.vector.tensor_copy(out=flat(ki), in_=flat(ph))
+            nc.vector.scalar_tensor_tensor(
+                out=flat(fr), in0=flat(ki), scalar=-1.0, in1=flat(ph), op0=ALU.mult, op1=ALU.add
+            )
+            nc.vector.scalar_tensor_tensor(
+                out=flat(gneg), in0=flat(fr), scalar=0.5, in1=flat(fr),
+                op0=ALU.is_gt, op1=ALU.subtract,
+            )
+            nc.vector.scalar_tensor_tensor(
+                out=flat(gabs), in0=flat(gneg), scalar=-1.0, in1=flat(gneg),
+                op0=ALU.mult, op1=ALU.max,
+            )
+
+        def signed_phases(lo, hi):
+            n = hi - lo
+            nc.vector.tensor_tensor(
+                out=gpm[:, lo:hi, :].rearrange("p a (c e) -> p a c e", e=2),
+                in0=gneg[:, lo:hi, :].unsqueeze(3).to_broadcast([P, n, NF, 2]),
+                in1=sgn[:].unsqueeze(1).unsqueeze(1).to_broadcast([P, n, NF, 2]),
+                op=ALU.mult,
+            )
+
+        def tables(lo, hi):
+            n = hi - lo
+            nc.scalar.activation(
+                out=tab_q[:, lo:hi, 0, :].rearrange("p a (c e) -> p a c e", e=2),
+                in_=gabs[:, lo:hi, :].unsqueeze(3).to_broadcast([P, n, NF, 2]),
+                func=ACT.Sin, scale=-2.0 * PI, bias=halfpi[:, 0:1],
+            )
+            nc.scalar.activation(
+                out=tab_q[:, lo:hi, 1, :], in_=gpm[:, lo:hi, :], func=ACT.Sin, scale=2.0 * PI
+            )
+
+        xg = {}
+        xt = {}
         xc = {}
         xs = {}
 
-        def x_prep(i):
+        def x_turn(i, t):
+            words = xraw[i][:, t, :].bitcast(F32)
+            xt[(i, t)] = psx.tile([P, 2, 2, P], F32, name="xt")
+            for g in range(2):
+                for u in range(2):
+                    nc.tensor.transpose(
+                        xt[(i, t)][:, g, u, :], words[:, 256 * g + u : 256 * (g + 1) : 2], ident[:]
+                    )
+
+        def x_copy(i, t):
+            lo, hi = X_GROUPS[i]
+            if t == 0:
+                xg[i] = keep.tile([P, (hi - lo) * 1024], BF16, name="xg%d" % i, align_bytes=64)
+            nc.scalar.copy(
+                out=xg[i][:, 1024 * t : 1024 * (t + 1)]
+                .bitcast(F32)
+                .rearrange("p (g r u) -> p g r u", g=2, u=2),
+                in_=xt[(i, t)][:].rearrange("p g u r -> p g r u"),
+            )
+
+        def x_quantise(i):
             lo, hi = X_GROUPS[i]
             n = hi - lo
-            xg = keep.tile([P, n * 1024], BF16, name="xg%d" % i, align_bytes=64)
-            for t in range(n):
-                words = xraw[i][:, t, :].bitcast(F32)
-                xt = psx.tile([P, 2, 2, P], F32, name="xt")
-                for g in range(2):
-                    for u in range(2):
-                        nc.tensor.transpose(
-                            xt[:, g, u, :], words[:, 256 * g + u : 256 * (g + 1) : 2], ident[:]
-                        )
-                nc.scalar.copy(
-                    out=xg[:, 1024 * t : 1024 * (t + 1)]
-                    .bitcast(F32)
-                    .rearrange("p (g r u) -> p g r u", g=2, u=2),
-                    in_=xt[:].rearrange("p g u r -> p g r u"),
-                )
             codes = keep.tile([P, n * 256], U32, name="xc%d" % i, align_bytes=64)
             scales = keep.tile([P, n * 256], U8, name="xs%d" % i, align_bytes=64)
-            nc.vector.quantize_mx(out=codes[:].bitcast(E5X4), scales=scales[:], in_=xg[:])
+            nc.vector.quantize_mx(out=codes[:].bitcast(E5X4), scales=scales[:], in_=xg[i][:])
             for t in range(n):
                 xc[lo + t] = codes[:, 256 * t : 256 * (t + 1)]
                 xs[lo + t] = scales[:, 256 * t : 256 * (t + 1)]
@@ -152,66 +190,36 @@ def tile_retnet_pa_kernel(tc, x, wq, wk, out_0, out_1):
 
         def new_stage(key):
             wgr[key] = stage.tile([P, 2, 4 * NC], BF16, name="wgr", align_bytes=64)
+            wc[key] = keep.tile([P, 2, NC], U32, name="wc%d" % key, align_bytes=64)
+            ws[key] = keep.tile([P, 2, NC], U8, name="ws%d" % key, align_bytes=64)
 
-        def interleave(cp, key, piece, src, n0, n1):
+        def interleave(cp, key, piece):
             cp(
-                out=wgr[key][:, piece, 4 * n0 : 4 * n1].rearrange("p (n j) -> p n j", j=4),
-                in_=src[:, :, n0:n1].rearrange("p j n -> p n j"),
+                out=wgr[key][:, piece, :].rearrange("p (n j) -> p n j", j=4),
+                in_=wraw[(key, piece)][:].rearrange("p j n -> p n j"),
             )
 
-        def w_quantise(key, split):
-            codes = keep.tile([P, 2, NC], U32, name="wc%d" % key, align_bytes=64)
-            scales = keep.tile([P, 2, NC], U8, name="ws%d" % key, align_bytes=64)
-            if split:
-                for i in range(2):
-                    nc.vector.quantize_mx(
-                        out=codes[:, i, :].bitcast(E5X4), scales=scales[:, i, :],
-                        in_=wgr[key][:, i, :],
-                    )
-            else:
-                nc.vector.quantize_mx(
-                    out=codes[:].rearrange("p g n -> p (g n)").bitcast(E5X4),
-                    scales=scales[:].rearrange("p g n -> p (g n)"),
-                    in_=wgr[key][:].rearrange("p g n -> p (g n)"),
-                )
-            wc[key] = codes
-            ws[key] = scales
+        def w_quantise_piece(key, i):
+            nc.vector.quantize_mx(
+                out=wc[key][:, i, :].bitcast(E5X4), scales=ws[key][:, i, :], in_=wgr[key][:, i, :]
+            )
 
-        x_prep(0)
-        new_stage(0)
-        interleave(nc.scalar.copy, 0, 0, wraw[(0, 0)][:], 0, NC)
-        interleave(nc.vector.tensor_copy, 0, 1, wraw[(0, 1)][:], 0, NC)
-
-        tab_q = const.tile([P, NT, 2, KD], F32, name="tab_q")
-        gabs = const.tile([P, NT, 64], F32, name="gabs")
-        nc.scalar.activation(out=gabs[:], in_=gneg[:], func=ACT.Abs)
-        nc.scalar.activation(
-            out=tab_q[:, :, 0, :].rearrange("p a (c e) -> p a c e", e=2),
-            in_=gabs[:].unsqueeze(3).to_broadcast([P, NT, 64, 2]),
-            func=ACT.Sin, scale=-2.0 * PI, bias=halfpi[:, 0:1],
-        )
-        nc.scalar.activation(out=tab_q[:, :, 1, :], in_=gpm[:], func=ACT.Sin, scale=2.0 * PI)
-
-        w_quantise(0, True)
-        x_prep(1)
+        def w_quantise(key):
+            nc.vector.quantize_mx(
+                out=wc[key][:].rearrange("p g n -> p (g n)").bitcast(E5X4),
+                scales=ws[key][:].rearrange("p g n -> p (g n)"),
+                in_=wgr[key][:].rearrange("p g n -> p (g n)"),
+            )
 
         def w_prep(c):
             new_stage(c)
             for g in range(2):
-                interleave(nc.scalar.copy, c, g, wraw[(c, g)][:], 0, NC)
+                interleave(nc.scalar.copy, c, g)
 
-        tab_k = const.tile([P, NT, 2, KD], F32, name="tab_k")
-        nc.gpsimd.tensor_scalar(
-            out=tab_k[:].rearrange("p a r f -> p (a r f)"),
-            in0=tab_q[:].rearrange("p a r f -> p (a r f)"),
-            scalar1=kappa, scalar2=0.0, op0=ALU.mult, op1=ALU.add,
-        )
-
+        accs = {}
         pair = {}
 
-        def bank(c, a, vector_adds):
-            tab, ov = (tab_q, oq) if c < 2 else (tab_k, ok)
-            hb = 4 * (c % 2)
+        def multiply(c, a):
             acc = psa.tile([P, NC], F32, name="acc")
             for g in range(2):
                 nc.tensor.matmul_mx(
@@ -223,13 +231,18 @@ def tile_retnet_pa_kernel(tc, x, wq, wk, out_0, out_1):
                     start=(g == 0),
                     stop=(g == 1),
                 )
+            accs[(c, a)] = acc
+
+        def rotate(c, a, vector_adds):
+            tab, ov = (tab_q, oq) if c < 2 else (tab_k, ok)
+            hb = 4 * (c % 2)
             aq = a % 2
             if aq == 0:
                 pair["m"] = prod.tile([P, 2, 4, 2, KD], F32, name="m")
             m = pair["m"]
             nc.vector.tensor_tensor(
                 out=m[:, :, :, aq, :],
-                in0=acc[:].rearrange("p (h f) -> p h f", h=4).unsqueeze(1)
+                in0=accs[(c, a)][:].rearrange("p (h f) -> p h f", h=4).unsqueeze(1)
                 .to_broadcast([P, 2, 4, KD]),
                 in1=tab[:, a, :, :].unsqueeze(2).to_broadcast([P, 2, 4, KD]),
                 op=ALU.mult,
@@ -248,17 +261,63 @@ def tile_retnet_pa_kernel(tc, x, wq, wk, out_0, out_1):
                         out=ov[:, hb + h0 : hb + h1, a - 1 : a + 1, :], in_=m[:, 0, h0:h1]
                     )
 
-        for c in range(4):
+        phases(*TAB_PARTS[0])
+        signed_phases(*TAB_PARTS[0])
+        tables(*TAB_PARTS[0])
+        phases(*TAB_PARTS[1])
+        x_turn(0, 0)
+        x_copy(0, 0)
+        new_stage(0)
+        interleave(nc.scalar.copy, 0, 0)
+        x_quantise(0)
+        interleave(nc.vector.tensor_copy, 0, 1)
+        w_quantise_piece(0, 1)
+        w_quantise_piece(0, 0)
+        x_turn(1, 0)
+        x_copy(1, 0)
+        for t in range(2):
+            x_turn(2, t)
+            x_copy(2, t)
+        x_quantise(1)
+        signed_phases(*TAB_PARTS[1])
+        multiply(0, 0)
+        multiply(0, 1)
+        tables(*TAB_PARTS[1])
+        rotate(0, 0, False)
+        x_quantise(2)
+        for t in range(2):
+            x_turn(3, t)
+            x_copy(3, t)
+        rotate(0, 1, False)
+        multiply(0, 2)
+        multiply(0, 3)
+        rotate(0, 2, False)
+        x_quantise(3)
+        for t in range(2):
+            x_turn(4, t)
+            x_copy(4, t)
+        rotate(0, 3, False)
+        multiply(0, 4)
+        multiply(0, 5)
+        rotate(0, 4, False)
+        x_quantise(4)
+        rotate(0, 5, False)
+        multiply(0, 6)
+        multiply(0, 7)
+        w_prep(1)
+        rotate(0, 6, False)
+        w_quantise(1)
+        rotate(0, 7, False)
+        w_prep(2)
+        nc.scalar.mul(
+            out=tab_k[:].rearrange("p a r f -> p (a r f)"),
+            in_=tab_q[:].rearrange("p a r f -> p (a r f)"),
+            mul=kappa,
+        )
+        w_prep(3)
+        for c in range(1, 4):
             for a in range(NT):
-                bank(c, a, c == 3 and a >= 6)
-                if c == 0 and a == 0:
-                    x_prep(2)
-                if c == 0 and a == 1:
-                    x_prep(3)
-                    x_prep(4)
-                if c == 0 and a == 2:
-                    w_prep(1)
-                if c < 2 and a == 6:
-                    w_prep(c + 2)
+                multiply(c, a)
+                rotate(c, a, c == 3 and a >= 6)
                 if a == 5 and c < 3:
-                    w_quantise(c + 1, False)
+                    w_quantise(c + 1)

@@ -21,7 +21,8 @@ PI = 3.141592653589793
 FLOPS = 2 * S * E * 2 * H * KD
 
 X_GROUPS = ((0, 1), (1, 2), (2, 4), (4, 6), (6, 8))
-TAB_PARTS = ((0, 2), (2, 8))
+AHEAD = 3
+NA = 4
 
 
 def tile_retnet_pa_kernel(tc, x, wq, wk, out_0, out_1):
@@ -36,8 +37,10 @@ def tile_retnet_pa_kernel(tc, x, wq, wk, out_0, out_1):
     with ExitStack() as ctx:
         const = ctx.enter_context(tc.tile_pool(name="const", bufs=1))
         keep = ctx.enter_context(tc.tile_pool(name="keep", bufs=1))
-        stage = ctx.enter_context(tc.tile_pool(name="stage", bufs=3))
+        stage = ctx.enter_context(tc.tile_pool(name="stage", bufs=2))
         prod = ctx.enter_context(tc.tile_pool(name="prod", bufs=4))
+        prodt = ctx.enter_context(tc.tile_pool(name="prodt", bufs=4))
+        outt = ctx.enter_context(tc.tile_pool(name="outt", bufs=3))
         psx = ctx.enter_context(tc.psum_pool(name="psx", bufs=3))
         psa = ctx.enter_context(tc.psum_pool(name="psa", bufs=5))
         ctx.enter_context(tc.manual_schedule())
@@ -104,7 +107,10 @@ def tile_retnet_pa_kernel(tc, x, wq, wk, out_0, out_1):
         gabs = const.tile([P, NT, NF], F32, name="gabs")
         gpm = const.tile([P, NT, KD], F32, name="gpm")
         tab_q = const.tile([P, NT, 2, KD], F32, name="tab_q")
-        tab_k = const.tile([P, NT, 2, KD], F32, name="tab_k")
+        tab_k = const.tile([P, NA, 2, KD], F32, name="tab_k")
+        tab_t = const.tile([P, 2, NC], F32, name="tab_t")
+        perm = const.tile([P, P], F32, name="perm")
+        late = const.tile([P, 1], F32, name="late")
 
         def phases(lo, hi):
             n = hi - lo
@@ -163,16 +169,23 @@ def tile_retnet_pa_kernel(tc, x, wq, wk, out_0, out_1):
                         xt[(i, t)][:, g, u, :], words[:, 256 * g + u : 256 * (g + 1) : 2], ident[:]
                     )
 
+        xg_b = keep.tile([P, 2, NT - NA, NC], BF16, name="xg_b", align_bytes=64)
+        xc_b = keep.tile([P, 2, NT - NA, P], U32, name="xc_b", align_bytes=64)
+        xs_b = keep.tile([P, 2, NT - NA, P], U8, name="xs_b", align_bytes=64)
+
         def x_copy(i, t):
             lo, hi = X_GROUPS[i]
-            if t == 0:
-                xg[i] = keep.tile([P, (hi - lo) * 1024], BF16, name="xg%d" % i, align_bytes=64)
-            nc.scalar.copy(
-                out=xg[i][:, 1024 * t : 1024 * (t + 1)]
-                .bitcast(F32)
-                .rearrange("p (g r u) -> p g r u", g=2, u=2),
-                in_=xt[(i, t)][:].rearrange("p g u r -> p g r u"),
-            )
+            if lo >= NA:
+                dst = xg_b[:, :, lo + t - NA, :].bitcast(F32).rearrange("p g (r u) -> p g r u", u=2)
+            else:
+                if t == 0:
+                    xg[i] = keep.tile([P, (hi - lo) * 1024], BF16, name="xg%d" % i, align_bytes=64)
+                dst = (
+                    xg[i][:, 1024 * t : 1024 * (t + 1)]
+                    .bitcast(F32)
+                    .rearrange("p (g r u) -> p g r u", g=2, u=2)
+                )
+            nc.scalar.copy(out=dst, in_=xt[(i, t)][:].rearrange("p g u r -> p g r u"))
 
         def x_quantise(i):
             lo, hi = X_GROUPS[i]
@@ -181,8 +194,20 @@ def tile_retnet_pa_kernel(tc, x, wq, wk, out_0, out_1):
             scales = keep.tile([P, n * 256], U8, name="xs%d" % i, align_bytes=64)
             nc.vector.quantize_mx(out=codes[:].bitcast(E5X4), scales=scales[:], in_=xg[i][:])
             for t in range(n):
-                xc[lo + t] = codes[:, 256 * t : 256 * (t + 1)]
-                xs[lo + t] = scales[:, 256 * t : 256 * (t + 1)]
+                for g in range(2):
+                    xc[(lo + t, g)] = codes[:, 256 * t + P * g : 256 * t + P * (g + 1)]
+                    xs[(lo + t, g)] = scales[:, 256 * t + P * g : 256 * t + P * (g + 1)]
+
+        def x_quantise_b():
+            nc.vector.quantize_mx(
+                out=xc_b[:].rearrange("p g a r -> p (g a r)").bitcast(E5X4),
+                scales=xs_b[:].rearrange("p g a r -> p (g a r)"),
+                in_=xg_b[:].rearrange("p g a n -> p (g a n)"),
+            )
+            for a in range(NA, NT):
+                for g in range(2):
+                    xc[(a, g)] = xc_b[:, g, a - NA, :]
+                    xs[(a, g)] = xs_b[:, g, a - NA, :]
 
         wgr = {}
         wc = {}
@@ -224,8 +249,8 @@ def tile_retnet_pa_kernel(tc, x, wq, wk, out_0, out_1):
             for g in range(2):
                 nc.tensor.matmul_mx(
                     out=acc[:],
-                    lhsT=xc[a][:, P * g : P * (g + 1)].bitcast(E5X4),
-                    lhsT_scale=xs[a][:, P * g : P * (g + 1)],
+                    lhsT=xc[(a, g)].bitcast(E5X4),
+                    lhsT_scale=xs[(a, g)],
                     rhs=wc[c][:, g, :].bitcast(E5X4),
                     rhs_scale=ws[c][:, g, :],
                     start=(g == 0),
@@ -233,13 +258,12 @@ def tile_retnet_pa_kernel(tc, x, wq, wk, out_0, out_1):
                 )
             accs[(c, a)] = acc
 
-        def rotate(c, a, vector_adds):
-            tab, ov = (tab_q, oq) if c < 2 else (tab_k, ok)
-            hb = 4 * (c % 2)
+        def rotate(c, a):
+            tab = tab_q if c < 2 else tab_k
             aq = a % 2
             if aq == 0:
-                pair["m"] = prod.tile([P, 2, 4, 2, KD], F32, name="m")
-            m = pair["m"]
+                pair[(c, a // 2)] = prod.tile([P, 2, 4, 2, KD], F32, name="m")
+            m = pair[(c, a // 2)]
             nc.vector.tensor_tensor(
                 out=m[:, :, :, aq, :],
                 in0=accs[(c, a)][:].rearrange("p (h f) -> p h f", h=4).unsqueeze(1)
@@ -247,24 +271,83 @@ def tile_retnet_pa_kernel(tc, x, wq, wk, out_0, out_1):
                 in1=tab[:, a, :, :].unsqueeze(2).to_broadcast([P, 2, 4, KD]),
                 op=ALU.mult,
             )
-            if aq == 1:
-                parts = ((0, 2), (2, 4)) if vector_adds else ((0, 4),)
-                eng = nc.vector if vector_adds else nc.gpsimd
-                for h0, h1 in parts:
-                    eng.tensor_tensor(
-                        out=m[:, 0, h0:h1].rearrange("p h a (c e) -> p (h a c) e", e=2),
-                        in0=m[:, 0, h0:h1].rearrange("p h a (c e) -> p (h a c) e", e=2),
-                        in1=m[:, 1, h0:h1].rearrange("p h a (c e) -> p (h a c) e", e=2)[:, :, ::-1],
-                        op=ALU.add,
-                    )
-                    nc.sync.dma_start(
-                        out=ov[:, hb + h0 : hb + h1, a - 1 : a + 1, :], in_=m[:, 0, h0:h1]
-                    )
 
-        phases(*TAB_PARTS[0])
-        signed_phases(*TAB_PARTS[0])
-        tables(*TAB_PARTS[0])
-        phases(*TAB_PARTS[1])
+        def add_pair(c, b):
+            ov = oq if c < 2 else ok
+            hb = 4 * (c % 2)
+            m = pair[(c, b)]
+            nc.gpsimd.tensor_tensor(
+                out=m[:, 0].rearrange("p h a (c e) -> p (h a c) e", e=2),
+                in0=m[:, 0].rearrange("p h a (c e) -> p (h a c) e", e=2),
+                in1=m[:, 1].rearrange("p h a (c e) -> p (h a c) e", e=2)[:, :, ::-1],
+                op=ALU.add,
+            )
+            nc.sync.dma_start(out=ov[:, hb : hb + 4, 2 * b : 2 * b + 2, :], in_=m[:, 0])
+
+        mts = {}
+
+        def multiply_t(c, h):
+            acc = psa.tile([P, NC], F32, name="acc")
+            for g in range(2):
+                nc.tensor.matmul_mx(
+                    out=acc[:],
+                    lhsT=wc[c][:, g, P * h : P * (h + 1)].bitcast(E5X4),
+                    lhsT_scale=ws[c][:, g, P * h : P * (h + 1)],
+                    rhs=xc_b[:, g].rearrange("p a r -> p (a r)").bitcast(E5X4),
+                    rhs_scale=xs_b[:, g].rearrange("p a r -> p (a r)"),
+                    start=(g == 0),
+                    stop=(g == 1),
+                )
+            accs[(c, "t", h)] = acc
+
+        def rotate_t(c, h):
+            mt = prodt.tile([P, 2, NC], F32, name="mt")
+            nc.vector.tensor_tensor(
+                out=mt[:],
+                in0=accs[(c, "t", h)][:].unsqueeze(1).to_broadcast([P, 2, NC]),
+                in1=tab_t[:],
+                op=ALU.mult,
+            )
+            mts[(c, h)] = mt
+
+        def turn_add_store(c, h):
+            mt = mts[(c, h)]
+            o = psx.tile([P, NT - NA, P], F32, name="xt")
+            for t in range(NT - NA):
+                nc.tensor.matmul(
+                    out=o[:, t, :], lhsT=mt[:, 0, P * t : P * (t + 1)], rhs=ident[:],
+                    start=True, stop=False, is_transpose=True,
+                )
+                nc.tensor.matmul(
+                    out=o[:, t, :], lhsT=mt[:, 1, P * t : P * (t + 1)], rhs=perm[:],
+                    start=False, stop=True, is_transpose=True,
+                )
+            r = outt.tile([P, NT - NA, KD], F32, name="r")
+            if c < 2:
+                nc.scalar.copy(
+                    out=r[:].rearrange("p a f -> p (a f)"), in_=o[:].rearrange("p a f -> p (a f)")
+                )
+            else:
+                nc.scalar.mul(
+                    out=r[:].rearrange("p a f -> p (a f)"), in_=o[:].rearrange("p a f -> p (a f)"),
+                    mul=kappa,
+                )
+            ov = oq if c < 2 else ok
+            nc.sync.dma_start(out=ov[:, 4 * (c % 2) + h, NA:NT, :], in_=r[:])
+
+        def tables_t_turn(rep):
+            tt = psx.tile([P, NT - NA, P], F32, name="xt")
+            for t in range(NT - NA):
+                nc.tensor.transpose(tt[:, t, :], tab_q[:, NA + t, rep, :], ident[:])
+            return tt
+
+        def tables_t_copy(rep, tt):
+            nc.scalar.copy(out=tab_t[:, rep, :], in_=tt[:].rearrange("p a r -> p (a r)"))
+
+        phases(0, 2)
+        signed_phases(0, 2)
+        tables(0, 2)
+        phases(2, NT)
         x_turn(0, 0)
         x_copy(0, 0)
         new_stage(0)
@@ -279,45 +362,92 @@ def tile_retnet_pa_kernel(tc, x, wq, wk, out_0, out_1):
             x_turn(2, t)
             x_copy(2, t)
         x_quantise(1)
-        signed_phases(*TAB_PARTS[1])
+        signed_phases(2, NT)
         multiply(0, 0)
         multiply(0, 1)
-        tables(*TAB_PARTS[1])
-        rotate(0, 0, False)
+        tables(2, NA)
+        rotate(0, 0)
         x_quantise(2)
         for t in range(2):
             x_turn(3, t)
             x_copy(3, t)
-        rotate(0, 1, False)
+        x_turn(4, 0)
+        x_copy(4, 0)
         multiply(0, 2)
+        x_turn(4, 1)
+        x_copy(4, 1)
         multiply(0, 3)
-        rotate(0, 2, False)
-        x_quantise(3)
-        for t in range(2):
-            x_turn(4, t)
-            x_copy(4, t)
-        rotate(0, 3, False)
+        tables(NA, NT)
+        tt0 = tables_t_turn(0)
+        tt1 = tables_t_turn(1)
+        rotate(0, 1)
+        rotate(0, 2)
+        x_quantise_b()
+        nc.vector.memset(late[:], 1.0)
+        nc.gpsimd.tensor_scalar(
+            out=perm[:].rearrange("p (c e) -> p c e", e=2),
+            in0=ident[:].rearrange("p (c e) -> p c e", e=2)[:, :, ::-1],
+            scalar1=late[:, 0:1], scalar2=0.0, op0=ALU.mult, op1=ALU.add,
+        )
+        add_pair(0, 0)
         multiply(0, 4)
         multiply(0, 5)
-        rotate(0, 4, False)
-        x_quantise(4)
-        rotate(0, 5, False)
         multiply(0, 6)
+        rotate(0, 3)
+        add_pair(0, 1)
         multiply(0, 7)
+        rotate(0, 4)
+        rotate(0, 5)
+        add_pair(0, 2)
         w_prep(1)
-        rotate(0, 6, False)
+        tables_t_copy(0, tt0)
+        tables_t_copy(1, tt1)
+        rotate(0, 6)
         w_quantise(1)
-        rotate(0, 7, False)
+
+        seq = []
+        for c in (1, 2):
+            for h in range(4):
+                seq.append(("t", c, h))
+            for a in range(NA):
+                seq.append(("a", c, a))
+        for a in range(NA):
+            seq.append(("a", 3, a))
+        for h in range(4):
+            seq.append(("t", 3, h))
+
+        def issue(kind, c, i):
+            if kind == "t":
+                multiply_t(c, i)
+            else:
+                multiply(c, i)
+
+        for j in range(AHEAD):
+            issue(*seq[j])
+        rotate(0, 7)
+        add_pair(0, 3)
         w_prep(2)
-        nc.scalar.mul(
-            out=tab_k[:].rearrange("p a r f -> p (a r f)"),
-            in_=tab_q[:].rearrange("p a r f -> p (a r f)"),
-            mul=kappa,
-        )
-        w_prep(3)
-        for c in range(1, 4):
-            for a in range(NT):
-                multiply(c, a)
-                rotate(c, a, c == 3 and a >= 6)
-                if a == 5 and c < 3:
-                    w_quantise(c + 1)
+        quantised = {0, 1}
+        for j in range(len(seq)):
+            if j + AHEAD < len(seq):
+                kind, c, i = seq[j + AHEAD]
+                if c not in quantised:
+                    w_quantise(c)
+                    quantised.add(c)
+                issue(kind, c, i)
+            kind, c, i = seq[j]
+            if kind == "t":
+                rotate_t(c, i)
+                turn_add_store(c, i)
+            else:
+                rotate(c, i)
+                if i % 2 == 1:
+                    add_pair(c, i // 2)
+            if j == 2:
+                nc.scalar.mul(
+                    out=tab_k[:].rearrange("p a r f -> p (a r f)"),
+                    in_=tab_q[:, 0:NA].rearrange("p a r f -> p (a r f)"),
+                    mul=kappa,
+                )
+            if j == 3:
+                w_prep(3)

@@ -21,6 +21,8 @@ PI = 3.141592653589793
 FLOPS = 2 * S * E * 2 * H * KD
 
 X_GROUPS = ((0, 1), (1, 2), (2, 4), (4, 6), (6, 8))
+WHOLE = ((0, 4),)
+HALVES = ((0, 2), (2, 4))
 AHEAD = 3
 NA = 4
 
@@ -272,17 +274,20 @@ def tile_retnet_pa_kernel(tc, x, wq, wk, out_0, out_1):
                 op=ALU.mult,
             )
 
-        def add_pair(c, b):
+        def add_pair(c, b, eng, parts):
             ov = oq if c < 2 else ok
             hb = 4 * (c % 2)
             m = pair[(c, b)]
-            nc.gpsimd.tensor_tensor(
-                out=m[:, 0].rearrange("p h a (c e) -> p (h a c) e", e=2),
-                in0=m[:, 0].rearrange("p h a (c e) -> p (h a c) e", e=2),
-                in1=m[:, 1].rearrange("p h a (c e) -> p (h a c) e", e=2)[:, :, ::-1],
-                op=ALU.add,
-            )
-            nc.sync.dma_start(out=ov[:, hb : hb + 4, 2 * b : 2 * b + 2, :], in_=m[:, 0])
+            for h0, h1 in parts:
+                eng.tensor_tensor(
+                    out=m[:, 0, h0:h1].rearrange("p h a (c e) -> p (h a c) e", e=2),
+                    in0=m[:, 0, h0:h1].rearrange("p h a (c e) -> p (h a c) e", e=2),
+                    in1=m[:, 1, h0:h1].rearrange("p h a (c e) -> p (h a c) e", e=2)[:, :, ::-1],
+                    op=ALU.add,
+                )
+                nc.sync.dma_start(
+                    out=ov[:, hb + h0 : hb + h1, 2 * b : 2 * b + 2, :], in_=m[:, 0, h0:h1]
+                )
 
         mts = {}
 
@@ -333,7 +338,7 @@ def tile_retnet_pa_kernel(tc, x, wq, wk, out_0, out_1):
                     mul=kappa,
                 )
             ov = oq if c < 2 else ok
-            nc.sync.dma_start(out=ov[:, 4 * (c % 2) + h, NA:NT, :], in_=r[:])
+            nc.scalar.dma_start(out=ov[:, 4 * (c % 2) + h, NA:NT, :], in_=r[:])
 
         def tables_t_turn(rep):
             tt = psx.tile([P, NT - NA, P], F32, name="xt")
@@ -389,16 +394,16 @@ def tile_retnet_pa_kernel(tc, x, wq, wk, out_0, out_1):
             in0=ident[:].rearrange("p (c e) -> p c e", e=2)[:, :, ::-1],
             scalar1=late[:, 0:1], scalar2=0.0, op0=ALU.mult, op1=ALU.add,
         )
-        add_pair(0, 0)
+        add_pair(0, 0, nc.gpsimd, WHOLE)
         multiply(0, 4)
         multiply(0, 5)
         multiply(0, 6)
         rotate(0, 3)
-        add_pair(0, 1)
+        add_pair(0, 1, nc.gpsimd, WHOLE)
         multiply(0, 7)
         rotate(0, 4)
         rotate(0, 5)
-        add_pair(0, 2)
+        add_pair(0, 2, nc.gpsimd, WHOLE)
         w_prep(1)
         tables_t_copy(0, tt0)
         tables_t_copy(1, tt1)
@@ -411,10 +416,12 @@ def tile_retnet_pa_kernel(tc, x, wq, wk, out_0, out_1):
                 seq.append(("t", c, h))
             for a in range(NA):
                 seq.append(("a", c, a))
-        for a in range(NA):
+        for a in range(2):
             seq.append(("a", 3, a))
         for h in range(4):
             seq.append(("t", 3, h))
+        for a in range(2, NA):
+            seq.append(("a", 3, a))
 
         def issue(kind, c, i):
             if kind == "t":
@@ -425,7 +432,7 @@ def tile_retnet_pa_kernel(tc, x, wq, wk, out_0, out_1):
         for j in range(AHEAD):
             issue(*seq[j])
         rotate(0, 7)
-        add_pair(0, 3)
+        add_pair(0, 3, nc.gpsimd, WHOLE)
         w_prep(2)
         quantised = {0, 1}
         for j in range(len(seq)):
@@ -441,8 +448,10 @@ def tile_retnet_pa_kernel(tc, x, wq, wk, out_0, out_1):
                 turn_add_store(c, i)
             else:
                 rotate(c, i)
-                if i % 2 == 1:
-                    add_pair(c, i // 2)
+                if j == len(seq) - 1:
+                    add_pair(c, i // 2, nc.vector, HALVES)
+                elif i % 2 == 1:
+                    add_pair(c, i // 2, nc.gpsimd, WHOLE)
             if j == 2:
                 nc.scalar.mul(
                     out=tab_k[:].rearrange("p a r f -> p (a r f)"),

@@ -222,8 +222,8 @@ def tile_retnet_pa_kernel(tc, x, wq, wk, out_0, out_1):
 
         def interleave(cp, key, piece):
             cp(
-                out=wgr[key][:, piece, :].rearrange("p (n j) -> p n j", j=4),
-                in_=wraw[(key, piece)][:].rearrange("p j n -> p n j"),
+                out=wgr[key][:, piece, :].rearrange("p (c i j) -> p c j i", i=4, j=4),
+                in_=wraw[(key, piece)][:].rearrange("p j (c i) -> p c j i", i=4),
             )
 
         def w_quantise_piece(key, i):

@@ -73,6 +73,11 @@ def tile_retnet_pa_kernel(tc, x, wq, wk, out_0, out_1):
             load_w(c, 0)
             load_w(c, 1)
 
+        def warm_up(n):
+            wp = psa.tile([P, NC], F32, name="acc")
+            for i in range(n):
+                nc.tensor.matmul(out=wp[:, 0:P], lhsT=ident[:], rhs=ident[:], start=True, stop=True)
+
         ones = const.tile([P, 1], F32, name="ones")
         nc.vector.memset(ones[:], 1.0)
         junk = const.tile([P, 1], F32, name="junk")
@@ -353,8 +358,10 @@ def tile_retnet_pa_kernel(tc, x, wq, wk, out_0, out_1):
         signed_phases(0, 2)
         tables(0, 2)
         phases(2, NT)
+        warm_up(3)
         x_turn(0, 0)
         x_copy(0, 0)
+        warm_up(5)
         new_stage(0)
         interleave(nc.scalar.copy, 0, 0)
         x_quantise(0)
@@ -363,6 +370,7 @@ def tile_retnet_pa_kernel(tc, x, wq, wk, out_0, out_1):
         w_quantise_piece(0, 0)
         x_turn(1, 0)
         x_copy(1, 0)
+        warm_up(1)
         for t in range(2):
             x_turn(2, t)
             x_copy(2, t)
@@ -411,17 +419,19 @@ def tile_retnet_pa_kernel(tc, x, wq, wk, out_0, out_1):
         w_quantise(1)
 
         seq = []
+        quantise_before = {}
         for c in (1, 2):
-            for h in range(4):
-                seq.append(("t", c, h))
-            for a in range(NA):
-                seq.append(("a", c, a))
-        for a in range(2):
-            seq.append(("a", 3, a))
-        for h in range(4):
-            seq.append(("t", 3, h))
-        for a in range(2, NA):
-            seq.append(("a", 3, a))
+            for i in range(NA):
+                seq.append(("t", c, i))
+                seq.append(("a", c, i))
+            quantise_before[len(seq) - 1] = c + 1
+        for i in range(2):
+            seq.append(("t", 3, i))
+            seq.append(("a", 3, i))
+        for i in range(2, NA):
+            seq.append(("t", 3, i))
+        for i in range(2, NA):
+            seq.append(("a", 3, i))
 
         def issue(kind, c, i):
             if kind == "t":
@@ -429,19 +439,27 @@ def tile_retnet_pa_kernel(tc, x, wq, wk, out_0, out_1):
             else:
                 multiply(c, i)
 
-        for j in range(AHEAD):
-            issue(*seq[j])
+        quantised = {0, 1}
+        issued = [0]
+
+        def issue_ahead(j):
+            while (
+                issued[0] < len(seq)
+                and issued[0] <= j + AHEAD
+                and seq[issued[0]][1] in quantised
+            ):
+                issue(*seq[issued[0]])
+                issued[0] = issued[0] + 1
+
+        issue_ahead(-1)
         rotate(0, 7)
         add_pair(0, 3, nc.gpsimd, WHOLE)
         w_prep(2)
-        quantised = {0, 1}
         for j in range(len(seq)):
-            if j + AHEAD < len(seq):
-                kind, c, i = seq[j + AHEAD]
-                if c not in quantised:
-                    w_quantise(c)
-                    quantised.add(c)
-                issue(kind, c, i)
+            if j in quantise_before:
+                w_quantise(quantise_before[j])
+                quantised.add(quantise_before[j])
+            issue_ahead(j)
             kind, c, i = seq[j]
             if kind == "t":
                 rotate_t(c, i)
@@ -458,5 +476,5 @@ def tile_retnet_pa_kernel(tc, x, wq, wk, out_0, out_1):
                     in_=tab_q[:, 0:NA].rearrange("p a r f -> p (a r f)"),
                     mul=kappa,
                 )
-            if j == 3:
+            if j == 4:
                 w_prep(3)

@@ -104,13 +104,12 @@ def tile_retnet_pa_kernel(tc, x, wq, wk, out_0, out_1):
         nc.vector.tensor_scalar_mul(out=halfpi[:], in0=ones[:], scalar1=PI / 2.0)
 
         sgn = const.tile([P, 2], F32, name="sgn")
-        nc.vector.memset(sgn[:, 0:1], -1.0)
-        nc.vector.memset(sgn[:, 1:2], 1.0)
+        nc.vector.memset(sgn[:, 0:1], 1.0)
+        nc.vector.memset(sgn[:, 1:2], -1.0)
 
         ph = const.tile([P, NT, NF], F32, name="ph")
         ki = const.tile([P, NT, NF], I32, name="ki")
         fr = const.tile([P, NT, NF], F32, name="fr")
-        gneg = const.tile([P, NT, NF], F32, name="gneg")
         gabs = const.tile([P, NT, NF], F32, name="gabs")
         gpm = const.tile([P, NT, KD], F32, name="gpm")
         tab_q = const.tile([P, NT, 2, KD], F32, name="tab_q")
@@ -134,11 +133,7 @@ def tile_retnet_pa_kernel(tc, x, wq, wk, out_0, out_1):
                 out=flat(fr), in0=flat(ki), scalar=-1.0, in1=flat(ph), op0=ALU.mult, op1=ALU.add
             )
             nc.vector.scalar_tensor_tensor(
-                out=flat(gneg), in0=flat(fr), scalar=0.5, in1=flat(fr),
-                op0=ALU.is_gt, op1=ALU.subtract,
-            )
-            nc.vector.scalar_tensor_tensor(
-                out=flat(gabs), in0=flat(gneg), scalar=-1.0, in1=flat(gneg),
+                out=flat(gabs), in0=flat(fr), scalar=-1.0, in1=flat(fr),
                 op0=ALU.mult, op1=ALU.max,
             )
 
@@ -146,7 +141,7 @@ def tile_retnet_pa_kernel(tc, x, wq, wk, out_0, out_1):
             n = hi - lo
             nc.vector.tensor_tensor(
                 out=gpm[:, lo:hi, :].rearrange("p a (c e) -> p a c e", e=2),
-                in0=gneg[:, lo:hi, :].unsqueeze(3).to_broadcast([P, n, NF, 2]),
+                in0=fr[:, lo:hi, :].unsqueeze(3).to_broadcast([P, n, NF, 2]),
                 in1=sgn[:].unsqueeze(1).unsqueeze(1).to_broadcast([P, n, NF, 2]),
                 op=ALU.mult,
             )

@@ -82,9 +82,9 @@ def tile_retnet_pa_kernel(tc, x, wq, wk, out_0, out_1):
         nc.vector.memset(ones[:], 1.0)
         junk = const.tile([P, 1], F32, name="junk")
         nc.scalar.activation(out=junk[:], in_=ones[:], func=ACT.Sin)
-        idx = const.tile([P, NT, NF], F32, name="idx")
+        idx = const.tile([P, NT], F32, name="idx")
         nc.gpsimd.iota(
-            idx[:], pattern=[[1, NT], [0, NF]], base=0, channel_multiplier=NT,
+            idx[:], pattern=[[1, NT]], base=0, channel_multiplier=NT,
             allow_small_or_imprecise_dtypes=True,
         )
         ident = const.tile([P, P], F32, name="ident")
@@ -118,24 +118,28 @@ def tile_retnet_pa_kernel(tc, x, wq, wk, out_0, out_1):
         perm = const.tile([P, P], F32, name="perm")
         late = const.tile([P, 1], F32, name="late")
 
-        def phases(lo, hi):
-            n = hi - lo
-            nc.vector.tensor_tensor(
-                out=ph[:, lo:hi, :], in0=idx[:, lo:hi, :],
-                in1=nu[:].unsqueeze(1).to_broadcast([P, n, NF]), op=ALU.mult,
-            )
-
-            def flat(t):
+        def phases(groups):
+            def flat(t, lo, hi):
                 return t[:, lo:hi, :].rearrange("p a c -> p (a c)")
 
-            nc.vector.tensor_copy(out=flat(ki), in_=flat(ph))
-            nc.vector.scalar_tensor_tensor(
-                out=flat(fr), in0=flat(ki), scalar=-1.0, in1=flat(ph), op0=ALU.mult, op1=ALU.add
-            )
-            nc.vector.scalar_tensor_tensor(
-                out=flat(gabs), in0=flat(fr), scalar=-1.0, in1=flat(fr),
-                op0=ALU.mult, op1=ALU.max,
-            )
+            for lo, hi in groups:
+                nc.vector.tensor_tensor(
+                    out=ph[:, lo:hi, :],
+                    in0=idx[:, lo:hi].unsqueeze(2).to_broadcast([P, hi - lo, NF]),
+                    in1=nu[:].unsqueeze(1).to_broadcast([P, hi - lo, NF]), op=ALU.mult,
+                )
+            for lo, hi in groups:
+                nc.vector.tensor_copy(out=flat(ki, lo, hi), in_=flat(ph, lo, hi))
+            for lo, hi in groups:
+                nc.vector.scalar_tensor_tensor(
+                    out=flat(fr, lo, hi), in0=flat(ki, lo, hi), scalar=-1.0, in1=flat(ph, lo, hi),
+                    op0=ALU.mult, op1=ALU.add,
+                )
+            for lo, hi in groups:
+                nc.vector.scalar_tensor_tensor(
+                    out=flat(gabs, lo, hi), in0=flat(fr, lo, hi), scalar=-1.0, in1=flat(fr, lo, hi),
+                    op0=ALU.mult, op1=ALU.max,
+                )
 
         def signed_phases(lo, hi):
             n = hi - lo
@@ -220,16 +224,24 @@ def tile_retnet_pa_kernel(tc, x, wq, wk, out_0, out_1):
             wc[key] = keep.tile([P, 2, NC], U32, name="wc%d" % key, align_bytes=64)
             ws[key] = keep.tile([P, 2, NC], U8, name="ws%d" % key, align_bytes=64)
 
-        def interleave(cp, key, piece):
-            cp(
-                out=wgr[key][:, piece, :].rearrange("p (c i j) -> p c j i", i=4, j=4),
-                in_=wraw[(key, piece)][:].rearrange("p j (c i) -> p c j i", i=4),
-            )
+        def interleave(cp, key, piece, parts=1):
+            n = NC // parts
+            for k in range(parts):
+                cp(
+                    out=wgr[key][:, piece, 4 * n * k : 4 * n * (k + 1)]
+                    .rearrange("p (c i j) -> p c j i", i=4, j=4),
+                    in_=wraw[(key, piece)][:, :, n * k : n * (k + 1)]
+                    .rearrange("p j (c i) -> p c j i", i=4),
+                )
 
-        def w_quantise_piece(key, i):
-            nc.vector.quantize_mx(
-                out=wc[key][:, i, :].bitcast(E5X4), scales=ws[key][:, i, :], in_=wgr[key][:, i, :]
-            )
+        def w_quantise_piece(key, i, parts=1):
+            n = NC // parts
+            for k in range(parts):
+                cols = slice(n * k, n * (k + 1))
+                nc.vector.quantize_mx(
+                    out=wc[key][:, i, cols].bitcast(E5X4), scales=ws[key][:, i, cols],
+                    in_=wgr[key][:, i, 4 * n * k : 4 * n * (k + 1)],
+                )
 
         def w_quantise(key):
             nc.vector.quantize_mx(
@@ -260,19 +272,33 @@ def tile_retnet_pa_kernel(tc, x, wq, wk, out_0, out_1):
                 )
             accs[(c, a)] = acc
 
-        def rotate(c, a):
+        def rotate(c, a, parts=WHOLE):
             tab = tab_q if c < 2 else tab_k
             aq = a % 2
             if aq == 0:
                 pair[(c, a // 2)] = prod.tile([P, 2, 4, 2, KD], F32, name="m")
             m = pair[(c, a // 2)]
-            nc.vector.tensor_tensor(
-                out=m[:, :, :, aq, :],
-                in0=accs[(c, a)][:].rearrange("p (h f) -> p h f", h=4).unsqueeze(1)
-                .to_broadcast([P, 2, 4, KD]),
-                in1=tab[:, a, :, :].unsqueeze(2).to_broadcast([P, 2, 4, KD]),
-                op=ALU.mult,
-            )
+            for h0, h1 in parts:
+                nc.vector.tensor_tensor(
+                    out=m[:, :, h0:h1, aq, :],
+                    in0=accs[(c, a)][:].rearrange("p (h f) -> p h f", h=4)[:, h0:h1].unsqueeze(1)
+                    .to_broadcast([P, 2, h1 - h0, KD]),
+                    in1=tab[:, a, :, :].unsqueeze(2).to_broadcast([P, 2, h1 - h0, KD]),
+                    op=ALU.mult,
+                )
+
+        def add_tile(c, a, eng, parts):
+            ov = oq if c < 2 else ok
+            hb = 4 * (c % 2)
+            m = pair[(c, a // 2)]
+            for h0, h1 in parts:
+                eng.tensor_tensor(
+                    out=m[:, 0, h0:h1, a % 2].rearrange("p h (c e) -> p h c e", e=2),
+                    in0=m[:, 0, h0:h1, a % 2].rearrange("p h (c e) -> p h c e", e=2),
+                    in1=m[:, 1, h0:h1, a % 2].rearrange("p h (c e) -> p h c e", e=2)[:, :, :, ::-1],
+                    op=ALU.add,
+                )
+                nc.sync.dma_start(out=ov[:, hb + h0 : hb + h1, a, :], in_=m[:, 0, h0:h1, a % 2])
 
         def add_pair(c, b, eng, parts):
             ov = oq if c < 2 else ok
@@ -349,10 +375,10 @@ def tile_retnet_pa_kernel(tc, x, wq, wk, out_0, out_1):
         def tables_t_copy(rep, tt):
             nc.scalar.copy(out=tab_t[:, rep, :], in_=tt[:].rearrange("p a r -> p (a r)"))
 
-        phases(0, 2)
+        phases(((0, 2), (2, NT)))
         signed_phases(0, 2)
+        signed_phases(2, NT)
         tables(0, 2)
-        phases(2, NT)
         warm_up(3)
         x_turn(0, 0)
         x_copy(0, 0)
@@ -360,8 +386,8 @@ def tile_retnet_pa_kernel(tc, x, wq, wk, out_0, out_1):
         new_stage(0)
         interleave(nc.scalar.copy, 0, 0)
         x_quantise(0)
-        interleave(nc.vector.tensor_copy, 0, 1)
-        w_quantise_piece(0, 1)
+        interleave(nc.vector.tensor_copy, 0, 1, 2)
+        w_quantise_piece(0, 1, 2)
         w_quantise_piece(0, 0)
         x_turn(1, 0)
         x_copy(1, 0)
@@ -370,10 +396,10 @@ def tile_retnet_pa_kernel(tc, x, wq, wk, out_0, out_1):
             x_turn(2, t)
             x_copy(2, t)
         x_quantise(1)
-        signed_phases(2, NT)
         multiply(0, 0)
         multiply(0, 1)
         tables(2, NA)
+        tables(NA, NT)
         rotate(0, 0)
         x_quantise(2)
         for t in range(2):
@@ -385,7 +411,6 @@ def tile_retnet_pa_kernel(tc, x, wq, wk, out_0, out_1):
         x_turn(4, 1)
         x_copy(4, 1)
         multiply(0, 3)
-        tables(NA, NT)
         tt0 = tables_t_turn(0)
         tt1 = tables_t_turn(1)
         rotate(0, 1)
@@ -460,9 +485,12 @@ def tile_retnet_pa_kernel(tc, x, wq, wk, out_0, out_1):
                 rotate_t(c, i)
                 turn_add_store(c, i)
             else:
-                rotate(c, i)
-                if j == len(seq) - 1:
-                    add_pair(c, i // 2, nc.vector, HALVES)
+                last = j == len(seq) - 1
+                rotate(c, i, HALVES if last else WHOLE)
+                if last:
+                    add_tile(c, i, nc.vector, HALVES)
+                elif j == len(seq) - 2:
+                    add_tile(c, i, nc.gpsimd, WHOLE)
                 elif i % 2 == 1:
                     add_pair(c, i // 2, nc.gpsimd, WHOLE)
             if j == 2:

@@ -20,11 +20,11 @@ NF = KD // 2
 PI = 3.141592653589793
 FLOPS = 2 * S * E * 2 * H * KD
 
-X_GROUPS = ((0, 1), (1, 2), (2, 4), (4, 6), (6, 8))
+TT = 4
+X_GROUPS = ((0, 1), (1, 2), (2, 3), (3, 4), (4, 6), (6, 8))
 WHOLE = ((0, 4),)
 HALVES = ((0, 2), (2, 4))
 AHEAD = 3
-NA = 4
 
 
 def tile_retnet_pa_kernel(tc, x, wq, wk, out_0, out_1):
@@ -41,8 +41,8 @@ def tile_retnet_pa_kernel(tc, x, wq, wk, out_0, out_1):
         keep = ctx.enter_context(tc.tile_pool(name="keep", bufs=1))
         stage = ctx.enter_context(tc.tile_pool(name="stage", bufs=2))
         prod = ctx.enter_context(tc.tile_pool(name="prod", bufs=4))
-        prodt = ctx.enter_context(tc.tile_pool(name="prodt", bufs=4))
-        outt = ctx.enter_context(tc.tile_pool(name="outt", bufs=3))
+        prodt = ctx.enter_context(tc.tile_pool(name="prodt", bufs=6))
+        outt = ctx.enter_context(tc.tile_pool(name="outt", bufs=4))
         psx = ctx.enter_context(tc.psum_pool(name="psx", bufs=3))
         psa = ctx.enter_context(tc.psum_pool(name="psa", bufs=5))
         ctx.enter_context(tc.manual_schedule())
@@ -56,115 +56,142 @@ def tile_retnet_pa_kernel(tc, x, wq, wk, out_0, out_1):
             nc.sync.dma_start(out=t[:], in_=xv[:, lo:hi, :])
             xraw[i] = t
 
-        def load_w(c, g):
-            t = keep.tile([P, 4, NC], BF16, name="wraw%d_%d" % (c, g))
+        def load_w(c, g, n0, n):
+            t = keep.tile([P, 4, n], BF16, name="wraw%d_%d_%d" % (c, g, n0))
             wv = wqv if c < 2 else wkv
-            nc.sync.dma_start(out=t[:], in_=wv[g][:, :, NC * (c % 2) : NC * (c % 2 + 1)])
-            wraw[(c, g)] = t
+            lo = NC * (c % 2) + n0
+            nc.sync.dma_start(out=t[:], in_=wv[g][:, :, lo : lo + n])
+            for k in range(n // P):
+                wraw[(c, g, n0 // P + k)] = t[:, :, P * k : P * (k + 1)]
 
-        load_x(0)
-        load_w(0, 0)
-        load_w(0, 1)
-        load_x(1)
-        load_x(2)
-        load_x(3)
+        for i in range(4):
+            load_x(i)
+        for n0 in (0, 256):
+            for g in range(2):
+                load_w(0, g, n0, 256)
         load_x(4)
+        load_x(5)
         for c in (1, 2, 3):
-            load_w(c, 0)
-            load_w(c, 1)
-
-        def warm_up(n):
-            wp = psa.tile([P, NC], F32, name="acc")
-            for i in range(n):
-                nc.tensor.matmul(out=wp[:, 0:P], lhsT=ident[:], rhs=ident[:], start=True, stop=True)
+            for g in range(2):
+                load_w(c, g, 0, NC)
 
         ones = const.tile([P, 1], F32, name="ones")
         nc.vector.memset(ones[:], 1.0)
         junk = const.tile([P, 1], F32, name="junk")
         nc.scalar.activation(out=junk[:], in_=ones[:], func=ACT.Sin)
+        ident = const.tile([P, P], F32, name="ident")
+        make_identity(nc, ident[:])
         idx = const.tile([P, NT], F32, name="idx")
         nc.gpsimd.iota(
             idx[:], pattern=[[1, NT]], base=0, channel_multiplier=NT,
             allow_small_or_imprecise_dtypes=True,
         )
-        ident = const.tile([P, P], F32, name="ident")
-        make_identity(nc, ident[:])
+        tok = const.tile([P, TT, P], F32, name="tok")
+        nc.gpsimd.iota(
+            tok[:], pattern=[[1, TT], [NT, P]], base=0, channel_multiplier=0,
+            allow_small_or_imprecise_dtypes=True,
+        )
+        perm = const.tile([P, P], F32, name="perm")
+        nc.gpsimd.tensor_scalar(
+            out=perm[:].rearrange("p (c e) -> p c e", e=2),
+            in0=ident[:].rearrange("p (c e) -> p c e", e=2)[:, :, ::-1],
+            scalar1=1.0, scalar2=0.0, op0=ALU.mult, op1=ALU.add,
+        )
         ratio = 10000.0 ** (-1.0 / 63.0)
         nu = const.tile([P, NF], F32, name="nu")
         for j in range(4):
             nc.vector.tensor_scalar_mul(
                 out=nu[:, j : j + 1], in0=ones[:], scalar1=ratio**j / (2.0 * PI)
             )
-        for w in (4, 16):
-            for m in range(1, 4):
-                nc.vector.tensor_scalar_mul(
-                    out=nu[:, w * m : w * (m + 1)], in0=nu[:, 0:w], scalar1=ratio ** (w * m)
-                )
         halfpi = const.tile([P, 1], F32, name="halfpi")
         nc.vector.tensor_scalar_mul(out=halfpi[:], in0=ones[:], scalar1=PI / 2.0)
-
+        for m in range(1, 4):
+            nc.vector.tensor_scalar_mul(
+                out=nu[:, 4 * m : 4 * (m + 1)], in0=nu[:, 0:4], scalar1=ratio ** (4 * m)
+            )
         sgn = const.tile([P, 2], F32, name="sgn")
         nc.vector.memset(sgn[:, 0:1], 1.0)
         nc.vector.memset(sgn[:, 1:2], -1.0)
+        for m in range(1, 4):
+            nc.vector.tensor_scalar_mul(
+                out=nu[:, 16 * m : 16 * (m + 1)], in0=nu[:, 0:16], scalar1=ratio ** (16 * m)
+            )
+        nus = const.tile([P, KD], F32, name="nus")
+        nc.vector.tensor_tensor(
+            out=nus[:].rearrange("p (c e) -> p c e", e=2),
+            in0=nu[:].unsqueeze(2).to_broadcast([P, NF, 2]),
+            in1=sgn[:].unsqueeze(1).to_broadcast([P, NF, 2]),
+            op=ALU.mult,
+        )
+        nut = psx.tile([P, P], F32, name="xt")
+        nc.tensor.transpose(nut[:], nus[:], ident[:])
 
-        ph = const.tile([P, NT, NF], F32, name="ph")
-        ki = const.tile([P, NT, NF], I32, name="ki")
-        fr = const.tile([P, NT, NF], F32, name="fr")
-        gabs = const.tile([P, NT, NF], F32, name="gabs")
-        gpm = const.tile([P, NT, KD], F32, name="gpm")
-        tab_q = const.tile([P, NT, 2, KD], F32, name="tab_q")
-        tab_k = const.tile([P, NA, 2, KD], F32, name="tab_k")
         tab_t = const.tile([P, 2, NC], F32, name="tab_t")
-        perm = const.tile([P, P], F32, name="perm")
+        tab_q = const.tile([P, NT - TT, 2, KD], F32, name="tab_q")
+        tab_k = const.tile([P, NT - TT, 2, KD], F32, name="tab_k")
+        nuf = const.tile([P, 1], F32, name="nuf")
+        pha = const.tile([P, NT - TT, KD], F32, name="pha")
+        kia = const.tile([P, NC], I32, name="kia")
+        kit = const.tile([P, NC], I32, name="kit")
+        fra = const.tile([P, NT - TT, NF, 2], F32, name="fra")
+        frt = const.tile([P, NC], F32, name="frt")
+        aba = const.tile([P, NT - TT, NF], F32, name="aba")
+        abt = const.tile([P, NC], F32, name="abt")
         late = const.tile([P, 1], F32, name="late")
+        held = const.tile([P, 1], F32, name="held")
 
-        def phases(groups):
-            def flat(t, lo, hi):
-                return t[:, lo:hi, :].rearrange("p a c -> p (a c)")
-
-            for lo, hi in groups:
-                nc.vector.tensor_tensor(
-                    out=ph[:, lo:hi, :],
-                    in0=idx[:, lo:hi].unsqueeze(2).to_broadcast([P, hi - lo, NF]),
-                    in1=nu[:].unsqueeze(1).to_broadcast([P, hi - lo, NF]), op=ALU.mult,
-                )
-            for lo, hi in groups:
-                nc.vector.tensor_copy(out=flat(ki, lo, hi), in_=flat(ph, lo, hi))
-            for lo, hi in groups:
-                nc.vector.scalar_tensor_tensor(
-                    out=flat(fr, lo, hi), in0=flat(ki, lo, hi), scalar=-1.0, in1=flat(ph, lo, hi),
-                    op0=ALU.mult, op1=ALU.add,
-                )
-            for lo, hi in groups:
-                nc.vector.scalar_tensor_tensor(
-                    out=flat(gabs, lo, hi), in0=flat(fr, lo, hi), scalar=-1.0, in1=flat(fr, lo, hi),
-                    op0=ALU.mult, op1=ALU.max,
-                )
-
-        def signed_phases(lo, hi):
-            n = hi - lo
+        def phases():
+            tokf = tok[:].rearrange("p a r -> p (a r)")
+            phf = pha[:].rearrange("p a f -> p (a f)")
             nc.vector.tensor_tensor(
-                out=gpm[:, lo:hi, :].rearrange("p a (c e) -> p a c e", e=2),
-                in0=fr[:, lo:hi, :].unsqueeze(3).to_broadcast([P, n, NF, 2]),
-                in1=sgn[:].unsqueeze(1).unsqueeze(1).to_broadcast([P, n, NF, 2]),
-                op=ALU.mult,
+                out=pha[:], in0=idx[:, TT:NT].unsqueeze(2).to_broadcast([P, NT - TT, KD]),
+                in1=nus[:].unsqueeze(1).to_broadcast([P, NT - TT, KD]), op=ALU.mult,
+            )
+            nc.vector.tensor_copy(out=nuf[:], in_=nut[:, 0:1])
+            nc.vector.tensor_copy(out=kia[:], in_=phf)
+            nc.vector.tensor_scalar(
+                out=kit[:], in0=tokf, scalar1=nuf[:, 0:1], scalar2=0.0, op0=ALU.mult, op1=ALU.add
+            )
+            nc.vector.scalar_tensor_tensor(
+                out=fra[:].rearrange("p a c e -> p (a c e)"), in0=kia[:], scalar=-1.0, in1=phf,
+                op0=ALU.mult, op1=ALU.add,
+            )
+            nc.vector.scalar_tensor_tensor(
+                out=frt[:], in0=tokf, scalar=nuf[:, 0:1], in1=kit[:],
+                op0=ALU.mult, op1=ALU.subtract,
+            )
+            nc.vector.scalar_tensor_tensor(
+                out=aba[:], in0=fra[:, :, :, 0], scalar=-1.0, in1=fra[:, :, :, 0],
+                op0=ALU.mult, op1=ALU.max,
+            )
+            nc.vector.scalar_tensor_tensor(
+                out=abt[:], in0=frt[:], scalar=-1.0, in1=frt[:], op0=ALU.mult, op1=ALU.max
             )
 
-        def tables(lo, hi):
-            n = hi - lo
+        def tables_t():
+            nc.scalar.activation(out=tab_t[:, 1, :], in_=frt[:], func=ACT.Sin, scale=2.0 * PI)
             nc.scalar.activation(
-                out=tab_q[:, lo:hi, 0, :].rearrange("p a (c e) -> p a c e", e=2),
-                in_=gabs[:, lo:hi, :].unsqueeze(3).to_broadcast([P, n, NF, 2]),
+                out=tab_t[:, 0, :], in_=abt[:], func=ACT.Sin, scale=-2.0 * PI, bias=halfpi[:, 0:1]
+            )
+
+        def tables_a():
+            nc.scalar.activation(
+                out=tab_q[:, :, 1, :], in_=fra[:].rearrange("p a c e -> p a (c e)"),
+                func=ACT.Sin, scale=2.0 * PI,
+            )
+            nc.scalar.activation(
+                out=tab_q[:, :, 0, :].rearrange("p a (c e) -> p a c e", e=2),
+                in_=aba[:].unsqueeze(3).to_broadcast([P, NT - TT, NF, 2]),
                 func=ACT.Sin, scale=-2.0 * PI, bias=halfpi[:, 0:1],
             )
-            nc.scalar.activation(
-                out=tab_q[:, lo:hi, 1, :], in_=gpm[:, lo:hi, :], func=ACT.Sin, scale=2.0 * PI
-            )
 
-        xg = {}
         xt = {}
         xc = {}
         xs = {}
+        xg_t = keep.tile([P, 2, TT, NC], BF16, name="xg_t", align_bytes=64)
+        xc_t = keep.tile([P, 2, TT, P], U32, name="xc_t", align_bytes=64)
+        xs_t = keep.tile([P, 2, TT, P], U8, name="xs_t", align_bytes=64)
+        xg = {}
 
         def x_turn(i, t):
             words = xraw[i][:, t, :].bitcast(F32)
@@ -175,14 +202,10 @@ def tile_retnet_pa_kernel(tc, x, wq, wk, out_0, out_1):
                         xt[(i, t)][:, g, u, :], words[:, 256 * g + u : 256 * (g + 1) : 2], ident[:]
                     )
 
-        xg_b = keep.tile([P, 2, NT - NA, NC], BF16, name="xg_b", align_bytes=64)
-        xc_b = keep.tile([P, 2, NT - NA, P], U32, name="xc_b", align_bytes=64)
-        xs_b = keep.tile([P, 2, NT - NA, P], U8, name="xs_b", align_bytes=64)
-
-        def x_copy(i, t):
+        def x_copy(cp, i, t):
             lo, hi = X_GROUPS[i]
-            if lo >= NA:
-                dst = xg_b[:, :, lo + t - NA, :].bitcast(F32).rearrange("p g (r u) -> p g r u", u=2)
+            if lo < TT:
+                dst = xg_t[:, :, lo + t, :].bitcast(F32).rearrange("p g (r u) -> p g r u", u=2)
             else:
                 if t == 0:
                     xg[i] = keep.tile([P, (hi - lo) * 1024], BF16, name="xg%d" % i, align_bytes=64)
@@ -191,7 +214,13 @@ def tile_retnet_pa_kernel(tc, x, wq, wk, out_0, out_1):
                     .bitcast(F32)
                     .rearrange("p (g r u) -> p g r u", g=2, u=2)
                 )
-            nc.scalar.copy(out=dst, in_=xt[(i, t)][:].rearrange("p g u r -> p g r u"))
+            cp(out=dst, in_=xt[(i, t)][:].rearrange("p g u r -> p g r u"))
+
+        def x_quantise_t(a):
+            for g in range(2):
+                nc.vector.quantize_mx(
+                    out=xc_t[:, g, a, :].bitcast(E5X4), scales=xs_t[:, g, a, :], in_=xg_t[:, g, a, :]
+                )
 
         def x_quantise(i):
             lo, hi = X_GROUPS[i]
@@ -204,17 +233,6 @@ def tile_retnet_pa_kernel(tc, x, wq, wk, out_0, out_1):
                     xc[(lo + t, g)] = codes[:, 256 * t + P * g : 256 * t + P * (g + 1)]
                     xs[(lo + t, g)] = scales[:, 256 * t + P * g : 256 * t + P * (g + 1)]
 
-        def x_quantise_b():
-            nc.vector.quantize_mx(
-                out=xc_b[:].rearrange("p g a r -> p (g a r)").bitcast(E5X4),
-                scales=xs_b[:].rearrange("p g a r -> p (g a r)"),
-                in_=xg_b[:].rearrange("p g a n -> p (g a n)"),
-            )
-            for a in range(NA, NT):
-                for g in range(2):
-                    xc[(a, g)] = xc_b[:, g, a - NA, :]
-                    xs[(a, g)] = xs_b[:, g, a - NA, :]
-
         wgr = {}
         wc = {}
         ws = {}
@@ -224,39 +242,31 @@ def tile_retnet_pa_kernel(tc, x, wq, wk, out_0, out_1):
             wc[key] = keep.tile([P, 2, NC], U32, name="wc%d" % key, align_bytes=64)
             ws[key] = keep.tile([P, 2, NC], U8, name="ws%d" % key, align_bytes=64)
 
-        def interleave(cp, key, piece, parts=1):
-            n = NC // parts
-            for k in range(parts):
-                cp(
-                    out=wgr[key][:, piece, 4 * n * k : 4 * n * (k + 1)]
-                    .rearrange("p (c i j) -> p c j i", i=4, j=4),
-                    in_=wraw[(key, piece)][:, :, n * k : n * (k + 1)]
-                    .rearrange("p j (c i) -> p c j i", i=4),
-                )
-
-        def w_quantise_piece(key, i, parts=1):
-            n = NC // parts
-            for k in range(parts):
-                cols = slice(n * k, n * (k + 1))
-                nc.vector.quantize_mx(
-                    out=wc[key][:, i, cols].bitcast(E5X4), scales=ws[key][:, i, cols],
-                    in_=wgr[key][:, i, 4 * n * k : 4 * n * (k + 1)],
-                )
-
-        def w_quantise(key):
-            nc.vector.quantize_mx(
-                out=wc[key][:].rearrange("p g n -> p (g n)").bitcast(E5X4),
-                scales=ws[key][:].rearrange("p g n -> p (g n)"),
-                in_=wgr[key][:].rearrange("p g n -> p (g n)"),
+        def interleave(cp, c, g, h):
+            cp(
+                out=wgr[c][:, g, NC * h : NC * (h + 1)].rearrange("p (c i j) -> p c j i", i=4, j=4),
+                in_=wraw[(c, g, h)].rearrange("p j (c i) -> p c j i", i=4),
             )
 
-        def w_prep(c):
-            new_stage(c)
+        def w_quantise_head(c, h):
             for g in range(2):
-                interleave(nc.scalar.copy, c, g)
+                nc.vector.quantize_mx(
+                    out=wc[c][:, g, P * h : P * (h + 1)].bitcast(E5X4),
+                    scales=ws[c][:, g, P * h : P * (h + 1)],
+                    in_=wgr[c][:, g, NC * h : NC * (h + 1)],
+                )
+
+        def w_quantise(c, b):
+            for g in range(2):
+                nc.vector.quantize_mx(
+                    out=wc[c][:, g, 2 * P * b : 2 * P * (b + 1)].bitcast(E5X4),
+                    scales=ws[c][:, g, 2 * P * b : 2 * P * (b + 1)],
+                    in_=wgr[c][:, g, 2 * NC * b : 2 * NC * (b + 1)],
+                )
 
         accs = {}
         pair = {}
+        mts = {}
 
         def multiply(c, a):
             acc = psa.tile([P, NC], F32, name="acc")
@@ -270,7 +280,7 @@ def tile_retnet_pa_kernel(tc, x, wq, wk, out_0, out_1):
                     start=(g == 0),
                     stop=(g == 1),
                 )
-            accs[(c, a)] = acc
+            accs[("a", c, a)] = acc
 
         def rotate(c, a, parts=WHOLE):
             tab = tab_q if c < 2 else tab_k
@@ -281,9 +291,9 @@ def tile_retnet_pa_kernel(tc, x, wq, wk, out_0, out_1):
             for h0, h1 in parts:
                 nc.vector.tensor_tensor(
                     out=m[:, :, h0:h1, aq, :],
-                    in0=accs[(c, a)][:].rearrange("p (h f) -> p h f", h=4)[:, h0:h1].unsqueeze(1)
+                    in0=accs[("a", c, a)][:].rearrange("p (h f) -> p h f", h=4)[:, h0:h1].unsqueeze(1)
                     .to_broadcast([P, 2, h1 - h0, KD]),
-                    in1=tab[:, a, :, :].unsqueeze(2).to_broadcast([P, 2, h1 - h0, KD]),
+                    in1=tab[:, a - TT, :, :].unsqueeze(2).to_broadcast([P, 2, h1 - h0, KD]),
                     op=ALU.mult,
                 )
 
@@ -315,8 +325,6 @@ def tile_retnet_pa_kernel(tc, x, wq, wk, out_0, out_1):
                     out=ov[:, hb + h0 : hb + h1, 2 * b : 2 * b + 2, :], in_=m[:, 0, h0:h1]
                 )
 
-        mts = {}
-
         def multiply_t(c, h):
             acc = psa.tile([P, NC], F32, name="acc")
             for g in range(2):
@@ -324,27 +332,35 @@ def tile_retnet_pa_kernel(tc, x, wq, wk, out_0, out_1):
                     out=acc[:],
                     lhsT=wc[c][:, g, P * h : P * (h + 1)].bitcast(E5X4),
                     lhsT_scale=ws[c][:, g, P * h : P * (h + 1)],
-                    rhs=xc_b[:, g].rearrange("p a r -> p (a r)").bitcast(E5X4),
-                    rhs_scale=xs_b[:, g].rearrange("p a r -> p (a r)"),
+                    rhs=xc_t[:, g].rearrange("p a r -> p (a r)").bitcast(E5X4),
+                    rhs_scale=xs_t[:, g].rearrange("p a r -> p (a r)"),
                     start=(g == 0),
                     stop=(g == 1),
                 )
-            accs[(c, "t", h)] = acc
+            accs[("t", c, h)] = acc
 
         def rotate_t(c, h):
             mt = prodt.tile([P, 2, NC], F32, name="mt")
             nc.vector.tensor_tensor(
                 out=mt[:],
-                in0=accs[(c, "t", h)][:].unsqueeze(1).to_broadcast([P, 2, NC]),
+                in0=accs[("t", c, h)][:].unsqueeze(1).to_broadcast([P, 2, NC]),
                 in1=tab_t[:],
                 op=ALU.mult,
             )
             mts[(c, h)] = mt
 
-        def turn_add_store(c, h):
+        def hold_gpsimd():
+            nc.vector.memset(late[:], 1.0)
+            nc.gpsimd.tensor_scalar(
+                out=held[:], in0=late[:], scalar1=1.0, scalar2=0.0, op0=ALU.mult, op1=ALU.add
+            )
+
+        outs = {}
+
+        def turn_add(c, h):
             mt = mts[(c, h)]
-            o = psx.tile([P, NT - NA, P], F32, name="xt")
-            for t in range(NT - NA):
+            o = psx.tile([P, TT, P], F32, name="xt")
+            for t in range(TT):
                 nc.tensor.matmul(
                     out=o[:, t, :], lhsT=mt[:, 0, P * t : P * (t + 1)], rhs=ident[:],
                     start=True, stop=False, is_transpose=True,
@@ -353,7 +369,11 @@ def tile_retnet_pa_kernel(tc, x, wq, wk, out_0, out_1):
                     out=o[:, t, :], lhsT=mt[:, 1, P * t : P * (t + 1)], rhs=perm[:],
                     start=False, stop=True, is_transpose=True,
                 )
-            r = outt.tile([P, NT - NA, KD], F32, name="r")
+            outs[(c, h)] = o
+
+        def store_t(c, h):
+            o = outs[(c, h)]
+            r = outt.tile([P, TT, KD], F32, name="r")
             if c < 2:
                 nc.scalar.copy(
                     out=r[:].rearrange("p a f -> p (a f)"), in_=o[:].rearrange("p a f -> p (a f)")
@@ -364,126 +384,125 @@ def tile_retnet_pa_kernel(tc, x, wq, wk, out_0, out_1):
                     mul=kappa,
                 )
             ov = oq if c < 2 else ok
-            nc.scalar.dma_start(out=ov[:, 4 * (c % 2) + h, NA:NT, :], in_=r[:])
+            nc.scalar.dma_start(out=ov[:, 4 * (c % 2) + h, 0:TT, :], in_=r[:])
 
-        def tables_t_turn(rep):
-            tt = psx.tile([P, NT - NA, P], F32, name="xt")
-            for t in range(NT - NA):
-                nc.tensor.transpose(tt[:, t, :], tab_q[:, NA + t, rep, :], ident[:])
-            return tt
-
-        def tables_t_copy(rep, tt):
-            nc.scalar.copy(out=tab_t[:, rep, :], in_=tt[:].rearrange("p a r -> p (a r)"))
-
-        phases(((0, 2), (2, NT)))
-        signed_phases(0, 2)
-        signed_phases(2, NT)
-        tables(0, 2)
-        warm_up(3)
-        x_turn(0, 0)
-        x_copy(0, 0)
-        warm_up(5)
+        sc, ve = nc.scalar.copy, nc.vector.tensor_copy
+        phases()
+        for a in range(TT):
+            x_turn(a, 0)
+            x_copy(sc, a, 0)
+        tables_t()
+        for a in range(TT):
+            x_quantise_t(a)
         new_stage(0)
-        interleave(nc.scalar.copy, 0, 0)
-        x_quantise(0)
-        interleave(nc.vector.tensor_copy, 0, 1, 2)
-        w_quantise_piece(0, 1, 2)
-        w_quantise_piece(0, 0)
-        x_turn(1, 0)
-        x_copy(1, 0)
-        warm_up(1)
+        for g in range(2):
+            interleave(ve, 0, g, 0)
+        interleave(sc, 0, 1, 1)
+        w_quantise_head(0, 0)
+        interleave(ve, 0, 0, 1)
+        multiply_t(0, 0)
+        w_quantise_head(0, 1)
+        multiply_t(0, 1)
         for t in range(2):
-            x_turn(2, t)
-            x_copy(2, t)
-        x_quantise(1)
-        multiply(0, 0)
-        multiply(0, 1)
-        tables(2, NA)
-        tables(NA, NT)
-        rotate(0, 0)
-        x_quantise(2)
+            x_turn(4, t)
+        for h in (2, 3):
+            for g in range(2):
+                interleave(sc, 0, g, h)
         for t in range(2):
-            x_turn(3, t)
-            x_copy(3, t)
-        x_turn(4, 0)
-        x_copy(4, 0)
-        multiply(0, 2)
-        x_turn(4, 1)
-        x_copy(4, 1)
-        multiply(0, 3)
-        tt0 = tables_t_turn(0)
-        tt1 = tables_t_turn(1)
-        rotate(0, 1)
-        rotate(0, 2)
-        x_quantise_b()
-        nc.vector.memset(late[:], 1.0)
-        nc.gpsimd.tensor_scalar(
-            out=perm[:].rearrange("p (c e) -> p c e", e=2),
-            in0=ident[:].rearrange("p (c e) -> p c e", e=2)[:, :, ::-1],
-            scalar1=late[:, 0:1], scalar2=0.0, op0=ALU.mult, op1=ALU.add,
-        )
-        add_pair(0, 0, nc.gpsimd, WHOLE)
+            x_copy(sc, 4, t)
+        rotate_t(0, 0)
+        w_quantise_head(0, 2)
+        multiply_t(0, 2)
+        rotate_t(0, 1)
+        for t in range(2):
+            x_turn(5, t)
+        w_quantise_head(0, 3)
+        multiply_t(0, 3)
+        tables_a()
+        for t in range(2):
+            x_copy(sc, 5, t)
+        rotate_t(0, 2)
+        x_quantise(4)
         multiply(0, 4)
+        rotate_t(0, 3)
         multiply(0, 5)
-        multiply(0, 6)
-        rotate(0, 3)
-        add_pair(0, 1, nc.gpsimd, WHOLE)
-        multiply(0, 7)
         rotate(0, 4)
+        x_quantise(5)
+        multiply(0, 6)
+        multiply(0, 7)
+        new_stage(1)
+        for h in range(4):
+            for g in range(2):
+                interleave(sc, 1, g, h)
         rotate(0, 5)
+        w_quantise(1, 0)
+        hold_gpsimd()
         add_pair(0, 2, nc.gpsimd, WHOLE)
-        w_prep(1)
-        tables_t_copy(0, tt0)
-        tables_t_copy(1, tt1)
+        multiply_t(1, 0)
+        multiply_t(1, 1)
         rotate(0, 6)
-        w_quantise(1)
+        for h in range(3):
+            turn_add(0, h)
+            store_t(0, h)
+        rotate(0, 7)
+        new_stage(2)
 
         seq = []
-        quantise_before = {}
+        quantise_before = {1: (1, 1)}
         for c in (1, 2):
-            for i in range(NA):
-                seq.append(("t", c, i))
-                seq.append(("a", c, i))
-            quantise_before[len(seq) - 1] = c + 1
+            seq = seq + [("t", c, 0), ("t", c, 1), ("a", c, TT), ("a", c, TT + 1)]
+            seq = seq + [("t", c, 2), ("a", c, TT + 2), ("t", c, 3), ("a", c, TT + 3)]
+            quantise_before[len(seq) - 5] = (c + 1, 0)
+            quantise_before[len(seq) - 1] = (c + 1, 1)
         for i in range(2):
             seq.append(("t", 3, i))
-            seq.append(("a", 3, i))
-        for i in range(2, NA):
+            seq.append(("a", 3, TT + i))
+        for i in range(2, 4):
             seq.append(("t", 3, i))
-        for i in range(2, NA):
-            seq.append(("a", 3, i))
+        for i in range(2, 4):
+            seq.append(("a", 3, TT + i))
 
-        def issue(kind, c, i):
+        parts_at = {}
+        for k in range(16):
+            parts_at.setdefault(k // 2 if k < 8 else k // 2 + 2, []).append((2 + k // 8, k % 2, k // 2 % 4))
+        done = {-1: [(0, 3)]}
+        quantised = {(1, 0)}
+        issued = [2]
+
+        def ready(kind, c, i):
             if kind == "t":
-                multiply_t(c, i)
-            else:
-                multiply(c, i)
-
-        quantised = {0, 1}
-        issued = [0]
+                return (c, i // 2) in quantised
+            return (c, 0) in quantised and (c, 1) in quantised
 
         def issue_ahead(j):
-            while (
-                issued[0] < len(seq)
-                and issued[0] <= j + AHEAD
-                and seq[issued[0]][1] in quantised
-            ):
-                issue(*seq[issued[0]])
+            while issued[0] < len(seq) and issued[0] <= j + AHEAD and ready(*seq[issued[0]]):
+                kind, c, i = seq[issued[0]]
+                if kind == "t":
+                    multiply_t(c, i)
+                else:
+                    multiply(c, i)
                 issued[0] = issued[0] + 1
 
-        issue_ahead(-1)
-        rotate(0, 7)
-        add_pair(0, 3, nc.gpsimd, WHOLE)
-        w_prep(2)
         for j in range(len(seq)):
             if j in quantise_before:
-                w_quantise(quantise_before[j])
+                w_quantise(*quantise_before[j])
                 quantised.add(quantise_before[j])
+                if j == 1:
+                    hold_gpsimd()
+                    add_pair(0, 3, nc.gpsimd, WHOLE)
             issue_ahead(j)
             kind, c, i = seq[j]
+            for c2, g, h in parts_at.get(j, ()):
+                if g == 0 and h == 0 and c2 == 3:
+                    new_stage(3)
+                interleave(sc, c2, g, h)
+            for b in done.get(j - 2, ()):
+                store_t(*b)
+            for b in done.get(j - 1, ()):
+                turn_add(*b)
             if kind == "t":
                 rotate_t(c, i)
-                turn_add_store(c, i)
+                done.setdefault(j, []).append((c, i))
             else:
                 last = j == len(seq) - 1
                 rotate(c, i, HALVES if last else WHOLE)
@@ -493,11 +512,9 @@ def tile_retnet_pa_kernel(tc, x, wq, wk, out_0, out_1):
                     add_tile(c, i, nc.gpsimd, WHOLE)
                 elif i % 2 == 1:
                     add_pair(c, i // 2, nc.gpsimd, WHOLE)
-            if j == 2:
+            if j == 4:
                 nc.scalar.mul(
                     out=tab_k[:].rearrange("p a r f -> p (a r f)"),
-                    in_=tab_q[:, 0:NA].rearrange("p a r f -> p (a r f)"),
+                    in_=tab_q[:].rearrange("p a r f -> p (a r f)"),
                     mul=kappa,
                 )
-            if j == 4:
-                w_prep(3)

@@ -24,6 +24,7 @@ TT = 4
 X_GROUPS = ((0, 1), (1, 2), (2, 3), (3, 4), (4, 6), (6, 8))
 WHOLE = ((0, 4),)
 HALVES = ((0, 2), (2, 4))
+HELPED = (("t", 1, 3), ("t", 2, 1), ("t", 2, 3), ("t", 3, 1))
 AHEAD = 3
 
 
@@ -43,6 +44,7 @@ def tile_retnet_pa_kernel(tc, x, wq, wk, out_0, out_1):
         prod = ctx.enter_context(tc.tile_pool(name="prod", bufs=4))
         prodt = ctx.enter_context(tc.tile_pool(name="prodt", bufs=6))
         outt = ctx.enter_context(tc.tile_pool(name="outt", bufs=4))
+        helped = ctx.enter_context(tc.tile_pool(name="helped", bufs=2))
         psx = ctx.enter_context(tc.psum_pool(name="psx", bufs=3))
         psa = ctx.enter_context(tc.psum_pool(name="psa", bufs=5))
         ctx.enter_context(tc.manual_schedule())
@@ -125,6 +127,11 @@ def tile_retnet_pa_kernel(tc, x, wq, wk, out_0, out_1):
         )
         nut = psx.tile([P, P], F32, name="xt")
         nc.tensor.transpose(nut[:], nus[:], ident[:])
+
+        def warm_up(n):
+            wp = psa.tile([P, NC], F32, name="acc")
+            for i in range(n):
+                nc.tensor.matmul(out=wp[:, 0:P], lhsT=ident[:], rhs=ident[:], start=True, stop=True)
 
         tab_t = const.tile([P, 2, NC], F32, name="tab_t")
         tab_q = const.tile([P, NT - TT, 2, KD], F32, name="tab_q")
@@ -268,6 +275,19 @@ def tile_retnet_pa_kernel(tc, x, wq, wk, out_0, out_1):
         pair = {}
         mts = {}
 
+        def assist(c, h):
+            q = helped.tile([P, NC], F32, name="q")
+            mts[(c, h)] = prodt.tile([P, 2, NC], F32, name="mt")
+            nc.scalar.copy(out=q[:], in_=accs[("t", c, h)][:])
+            nc.gpsimd.tensor_tensor(
+                out=mts[(c, h)][:, 1, :], in0=q[:], in1=tab_t[:, 1, :], op=ALU.mult
+            )
+
+        def rotate_h(c, h):
+            nc.vector.tensor_tensor(
+                out=mts[(c, h)][:, 0, :], in0=accs[("t", c, h)][:], in1=tab_t[:, 0, :], op=ALU.mult
+            )
+
         def multiply(c, a):
             acc = psa.tile([P, NC], F32, name="acc")
             for g in range(2):
@@ -390,7 +410,8 @@ def tile_retnet_pa_kernel(tc, x, wq, wk, out_0, out_1):
         phases()
         for a in range(TT):
             x_turn(a, 0)
-            x_copy(sc, a, 0)
+            x_copy(ve if a == 2 else sc, a, 0)
+        warm_up(4)
         tables_t()
         for a in range(TT):
             x_quantise_t(a)
@@ -426,6 +447,7 @@ def tile_retnet_pa_kernel(tc, x, wq, wk, out_0, out_1):
         multiply(0, 4)
         rotate_t(0, 3)
         multiply(0, 5)
+        turn_add(0, 0)
         rotate(0, 4)
         x_quantise(5)
         multiply(0, 6)
@@ -434,39 +456,45 @@ def tile_retnet_pa_kernel(tc, x, wq, wk, out_0, out_1):
         for h in range(4):
             for g in range(2):
                 interleave(sc, 1, g, h)
+        turn_add(0, 1)
+        for h in range(2):
+            store_t(0, h)
+        nc.gpsimd.tensor_scalar(
+            out=tab_k[:].rearrange("p a r f -> p (a r f)"),
+            in0=tab_q[:].rearrange("p a r f -> p (a r f)"),
+            scalar1=kappa, scalar2=0.0, op0=ALU.mult, op1=ALU.add,
+        )
         rotate(0, 5)
         w_quantise(1, 0)
         hold_gpsimd()
         add_pair(0, 2, nc.gpsimd, WHOLE)
         multiply_t(1, 0)
         multiply_t(1, 1)
+        turn_add(0, 2)
+        store_t(0, 2)
         rotate(0, 6)
-        for h in range(3):
-            turn_add(0, h)
-            store_t(0, h)
         rotate(0, 7)
+        w_quantise(1, 1)
+        hold_gpsimd()
+        add_pair(0, 3, nc.gpsimd, WHOLE)
         new_stage(2)
 
         seq = []
-        quantise_before = {1: (1, 1)}
-        for c in (1, 2):
-            seq = seq + [("t", c, 0), ("t", c, 1), ("a", c, TT), ("a", c, TT + 1)]
-            seq = seq + [("t", c, 2), ("a", c, TT + 2), ("t", c, 3), ("a", c, TT + 3)]
-            quantise_before[len(seq) - 5] = (c + 1, 0)
-            quantise_before[len(seq) - 1] = (c + 1, 1)
-        for i in range(2):
-            seq.append(("t", 3, i))
-            seq.append(("a", 3, TT + i))
-        for i in range(2, 4):
-            seq.append(("t", 3, i))
-        for i in range(2, 4):
-            seq.append(("a", 3, TT + i))
+        quantise_after = {}
+        for c in (1, 2, 3):
+            for b in range(2):
+                seq = seq + [("t", c, 2 * b), ("t", c, 2 * b + 1)]
+                seq = seq + [("a", c, TT + 2 * b), ("a", c, TT + 2 * b + 1)]
+                if c < 3:
+                    quantise_after[len(seq) - 1] = (c + 1, b)
 
         parts_at = {}
-        for k in range(16):
-            parts_at.setdefault(k // 2 if k < 8 else k // 2 + 2, []).append((2 + k // 8, k % 2, k // 2 % 4))
+        for k in range(8):
+            g, h = k % 2, k // 2
+            parts_at.setdefault(k // 2 if h < 2 else k - 1, []).append((2, g, h))
+            parts_at.setdefault(7 + k, []).append((3, g, h))
         done = {-1: [(0, 3)]}
-        quantised = {(1, 0)}
+        quantised = {(1, 0), (1, 1)}
         issued = [2]
 
         def ready(kind, c, i):
@@ -484,37 +512,33 @@ def tile_retnet_pa_kernel(tc, x, wq, wk, out_0, out_1):
                 issued[0] = issued[0] + 1
 
         for j in range(len(seq)):
-            if j in quantise_before:
-                w_quantise(*quantise_before[j])
-                quantised.add(quantise_before[j])
-                if j == 1:
-                    hold_gpsimd()
-                    add_pair(0, 3, nc.gpsimd, WHOLE)
             issue_ahead(j)
-            kind, c, i = seq[j]
-            for c2, g, h in parts_at.get(j, ()):
-                if g == 0 and h == 0 and c2 == 3:
+            if j + 1 < len(seq) and seq[j + 1] in HELPED:
+                assist(*seq[j + 1][1:])
+            for c, g, h in parts_at.get(j, ()):
+                if g == 0 and h == 0 and c == 3:
                     new_stage(3)
-                interleave(sc, c2, g, h)
+                interleave(sc, c, g, h)
             for b in done.get(j - 2, ()):
                 store_t(*b)
             for b in done.get(j - 1, ()):
                 turn_add(*b)
-            if kind == "t":
+            kind, c, i = seq[j]
+            if seq[j] in HELPED:
+                rotate_h(c, i)
+                done.setdefault(j + 1, []).append((c, i))
+            elif kind == "t":
                 rotate_t(c, i)
                 done.setdefault(j, []).append((c, i))
             else:
                 last = j == len(seq) - 1
                 rotate(c, i, HALVES if last else WHOLE)
+                if j in quantise_after:
+                    w_quantise(*quantise_after[j])
+                    quantised.add(quantise_after[j])
                 if last:
                     add_tile(c, i, nc.vector, HALVES)
                 elif j == len(seq) - 2:
                     add_tile(c, i, nc.gpsimd, WHOLE)
                 elif i % 2 == 1:
                     add_pair(c, i // 2, nc.gpsimd, WHOLE)
-            if j == 4:
-                nc.scalar.mul(
-                    out=tab_k[:].rearrange("p a r f -> p (a r f)"),
-                    in_=tab_q[:].rearrange("p a r f -> p (a r f)"),
-                    mul=kappa,
-                )

@@ -24,7 +24,7 @@ TT = 4
 X_GROUPS = ((0, 1), (1, 2), (2, 3), (3, 4), (4, 6), (6, 8))
 WHOLE = ((0, 4),)
 HALVES = ((0, 2), (2, 4))
-HELPED = (("t", 1, 3), ("t", 2, 1), ("t", 2, 3), ("t", 3, 1))
+HELPED = (("t", 1, 1), ("t", 1, 3), ("t", 2, 1), ("t", 2, 3), ("t", 3, 1))
 AHEAD = 3
 
 
@@ -275,12 +275,16 @@ def tile_retnet_pa_kernel(tc, x, wq, wk, out_0, out_1):
         pair = {}
         mts = {}
 
+        copies = {}
+
+        def assist_copy(c, h):
+            copies[(c, h)] = helped.tile([P, NC], F32, name="q")
+            nc.scalar.copy(out=copies[(c, h)][:], in_=accs[("t", c, h)][:])
+
         def assist(c, h):
-            q = helped.tile([P, NC], F32, name="q")
             mts[(c, h)] = prodt.tile([P, 2, NC], F32, name="mt")
-            nc.scalar.copy(out=q[:], in_=accs[("t", c, h)][:])
             nc.gpsimd.tensor_tensor(
-                out=mts[(c, h)][:, 1, :], in0=q[:], in1=tab_t[:, 1, :], op=ALU.mult
+                out=mts[(c, h)][:, 1, :], in0=copies[(c, h)][:], in1=tab_t[:, 1, :], op=ALU.mult
             )
 
         def rotate_h(c, h):
@@ -404,7 +408,7 @@ def tile_retnet_pa_kernel(tc, x, wq, wk, out_0, out_1):
                     mul=kappa,
                 )
             ov = oq if c < 2 else ok
-            nc.scalar.dma_start(out=ov[:, 4 * (c % 2) + h, 0:TT, :], in_=r[:])
+            nc.sync.dma_start(out=ov[:, 4 * (c % 2) + h, 0:TT, :], in_=r[:])
 
         sc, ve = nc.scalar.copy, nc.vector.tensor_copy
         phases()
@@ -487,6 +491,7 @@ def tile_retnet_pa_kernel(tc, x, wq, wk, out_0, out_1):
                 seq = seq + [("a", c, TT + 2 * b), ("a", c, TT + 2 * b + 1)]
                 if c < 3:
                     quantise_after[len(seq) - 1] = (c + 1, b)
+        seq = seq[:-4] + [("t", 3, 2), ("a", 3, TT + 2), ("t", 3, 3), ("a", 3, TT + 3)]
 
         parts_at = {}
         for k in range(8):
@@ -511,8 +516,13 @@ def tile_retnet_pa_kernel(tc, x, wq, wk, out_0, out_1):
                     multiply(c, i)
                 issued[0] = issued[0] + 1
 
-        for j in range(len(seq)):
+        for b in seq[:2]:
+            if b in HELPED:
+                assist_copy(*b[1:])
+        for j in range(len(seq) + 2):
             issue_ahead(j)
+            if j + 2 < len(seq) and seq[j + 2] in HELPED:
+                assist_copy(*seq[j + 2][1:])
             if j + 1 < len(seq) and seq[j + 1] in HELPED:
                 assist(*seq[j + 1][1:])
             for c, g, h in parts_at.get(j, ()):
@@ -523,6 +533,8 @@ def tile_retnet_pa_kernel(tc, x, wq, wk, out_0, out_1):
                 store_t(*b)
             for b in done.get(j - 1, ()):
                 turn_add(*b)
+            if j >= len(seq):
+                continue
             kind, c, i = seq[j]
             if seq[j] in HELPED:
                 rotate_h(c, i)
@@ -531,14 +543,14 @@ def tile_retnet_pa_kernel(tc, x, wq, wk, out_0, out_1):
                 rotate_t(c, i)
                 done.setdefault(j, []).append((c, i))
             else:
-                last = j == len(seq) - 1
+                last = c == 3 and i == NT - 1
                 rotate(c, i, HALVES if last else WHOLE)
                 if j in quantise_after:
                     w_quantise(*quantise_after[j])
                     quantised.add(quantise_after[j])
                 if last:
                     add_tile(c, i, nc.vector, HALVES)
-                elif j == len(seq) - 2:
+                elif c == 3 and i == NT - 2:
                     add_tile(c, i, nc.gpsimd, WHOLE)
                 elif i % 2 == 1:
-                    add_pair(c, i // 2, nc.gpsimd, WHOLE)
+                    add_pair(c, i // 2, nc.gpsimd, HALVES)

@@ -553,4 +553,4 @@ def tile_retnet_pa_kernel(tc, x, wq, wk, out_0, out_1):
                 elif c == 3 and i == NT - 2:
                     add_tile(c, i, nc.gpsimd, WHOLE)
                 elif i % 2 == 1:
-                    add_pair(c, i // 2, nc.gpsimd, HALVES)
+                    add_pair(c, i // 2, nc.gpsimd, HALVES if c == 3 else WHOLE)

@@ -144,8 +144,6 @@ def tile_retnet_pa_kernel(tc, x, wq, wk, out_0, out_1):
         frt = const.tile([P, NC], F32, name="frt")
         aba = const.tile([P, NT - TT, NF], F32, name="aba")
         abt = const.tile([P, NC], F32, name="abt")
-        late = const.tile([P, 1], F32, name="late")
-        held = const.tile([P, 1], F32, name="held")
 
         def phases():
             tokf = tok[:].rearrange("p a r -> p (a r)")
@@ -373,12 +371,6 @@ def tile_retnet_pa_kernel(tc, x, wq, wk, out_0, out_1):
             )
             mts[(c, h)] = mt
 
-        def hold_gpsimd():
-            nc.vector.memset(late[:], 1.0)
-            nc.gpsimd.tensor_scalar(
-                out=held[:], in0=late[:], scalar1=1.0, scalar2=0.0, op0=ALU.mult, op1=ALU.add
-            )
-
         outs = {}
 
         def turn_add(c, h):
@@ -470,7 +462,6 @@ def tile_retnet_pa_kernel(tc, x, wq, wk, out_0, out_1):
         )
         rotate(0, 5)
         w_quantise(1, 0)
-        hold_gpsimd()
         add_pair(0, 2, nc.gpsimd, WHOLE)
         multiply_t(1, 0)
         multiply_t(1, 1)
@@ -479,7 +470,6 @@ def tile_retnet_pa_kernel(tc, x, wq, wk, out_0, out_1):
         rotate(0, 6)
         rotate(0, 7)
         w_quantise(1, 1)
-        hold_gpsimd()
         add_pair(0, 3, nc.gpsimd, WHOLE)
         new_stage(2)
 

from contextlib import ExitStack

import concourse.mybir as mybir
from concourse.masks import make_identity

F32 = mybir.dt.float32
BF16 = mybir.dt.bfloat16
U32 = mybir.dt.uint32
U8 = mybir.dt.uint8
I32 = mybir.dt.int32
E5X4 = mybir.dt.float8_e5m2_x4
ALU = mybir.AluOpType
ACT = mybir.ActivationFunctionType

S, E, H, KD = 1024, 1024, 8, 128
P = 128
NT = S // P
NC = 512
NF = KD // 2
PI = 3.141592653589793
FLOPS = 2 * S * E * 2 * H * KD

TT = 4
X_GROUPS = ((0, 1), (1, 2), (2, 3), (3, 4), (4, 6), (6, 8))
WHOLE = ((0, 4),)
HALVES = ((0, 2), (2, 4))
HELPED = (("t", 1, 1), ("t", 1, 3), ("t", 2, 1), ("t", 2, 3), ("t", 3, 1))
AHEAD = 3


def tile_retnet_pa_kernel(tc, x, wq, wk, out_0, out_1):
    nc = tc.nc
    xv = x.rearrange("b (p a) k -> p (b a) k", a=NT)
    wqv = wq.rearrange("(g p j) n -> g p j n", g=2, j=4)
    wkv = wk.rearrange("(g p j) n -> g p j n", g=2, j=4)
    oq = out_0.rearrange("b h (p a) f -> p (b h) a f", a=NT)
    ok = out_1.rearrange("b h (p a) f -> p (b h) a f", a=NT)
    kappa = KD**-0.5

    with ExitStack() as ctx:
        const = ctx.enter_context(tc.tile_pool(name="const", bufs=1))
        keep = ctx.enter_context(tc.tile_pool(name="keep", bufs=1))
        stage = ctx.enter_context(tc.tile_pool(name="stage", bufs=2))
        prod = ctx.enter_context(tc.tile_pool(name="prod", bufs=4))
        prodt = ctx.enter_context(tc.tile_pool(name="prodt", bufs=6))
        outt = ctx.enter_context(tc.tile_pool(name="outt", bufs=4))
        helped = ctx.enter_context(tc.tile_pool(name="helped", bufs=2))
        psx = ctx.enter_context(tc.psum_pool(name="psx", bufs=3))
        psa = ctx.enter_context(tc.psum_pool(name="psa", bufs=5))
        ctx.enter_context(tc.manual_schedule())

        xraw = {}
        wraw = {}

        def load_x(i):
            lo, hi = X_GROUPS[i]
            t = keep.tile([P, hi - lo, E], BF16, name="xraw%d" % i)
            nc.sync.dma_start(out=t[:], in_=xv[:, lo:hi, :])
            xraw[i] = t

        def load_w(c, g, n0, n):
            t = keep.tile([P, 4, n], BF16, name="wraw%d_%d_%d" % (c, g, n0))
            wv = wqv if c < 2 else wkv
            lo = NC * (c % 2) + n0
            nc.sync.dma_start(out=t[:], in_=wv[g][:, :, lo : lo + n])
            for k in range(n // P):
                wraw[(c, g, n0 // P + k)] = t[:, :, P * k : P * (k + 1)]

        for i in range(4):
            load_x(i)
        for n0 in (0, 256):
            for g in range(2):
                load_w(0, g, n0, 256)
        load_x(4)
        load_x(5)
        for c in (1, 2, 3):
            for g in range(2):
                load_w(c, g, 0, NC)

        ones = const.tile([P, 1], F32, name="ones")
        nc.vector.memset(ones[:], 1.0)
        junk = const.tile([P, 1], F32, name="junk")
        nc.scalar.activation(out=junk[:], in_=ones[:], func=ACT.Sin)
        ident = const.tile([P, P], F32, name="ident")
        make_identity(nc, ident[:])
        idx = const.tile([P, NT], F32, name="idx")
        nc.gpsimd.iota(
            idx[:], pattern=[[1, NT]], base=0, channel_multiplier=NT,
            allow_small_or_imprecise_dtypes=True,
        )
        tok = const.tile([P, TT, P], F32, name="tok")
        nc.gpsimd.iota(
            tok[:], pattern=[[1, TT], [NT, P]], base=0, channel_multiplier=0,
            allow_small_or_imprecise_dtypes=True,
        )
        perm = const.tile([P, P], F32, name="perm")
        nc.gpsimd.tensor_scalar(
            out=perm[:].rearrange("p (c e) -> p c e", e=2),
            in0=ident[:].rearrange("p (c e) -> p c e", e=2)[:, :, ::-1],
            scalar1=1.0, scalar2=0.0, op0=ALU.mult, op1=ALU.add,
        )
        ratio = 10000.0 ** (-1.0 / 63.0)
        nu = const.tile([P, NF], F32, name="nu")
        for j in range(4):
            nc.vector.tensor_scalar_mul(
                out=nu[:, j : j + 1], in0=ones[:], scalar1=ratio**j / (2.0 * PI)
            )
        halfpi = const.tile([P, 1], F32, name="halfpi")
        nc.vector.tensor_scalar_mul(out=halfpi[:], in0=ones[:], scalar1=PI / 2.0)
        for m in range(1, 4):
            nc.vector.tensor_scalar_mul(
                out=nu[:, 4 * m : 4 * (m + 1)], in0=nu[:, 0:4], scalar1=ratio ** (4 * m)
            )
        sgn = const.tile([P, 2], F32, name="sgn")
        nc.vector.memset(sgn[:, 0:1], 1.0)
        nc.vector.memset(sgn[:, 1:2], -1.0)
        for m in range(1, 4):
            nc.vector.tensor_scalar_mul(
                out=nu[:, 16 * m : 16 * (m + 1)], in0=nu[:, 0:16], scalar1=ratio ** (16 * m)
            )
        nus = const.tile([P, KD], F32, name="nus")
        nc.vector.tensor_tensor(
            out=nus[:].rearrange("p (c e) -> p c e", e=2),
            in0=nu[:].unsqueeze(2).to_broadcast([P, NF, 2]),
            in1=sgn[:].unsqueeze(1).to_broadcast([P, NF, 2]),
            op=ALU.mult,
        )
        nut = psx.tile([P, P], F32, name="xt")
        nc.tensor.transpose(nut[:], nus[:], ident[:])

        def warm_up(n):
            wp = psa.tile([P, NC], F32, name="acc")
            for i in range(n):
                nc.tensor.matmul(out=wp[:, 0:P], lhsT=ident[:], rhs=ident[:], start=True, stop=True)

        tab_t = const.tile([P, 2, NC], F32, name="tab_t")
        tab_q = const.tile([P, NT - TT, 2, KD], F32, name="tab_q")
        tab_k = const.tile([P, NT - TT, 2, KD], F32, name="tab_k")
        nuf = const.tile([P, 1], F32, name="nuf")
        pha = const.tile([P, NT - TT, KD], F32, name="pha")
        kia = const.tile([P, NC], I32, name="kia")
        kit = const.tile([P, NC], I32, name="kit")
        fra = const.tile([P, NT - TT, NF, 2], F32, name="fra")
        frt = const.tile([P, NC], F32, name="frt")
        aba = const.tile([P, NT - TT, NF], F32, name="aba")
        abt = const.tile([P, NC], F32, name="abt")

        def phases():
            tokf = tok[:].rearrange("p a r -> p (a r)")
            phf = pha[:].rearrange("p a f -> p (a f)")
            nc.vector.tensor_tensor(
                out=pha[:], in0=idx[:, TT:NT].unsqueeze(2).to_broadcast([P, NT - TT, KD]),
                in1=nus[:].unsqueeze(1).to_broadcast([P, NT - TT, KD]), op=ALU.mult,
            )
            nc.vector.tensor_copy(out=nuf[:], in_=nut[:, 0:1])
            nc.vector.tensor_copy(out=kia[:], in_=phf)
            nc.vector.tensor_scalar(
                out=kit[:], in0=tokf, scalar1=nuf[:, 0:1], scalar2=0.0, op0=ALU.mult, op1=ALU.add
            )
            nc.vector.scalar_tensor_tensor(
                out=fra[:].rearrange("p a c e -> p (a c e)"), in0=kia[:], scalar=-1.0, in1=phf,
                op0=ALU.mult, op1=ALU.add,
            )
            nc.vector.scalar_tensor_tensor(
                out=frt[:], in0=tokf, scalar=nuf[:, 0:1], in1=kit[:],
                op0=ALU.mult, op1=ALU.subtract,
            )
            nc.vector.scalar_tensor_tensor(
                out=aba[:], in0=fra[:, :, :, 0], scalar=-1.0, in1=fra[:, :, :, 0],
                op0=ALU.mult, op1=ALU.max,
            )
            nc.vector.scalar_tensor_tensor(
                out=abt[:], in0=frt[:], scalar=-1.0, in1=frt[:], op0=ALU.mult, op1=ALU.max
            )

        def tables_t():
            nc.scalar.activation(out=tab_t[:, 1, :], in_=frt[:], func=ACT.Sin, scale=2.0 * PI)
            nc.scalar.activation(
                out=tab_t[:, 0, :], in_=abt[:], func=ACT.Sin, scale=-2.0 * PI, bias=halfpi[:, 0:1]
            )

        def tables_a():
            nc.scalar.activation(
                out=tab_q[:, :, 1, :], in_=fra[:].rearrange("p a c e -> p a (c e)"),
                func=ACT.Sin, scale=2.0 * PI,
            )
            nc.scalar.activation(
                out=tab_q[:, :, 0, :].rearrange("p a (c e) -> p a c e", e=2),
                in_=aba[:].unsqueeze(3).to_broadcast([P, NT - TT, NF, 2]),
                func=ACT.Sin, scale=-2.0 * PI, bias=halfpi[:, 0:1],
            )

        xt = {}
        xc = {}
        xs = {}
        xg_t = keep.tile([P, 2, TT, NC], BF16, name="xg_t", align_bytes=64)
        xc_t = keep.tile([P, 2, TT, P], U32, name="xc_t", align_bytes=64)
        xs_t = keep.tile([P, 2, TT, P], U8, name="xs_t", align_bytes=64)
        xg = {}

        def x_turn(i, t):
            words = xraw[i][:, t, :].bitcast(F32)
            xt[(i, t)] = psx.tile([P, 2, 2, P], F32, name="xt")
            for g in range(2):
                for u in range(2):
                    nc.tensor.transpose(
                        xt[(i, t)][:, g, u, :], words[:, 256 * g + u : 256 * (g + 1) : 2], ident[:]
                    )

        def x_copy(cp, i, t):
            lo, hi = X_GROUPS[i]
            if lo < TT:
                dst = xg_t[:, :, lo + t, :].bitcast(F32).rearrange("p g (r u) -> p g r u", u=2)
            else:
                if t == 0:
                    xg[i] = keep.tile([P, (hi - lo) * 1024], BF16, name="xg%d" % i, align_bytes=64)
                dst = (
                    xg[i][:, 1024 * t : 1024 * (t + 1)]
                    .bitcast(F32)
                    .rearrange("p (g r u) -> p g r u", g=2, u=2)
                )
            cp(out=dst, in_=xt[(i, t)][:].rearrange("p g u r -> p g r u"))

        def x_quantise_t(a):
            for g in range(2):
                nc.vector.quantize_mx(
                    out=xc_t[:, g, a, :].bitcast(E5X4), scales=xs_t[:, g, a, :], in_=xg_t[:, g, a, :]
                )

        def x_quantise(i):
            lo, hi = X_GROUPS[i]
            n = hi - lo
            codes = keep.tile([P, n * 256], U32, name="xc%d" % i, align_bytes=64)
            scales = keep.tile([P, n * 256], U8, name="xs%d" % i, align_bytes=64)
            nc.vector.quantize_mx(out=codes[:].bitcast(E5X4), scales=scales[:], in_=xg[i][:])
            for t in range(n):
                for g in range(2):
                    xc[(lo + t, g)] = codes[:, 256 * t + P * g : 256 * t + P * (g + 1)]
                    xs[(lo + t, g)] = scales[:, 256 * t + P * g : 256 * t + P * (g + 1)]

        wgr = {}
        wc = {}
        ws = {}

        def new_stage(key):
            wgr[key] = stage.tile([P, 2, 4 * NC], BF16, name="wgr", align_bytes=64)
            wc[key] = keep.tile([P, 2, NC], U32, name="wc%d" % key, align_bytes=64)
            ws[key] = keep.tile([P, 2, NC], U8, name="ws%d" % key, align_bytes=64)

        def interleave(cp, c, g, h):
            cp(
                out=wgr[c][:, g, NC * h : NC * (h + 1)].rearrange("p (c i j) -> p c j i", i=4, j=4),
                in_=wraw[(c, g, h)].rearrange("p j (c i) -> p c j i", i=4),
            )

        def w_quantise_head(c, h):
            for g in range(2):
                nc.vector.quantize_mx(
                    out=wc[c][:, g, P * h : P * (h + 1)].bitcast(E5X4),
                    scales=ws[c][:, g, P * h : P * (h + 1)],
                    in_=wgr[c][:, g, NC * h : NC * (h + 1)],
                )

        def w_quantise(c, b):
            for g in range(2):
                nc.vector.quantize_mx(
                    out=wc[c][:, g, 2 * P * b : 2 * P * (b + 1)].bitcast(E5X4),
                    scales=ws[c][:, g, 2 * P * b : 2 * P * (b + 1)],
                    in_=wgr[c][:, g, 2 * NC * b : 2 * NC * (b + 1)],
                )

        accs = {}
        pair = {}
        mts = {}

        copies = {}

        def assist_copy(c, h):
            copies[(c, h)] = helped.tile([P, NC], F32, name="q")
            nc.scalar.copy(out=copies[(c, h)][:], in_=accs[("t", c, h)][:])

        def assist(c, h):
            mts[(c, h)] = prodt.tile([P, 2, NC], F32, name="mt")
            nc.gpsimd.tensor_tensor(
                out=mts[(c, h)][:, 1, :], in0=copies[(c, h)][:], in1=tab_t[:, 1, :], op=ALU.mult
            )

        def rotate_h(c, h):
            nc.vector.tensor_tensor(
                out=mts[(c, h)][:, 0, :], in0=accs[("t", c, h)][:], in1=tab_t[:, 0, :], op=ALU.mult
            )

        def multiply(c, a):
            acc = psa.tile([P, NC], F32, name="acc")
            for g in range(2):
                nc.tensor.matmul_mx(
                    out=acc[:],
                    lhsT=xc[(a, g)].bitcast(E5X4),
                    lhsT_scale=xs[(a, g)],
                    rhs=wc[c][:, g, :].bitcast(E5X4),
                    rhs_scale=ws[c][:, g, :],
                    start=(g == 0),
                    stop=(g == 1),
                )
            accs[("a", c, a)] = acc

        def rotate(c, a, parts=WHOLE):
            tab = tab_q if c < 2 else tab_k
            aq = a % 2
            if aq == 0:
                pair[(c, a // 2)] = prod.tile([P, 2, 4, 2, KD], F32, name="m")
            m = pair[(c, a // 2)]
            for h0, h1 in parts:
                nc.vector.tensor_tensor(
                    out=m[:, :, h0:h1, aq, :],
                    in0=accs[("a", c, a)][:].rearrange("p (h f) -> p h f", h=4)[:, h0:h1].unsqueeze(1)
                    .to_broadcast([P, 2, h1 - h0, KD]),
                    in1=tab[:, a - TT, :, :].unsqueeze(2).to_broadcast([P, 2, h1 - h0, KD]),
                    op=ALU.mult,
                )

        def add_tile(c, a, eng, parts):
            ov = oq if c < 2 else ok
            hb = 4 * (c % 2)
            m = pair[(c, a // 2)]
            for h0, h1 in parts:
                eng.tensor_tensor(
                    out=m[:, 0, h0:h1, a % 2].rearrange("p h (c e) -> p h c e", e=2),
                    in0=m[:, 0, h0:h1, a % 2].rearrange("p h (c e) -> p h c e", e=2),
                    in1=m[:, 1, h0:h1, a % 2].rearrange("p h (c e) -> p h c e", e=2)[:, :, :, ::-1],
                    op=ALU.add,
                )
                nc.sync.dma_start(out=ov[:, hb + h0 : hb + h1, a, :], in_=m[:, 0, h0:h1, a % 2])

        def add_pair(c, b, eng, parts):
            ov = oq if c < 2 else ok
            hb = 4 * (c % 2)
            m = pair[(c, b)]
            for h0, h1 in parts:
                eng.tensor_tensor(
                    out=m[:, 0, h0:h1].rearrange("p h a (c e) -> p (h a c) e", e=2),
                    in0=m[:, 0, h0:h1].rearrange("p h a (c e) -> p (h a c) e", e=2),
                    in1=m[:, 1, h0:h1].rearrange("p h a (c e) -> p (h a c) e", e=2)[:, :, ::-1],
                    op=ALU.add,
                )
                nc.sync.dma_start(
                    out=ov[:, hb + h0 : hb + h1, 2 * b : 2 * b + 2, :], in_=m[:, 0, h0:h1]
                )

        def multiply_t(c, h):
            acc = psa.tile([P, NC], F32, name="acc")
            for g in range(2):
                nc.tensor.matmul_mx(
                    out=acc[:],
                    lhsT=wc[c][:, g, P * h : P * (h + 1)].bitcast(E5X4),
                    lhsT_scale=ws[c][:, g, P * h : P * (h + 1)],
                    rhs=xc_t[:, g].rearrange("p a r -> p (a r)").bitcast(E5X4),
                    rhs_scale=xs_t[:, g].rearrange("p a r -> p (a r)"),
                    start=(g == 0),
                    stop=(g == 1),
                )
            accs[("t", c, h)] = acc

        def rotate_t(c, h):
            mt = prodt.tile([P, 2, NC], F32, name="mt")
            nc.vector.tensor_tensor(
                out=mt[:],
                in0=accs[("t", c, h)][:].unsqueeze(1).to_broadcast([P, 2, NC]),
                in1=tab_t[:],
                op=ALU.mult,
            )
            mts[(c, h)] = mt

        outs = {}

        def turn_add(c, h):
            mt = mts[(c, h)]
            o = psx.tile([P, TT, P], F32, name="xt")
            for t in range(TT):
                nc.tensor.matmul(
                    out=o[:, t, :], lhsT=mt[:, 0, P * t : P * (t + 1)], rhs=ident[:],
                    start=True, stop=False, is_transpose=True,
                )
                nc.tensor.matmul(
                    out=o[:, t, :], lhsT=mt[:, 1, P * t : P * (t + 1)], rhs=perm[:],
                    start=False, stop=True, is_transpose=True,
                )
            outs[(c, h)] = o

        def store_t(c, h):
            o = outs[(c, h)]
            r = outt.tile([P, TT, KD], F32, name="r")
            if c < 2:
                nc.scalar.copy(
                    out=r[:].rearrange("p a f -> p (a f)"), in_=o[:].rearrange("p a f -> p (a f)")
                )
            else:
                nc.scalar.mul(
                    out=r[:].rearrange("p a f -> p (a f)"), in_=o[:].rearrange("p a f -> p (a f)"),
                    mul=kappa,
                )
            ov = oq if c < 2 else ok
            nc.sync.dma_start(out=ov[:, 4 * (c % 2) + h, 0:TT, :], in_=r[:])

        sc, ve = nc.scalar.copy, nc.vector.tensor_copy
        phases()
        for a in range(TT):
            x_turn(a, 0)
            x_copy(ve if a == 2 else sc, a, 0)
        warm_up(4)
        tables_t()
        for a in range(TT):
            x_quantise_t(a)
        new_stage(0)
        for g in range(2):
            interleave(ve, 0, g, 0)
        interleave(sc, 0, 1, 1)
        w_quantise_head(0, 0)
        interleave(ve, 0, 0, 1)
        multiply_t(0, 0)
        w_quantise_head(0, 1)
        multiply_t(0, 1)
        for t in range(2):
            x_turn(4, t)
        for h in (2, 3):
            for g in range(2):
                interleave(sc, 0, g, h)
        for t in range(2):
            x_copy(sc, 4, t)
        rotate_t(0, 0)
        w_quantise_head(0, 2)
        multiply_t(0, 2)
        rotate_t(0, 1)
        for t in range(2):
            x_turn(5, t)
        w_quantise_head(0, 3)
        multiply_t(0, 3)
        tables_a()
        for t in range(2):
            x_copy(sc, 5, t)
        rotate_t(0, 2)
        x_quantise(4)
        multiply(0, 4)
        rotate_t(0, 3)
        multiply(0, 5)
        turn_add(0, 0)
        rotate(0, 4)
        x_quantise(5)
        multiply(0, 6)
        multiply(0, 7)
        new_stage(1)
        for h in range(4):
            for g in range(2):
                interleave(sc, 1, g, h)
        turn_add(0, 1)
        for h in range(2):
            store_t(0, h)
        nc.gpsimd.tensor_scalar(
            out=tab_k[:].rearrange("p a r f -> p (a r f)"),
            in0=tab_q[:].rearrange("p a r f -> p (a r f)"),
            scalar1=kappa, scalar2=0.0, op0=ALU.mult, op1=ALU.add,
        )
        rotate(0, 5)
        w_quantise(1, 0)
        add_pair(0, 2, nc.gpsimd, WHOLE)
        multiply_t(1, 0)
        multiply_t(1, 1)
        turn_add(0, 2)
        store_t(0, 2)
        rotate(0, 6)
        rotate(0, 7)
        w_quantise(1, 1)
        add_pair(0, 3, nc.gpsimd, WHOLE)
        new_stage(2)

        seq = []
        quantise_after = {}
        for c in (1, 2, 3):
            for b in range(2):
                seq = seq + [("t", c, 2 * b), ("t", c, 2 * b + 1)]
                seq = seq + [("a", c, TT + 2 * b), ("a", c, TT + 2 * b + 1)]
                if c < 3:
                    quantise_after[len(seq) - 1] = (c + 1, b)
        seq = seq[:-4] + [("t", 3, 2), ("a", 3, TT + 2), ("t", 3, 3), ("a", 3, TT + 3)]

        parts_at = {}
        for k in range(8):
            g, h = k % 2, k // 2
            parts_at.setdefault(k // 2 if h < 2 else k - 1, []).append((2, g, h))
            parts_at.setdefault(7 + k, []).append((3, g, h))
        done = {-1: [(0, 3)]}
        quantised = {(1, 0), (1, 1)}
        issued = [2]

        def ready(kind, c, i):
            if kind == "t":
                return (c, i // 2) in quantised
            return (c, 0) in quantised and (c, 1) in quantised

        def issue_ahead(j):
            while issued[0] < len(seq) and issued[0] <= j + AHEAD and ready(*seq[issued[0]]):
                kind, c, i = seq[issued[0]]
                if kind == "t":
                    multiply_t(c, i)
                else:
                    multiply(c, i)
                issued[0] = issued[0] + 1

        for b in seq[:2]:
            if b in HELPED:
                assist_copy(*b[1:])
        for j in range(len(seq) + 2):
            issue_ahead(j)
            if j + 2 < len(seq) and seq[j + 2] in HELPED:
                assist_copy(*seq[j + 2][1:])
            if j + 1 < len(seq) and seq[j + 1] in HELPED:
                assist(*seq[j + 1][1:])
            for c, g, h in parts_at.get(j, ()):
                if g == 0 and h == 0 and c == 3:
                    new_stage(3)
                interleave(sc, c, g, h)
            for b in done.get(j - 2, ()):
                store_t(*b)
            for b in done.get(j - 1, ()):
                turn_add(*b)
            if j >= len(seq):
                continue
            kind, c, i = seq[j]
            if seq[j] in HELPED:
                rotate_h(c, i)
                done.setdefault(j + 1, []).append((c, i))
            elif kind == "t":
                rotate_t(c, i)
                done.setdefault(j, []).append((c, i))
            else:
                last = c == 3 and i == NT - 1
                rotate(c, i, HALVES if last else WHOLE)
                if j in quantise_after:
                    w_quantise(*quantise_after[j])
                    quantised.add(quantise_after[j])
                if last:
                    add_tile(c, i, nc.vector, HALVES)
                elif c == 3 and i == NT - 2:
                    add_tile(c, i, nc.gpsimd, WHOLE)
                elif i % 2 == 1:
                    add_pair(c, i // 2, nc.gpsimd, HALVES if c == 3 else WHOLE)
